import numpy as np
import ml_dtypes


def mxq(x, axis, fmt="e4m3"):
    dtype, down = {"e4m3": (ml_dtypes.float8_e4m3fn, 7), "e5m2": (ml_dtypes.float8_e5m2, 14)}[fmt]
    v = np.moveaxis(np.asarray(x, np.float32).astype(ml_dtypes.bfloat16).astype(np.float64), axis, -1)
    blocks = v.reshape(v.shape[:-1] + (-1, 32))
    amax = np.abs(blocks).max(-1, keepdims=True)
    byte = np.maximum(np.where(amax > 0, np.frexp(amax)[1] - 1 + 127, 0) - down, 1)
    scale = np.exp2(byte - 127.0)
    codes = (blocks / scale).astype(np.float32).astype(dtype).astype(np.float64)
    return np.moveaxis((codes * scale).reshape(v.shape), -1, axis)


WIDE = False


def mx_kscale(k):
    if not WIDE:
        return np.ones(k)
    levels = np.array([10, -10, 5, -5, 0])
    if k % 512:
        return np.exp2(np.random.permutation(np.resize(levels, k // 32))).repeat(32)
    a = np.empty((k // 512, 16))
    for p in range(k // 512):
        a[p, :8] = np.random.permutation(np.resize(levels, 8))
        for g in range(8):
            far = levels[np.abs(levels - a[p, g]) >= 10]
            a[p, g + 8] = far[np.random.randint(len(far))]
    return np.exp2(a.ravel()).repeat(32)


BF16 = ml_dtypes.bfloat16


def bf(x):
    return np.asarray(x, np.float32).astype(BF16)


def f64(x):
    return np.asarray(x).astype(np.float64)


B, N, W, H, D = 1, 4, 512, 2, 512


def setup_inputs():
    s = mx_kscale(D)
    u = mx_kscale(D)
    m = np.random.uniform(0.2, 1.0, (N, N))
    k0 = bf(np.maximum(np.random.standard_normal((B, H, N, W, D)) * 0.5, 0.0))
    v0 = bf(np.random.standard_normal((B, H, N, W, D)) * 0.5)
    g = np.random.standard_normal((B, H, N, D, D)) * np.exp2(np.random.randint(-6, 1, (B, H, N, D, 1)))
    return {"k_feat": bf(f64(k0) * s),
            "v": bf(f64(v0) / u),
            "w_piece": bf(m / m.sum(axis=0, keepdims=True)),
            "grad_out": bf(g / s[:, None] * u)}


def reference(k_feat, v, w_piece, grad_out):
    wp = f64(w_piece)
    g = f64(grad_out)
    dkv = (wp[None, None, :, :, None, None] * g[:, :, :, None, :, :]).sum(axis=2)
    dk = mxq(f64(v), 4, "e4m3") @ mxq(dkv, 4, "e5m2").transpose(0, 1, 2, 4, 3)
    dv = mxq(f64(k_feat), 4, "e4m3") @ mxq(dkv, 3, "e5m2")
    return dk, dv

@@ -1,0 +1,397 @@
+from contextlib import ExitStack
+
+import concourse.mybir as mybir
+from concourse.masks import make_identity
+
+F32 = mybir.dt.float32
+BF16 = mybir.dt.bfloat16
+U32 = mybir.dt.uint32
+U8 = mybir.dt.uint8
+E4M3 = mybir.dt.float8_e4m3fn_x4
+E5M2 = mybir.dt.float8_e5m2_x4
+MULT = mybir.AluOpType.mult
+ADD = mybir.AluOpType.add
+
+H, N, W, D = 2, 4, 512, 512
+P = 128
+PAIRS = H * N
+FLOPS = 2 * 2 * PAIRS * W * D * D
+
+
+def tile_mhla_pa_v_kernel(tc, k_feat, v, w_piece, grad_out, out_0, out_1):
+    nc = tc.nc
+    with ExitStack() as ctx:
+        const = ctx.enter_context(tc.tile_pool(name="const", bufs=1))
+        keep = ctx.enter_context(tc.tile_pool(name="keep", bufs=1))
+        work = ctx.enter_context(tc.tile_pool(name="work", bufs=2))
+        psum = ctx.enter_context(tc.psum_pool(name="psum", bufs=8))
+
+        w_rows = const.tile([P, N], BF16, name="w_rows")
+        nc.vector.memset(w_rows[:], 0.0)
+        nc.scalar.dma_start(out=w_rows[0:N, :], in_=w_piece)
+        ones = const.tile([P, P], BF16, name="ones", align_bytes=64)
+        nc.vector.memset(ones[:], 1.0)
+        ident = const.tile([P, P], BF16, name="ident")
+        make_identity(nc, ident[:])
+        ident_f = const.tile([P, P], F32, name="ident_f")
+        make_identity(nc, ident_f[:])
+
+        raw = {}
+        g_mix = {}
+        g_row = {}
+
+        def load_kv(which, n, part=None):
+            h, j = divmod(n, N)
+            if (which, n) not in raw:
+                raw[which, n] = keep.tile([P, 2048], BF16, name="raw_" + which, bufs=5, align_bytes=64)
+            src = (k_feat if which == "k" else v)[0, h, j].rearrange("(m b) d -> m (b d)", b=4)
+            cols = slice(0, 2048) if part is None else slice(1024 * part, 1024 * part + 1024)
+            nc.sync.dma_start(out=raw[which, n][:, cols], in_=src[:, cols])
+
+        def load_rows(h, half):
+            if h not in g_row:
+                g_row[h] = keep.tile([P, N, 512], BF16, name="g_row" + str(h), align_bytes=64)
+            i0 = 2 * half
+            nc.sync.dma_start(
+                out=g_row[h][:, i0 : i0 + 2, :], in_=grad_out[0, h].rearrange("i q d -> q i d")[384:512, i0 : i0 + 2, :]
+            )
+
+        def load_mix(h, half):
+            if h not in g_mix:
+                g_mix[h] = keep.tile([P, 12, 512], BF16, name="g_mix" + str(h), align_bytes=64)
+            for i in range(N):
+                src = grad_out[0, h, i].rearrange("(x r) d -> r x d", r=32)
+                nc.sync.dma_start(
+                    out=g_mix[h][i:P:4, 6 * half : 6 * half + 6, :], in_=src[:, 6 * half : 6 * half + 6, :]
+                )
+
+        load_mix(0, 0)
+        load_rows(0, 0)
+        load_kv("v", 0, 0)
+        load_rows(0, 1)
+        load_mix(0, 1)
+        load_kv("v", 0, 1)
+        load_kv("v", 1)
+        load_kv("k", 0)
+        load_mix(1, 1)
+        load_kv("k", 2)
+        load_kv("k", 1)
+        load_mix(1, 0)
+        load_kv("k", 4)
+        load_kv("v", 4)
+        load_kv("v", 2)
+        load_kv("k", 3)
+        load_kv("v", 3)
+        load_rows(1, 0)
+        load_rows(1, 1)
+
+        warm = const.tile([P, 1], F32, name="warm")
+        nc.vector.memset(warm[:], 0.0)
+        nc.scalar.copy(out=warm[:], in_=warm[:])
+        eye = const.tile([P, 32], F32, name="eye")
+        nc.vector.tensor_reduce(
+            out=eye[:].rearrange("p (u q e) -> p q u e", u=2, e=2),
+            in_=ident[:].rearrange("p (q u e i) -> p q u e i", u=2, e=2, i=4),
+            axis=mybir.AxisListType.X,
+            op=ADD,
+        )
+        spread = const.tile([P, 32, N], BF16, name="spread", align_bytes=64)
+        nc.vector.tensor_copy(out=spread[:], in_=ident[:, 0:N].unsqueeze(1).to_broadcast([P, 32, N]))
+        perm = const.tile([P, P], BF16, name="perm", align_bytes=64)
+        nc.vector.tensor_copy(
+            out=perm[:].rearrange("p (u q e) -> p q u e", u=2, e=2),
+            in_=ident[:].rearrange("p (q u e) -> p q u e", u=2, e=2),
+        )
+        w_diag = const.tile([P, N, N], BF16, name="w_diag")
+        nc.vector.tensor_tensor(
+            out=w_diag[:],
+            in0=w_rows[:].unsqueeze(1).to_broadcast([P, N, N]),
+            in1=ident[:, 0:N].unsqueeze(2).to_broadcast([P, N, N]),
+            op=MULT,
+        )
+        w_bank = psum.tile([P, 512], F32, name="bank")
+        nc.tensor.matmul(
+            w_bank[:, 0:16], lhsT=ones[:], rhs=w_diag[:].rearrange("p i j -> p (i j)"), start=True, stop=True
+        )
+        nc.tensor.matmul(
+            w_bank[:, 16:20], lhsT=spread[:].rearrange("p r i -> p (r i)"), rhs=w_rows[:], start=True, stop=True
+        )
+        w_f = const.tile([P, 20], F32, name="w_f")
+        nc.vector.tensor_copy(out=w_f[:], in_=w_bank[:, 0:20])
+        mixer = const.tile([P, P], BF16, name="mixer", align_bytes=64)
+        nc.vector.tensor_tensor(
+            out=mixer[:].rearrange("p (j r) -> p j r", j=N),
+            in0=eye[:].unsqueeze(1).to_broadcast([P, N, 32]),
+            in1=w_f[:, 16:20].unsqueeze(2).to_broadcast([P, N, 32]),
+            op=MULT,
+        )
+
+        mixed = [keep.tile([P, 4, N, 512], BF16, name="mixed" + str(h), align_bytes=64) for h in range(H)]
+        b_in = {}
+        acc = {}
+        mixed_terms = {}
+        row = {}
+        a_in = {}
+        grouped = {}
+        codes = {}
+        on_vector = set("mul-5 mul-6 mul-4 mul-7 rows-0 back-7-0 rows-7 k-0-0 k-7-0 out-6-0-1 out-7-0-0 v-7-0 k-3-0 out-3-1-3 k-3-1 back-5-1 out-5-1-2 v-6-1 k-1-0 rows-4 mul-0 out-1-0-0 back-2-1 out-1-0-3 out-1-1-3 out-1-1-2 out-3-1-1 out-3-0-0 mul-2 out-1-0-1 out-7-1-0".split())
+
+        def copy_out(dst, src, *key):
+            if "-".join(str(x) for x in key) in on_vector:
+                nc.vector.tensor_copy(out=dst, in_=src)
+            else:
+                nc.scalar.copy(out=dst, in_=src)
+
+        def f32_bank():
+            return psum.tile([P, 512], F32, name="bank")
+
+        def bf16_bank():
+            return psum.tile([P, 1024], BF16, name="bank")
+
+        def mix(n):
+            if n >= PAIRS:
+                return
+            i = mixed_terms.get(n, 0)
+            if i == N:
+                return
+            mixed_terms[n] = i + 1
+            h, j = divmod(n, N)
+            w_ij = w_f[:, 4 * i + j : 4 * i + j + 1]
+            src = g_row[h][:, i, :].rearrange("m (p t) -> m t p", t=4)
+            if i == 0:
+                acc[n] = work.tile([P, 4, 128], F32, name="acc", bufs=4)
+                if "mul-" + str(n) in on_vector:
+                    nc.vector.tensor_scalar(out=acc[n][:], in0=src, scalar1=w_ij, scalar2=None, op0=MULT)
+                else:
+                    nc.scalar.activation(
+                        out=acc[n][:], in_=src, func=mybir.ActivationFunctionType.Copy, scale=w_ij
+                    )
+                return
+            if i == 3:
+                row[n] = work.tile([P, 4, 128], BF16, name="row", bufs=4, align_bytes=64)
+            dst = row[n] if i == 3 else acc[n]
+            nc.vector.scalar_tensor_tensor(out=dst[:], in0=src, scalar=w_ij, in1=acc[n][:], op0=MULT, op1=ADD)
+
+        def spread_rows(n):
+            if n >= PAIRS:
+                return
+            h, j = divmod(n, N)
+            bank = bf16_bank()
+            for t in range(4):
+                nc.tensor.transpose(bank[:, 128 * t : 128 * t + 128], row[n][:, t, :], perm[:])
+            dst = mixed[h][:, :, j, :].rearrange("p t (u q) -> p t u q", u=2)
+            copy_out(dst[:, :, :, 192:256], bank[:, 0:512].rearrange("p (t u q) -> p t u q", t=4, u=2), "rows", n)
+
+        def kron(h, x):
+            bank = bf16_bank()
+            for g in range(2):
+                for t in range(4):
+                    c0 = 512 * g + 128 * t
+                    nc.tensor.matmul(
+                        bank[:, c0 : c0 + 128],
+                        lhsT=g_mix[h][:, 2 * x + g, t:512:4],
+                        rhs=mixer[:],
+                        start=True,
+                        stop=True,
+                    )
+            dst = mixed[h][:].rearrange("p t j (u q) -> p (t j u) q", u=2)[:, :, 32 * x : 32 * x + 32]
+            copy_out(
+                dst.rearrange("p a (g y) -> p a g y", g=2), bank[:].rearrange("p (g a y) -> p a g y", g=2, y=16), "mix", h, x
+            )
+
+        def interleave(n):
+            if n >= PAIRS:
+                return
+            h, j = divmod(n, N)
+            b_in[n] = work.tile([P, 2048], BF16, name="b_in", align_bytes=64)
+            nc.vector.tensor_copy(
+                out=b_in[n][:].rearrange("p (c i t) -> p c t i", i=4, t=4),
+                in_=mixed[h][:, :, j, :].rearrange("p t (c i) -> p c t i", i=4),
+            )
+
+        def turn(which, n, half):
+            if n >= PAIRS:
+                return
+            if (which, n) not in grouped:
+                grouped[which, n] = work.tile([P, 2048], BF16, name="grouped_" + which, align_bytes=64)
+            words = raw[which, n][:].bitcast(F32)
+            bank = f32_bank()
+            for b in range(2):
+                for u in range(2):
+                    w0 = 256 * (2 * half + b)
+                    nc.tensor.transpose(
+                        bank[:, 256 * b + 128 * u : 256 * b + 128 * u + 128], words[:, w0 + u : w0 + 256 : 2], ident_f[:]
+                    )
+            dst = grouped[which, n][:].bitcast(F32)[:, 512 * half : 512 * half + 512]
+            copy_out(
+                dst.rearrange("p (b m u) -> p b m u", b=2, u=2),
+                bank[:].rearrange("p (b u m) -> p b m u", b=2, u=2),
+                which,
+                n,
+                half,
+            )
+
+        def quant(which, n):
+            if n >= PAIRS:
+                return
+            h, j = divmod(n, N)
+            if which == "b":
+                src, fmt = b_in[n][:], E5M2
+            elif which == "a":
+                src, fmt = a_in[n][:], E5M2
+            else:
+                src, fmt = grouped[which, n][:], E4M3
+            depth = 2 if which in "ab" else 5
+            c = work.tile([P, 512], U32, name="codes_" + which, bufs=depth, align_bytes=64)
+            sc = work.tile([P, 512], U8, name="scales_" + which, bufs=depth, align_bytes=64)
+            nc.vector.quantize_mx(out=c[:].bitcast(fmt), scales=sc[:], in_=src)
+            codes[which, n] = (c, sc)
+
+        def back(n, half):
+            if n >= PAIRS:
+                return
+            h, j = divmod(n, N)
+            if n not in a_in:
+                a_in[n] = work.tile([P, 2048], BF16, name="a_in", align_bytes=64)
+            words = mixed[h][:].rearrange("p t j c -> p (t j c)").bitcast(F32)
+            bank = f32_bank()
+            for tt in range(2):
+                for u in range(2):
+                    c0 = 256 * tt + 128 * u
+                    w0 = 256 * (N * (2 * half + tt) + j) + 128 * u
+                    nc.tensor.transpose(bank[:, c0 : c0 + 128], words[:, w0 : w0 + 128], ident_f[:])
+            dst = a_in[n][:].bitcast(F32)[:, 512 * half : 512 * half + 512]
+            copy_out(
+                dst.rearrange("q (t p u) -> q t p u", t=2, u=2),
+                bank[:].rearrange("q (t u p) -> q t p u", t=2, u=2),
+                "back",
+                n,
+                half,
+            )
+
+        results = {}
+
+        def product(n, which, pair):
+            if n >= PAIRS:
+                return
+            h, j = divmod(n, N)
+            left, right, dram = ("v", "b", out_0) if which == 0 else ("k", "a", out_1)
+            lc, ls = codes[left, n]
+            rc, rs = codes[right, n]
+            if pair == 0:
+                results[which] = work.tile([P, 4, 512], F32, name="res" + str(which))
+            res = results[which]
+            view = dram[0, h, j].rearrange("(m b) d -> m b d", b=4)
+            for b in range(2 * pair, 2 * pair + 2):
+                bank = f32_bank()
+                cols = slice(128 * b, 128 * b + 128)
+                nc.tensor.matmul_mx(
+                    out=bank[:],
+                    lhsT=lc[:, cols].bitcast(E4M3),
+                    lhsT_scale=ls[:, cols],
+                    rhs=rc[:].bitcast(E5M2),
+                    rhs_scale=rs[:],
+                    start=True,
+                    stop=True,
+                )
+                if which == 0:
+                    dst = res[:, b, :].rearrange("m (q u e) -> m q u e", u=2, e=2)
+                    src = bank[:].rearrange("m (u q e) -> m q u e", u=2, e=2)
+                else:
+                    dst = res[:, b, :].rearrange("m (p t) -> m p t", t=4)
+                    src = bank[:].rearrange("m (t p) -> m p t", t=4)
+                copy_out(dst, src, "out", n, which, b)
+                if n == PAIRS - 1 and which == 1:
+                    nc.sync.dma_start(out=view[:, b, :], in_=res[:, b, :])
+            if not (n == PAIRS - 1 and which == 1):
+                nc.sync.dma_start(out=view[:, 2 * pair : 2 * pair + 2, :], in_=res[:, 2 * pair : 2 * pair + 2, :])
+
+        with tc.manual_schedule():
+            mix(2)
+            mix(3)
+            mix(2)
+            mix(1)
+            kron(0, 1)
+            kron(0, 2)
+            turn("v", 0, 0)
+            kron(0, 3)
+            kron(0, 0)
+            mix(1)
+            mix(0)
+            mix(0)
+            turn("v", 0, 1)
+            mix(2)
+            mix(3)
+            mix(3)
+            mix(1)
+            mix(1)
+            mix(0)
+            kron(0, 5)
+            kron(0, 4)
+            mix(0)
+            quant("v", 0)
+            spread_rows(0)
+            back(0, 0)
+            interleave(0)
+            back(0, 1)
+            spread_rows(1)
+            quant("b", 0)
+            turn("k", 0, 0)
+            quant("a", 0)
+            turn("k", 0, 1)
+            product(0, 0, 0)
+            quant("k", 0)
+            product(0, 0, 1)
+            mix(3)
+            for n in range(3):
+                mix(n + 2)
+                mix(n + 2)
+                turn("v", n + 1, 1)
+                turn("v", n + 1, 0)
+                back(n + 1, 0)
+                interleave(n + 1)
+                product(n, 1, 0)
+                mix(n + 2)
+                quant("b", n + 1)
+                quant("v", n + 1)
+                back(n + 1, 1)
+                turn("k", n + 1, 0)
+                turn("k", n + 1, 1)
+                product(n, 1, 1)
+                mix(n + 2)
+                if n + 5 < PAIRS:
+                    load_kv("v", n + 5)
+                product(n + 1, 0, 0)
+                quant("k", n + 1)
+                quant("a", n + 1)
+                product(n + 1, 0, 1)
+                spread_rows(n + 2)
+                kron(1, 2 * n)
+                if n + 5 < PAIRS:
+                    load_kv("k", n + 5)
+                kron(1, 2 * n + 1)
+            for n in range(3, PAIRS):
+                mix(n + 2)
+                mix(n + 2)
+                turn("v", n + 1, 1)
+                turn("v", n + 1, 0)
+                mix(n + 2)
+                interleave(n + 1)
+                product(n, 1, 0)
+                if n + 5 < PAIRS:
+                    load_kv("k", n + 5)
+                quant("v", n + 1)
+                quant("b", n + 1)
+                turn("k", n + 1, 1)
+                back(n + 1, 0)
+                turn("k", n + 1, 0)
+                mix(n + 2)
+                product(n, 1, 1)
+                back(n + 1, 1)
+                product(n + 1, 0, 0)
+                quant("k", n + 1)
+                quant("a", n + 1)
+                if n + 5 < PAIRS:
+                    load_kv("v", n + 5)
+                spread_rows(n + 2)
+                product(n + 1, 0, 1)

@@ -16,187 +16,157 @@ H, N, W, D = 2, 4, 512, 512
 P = 128
 PAIRS = H * N
 FLOPS = 2 * 2 * PAIRS * W * D * D
+BANKS = 8
+RAW_BUFS = 5
+RES_BUFS = 2
+CODE_BUFS = 2
 
 
 def tile_mhla_pa_v_kernel(tc, k_feat, v, w_piece, grad_out, out_0, out_1):
     nc = tc.nc
+    V, S = nc.vector, nc.scalar
     with ExitStack() as ctx:
         const = ctx.enter_context(tc.tile_pool(name="const", bufs=1))
         keep = ctx.enter_context(tc.tile_pool(name="keep", bufs=1))
         work = ctx.enter_context(tc.tile_pool(name="work", bufs=2))
-        psum = ctx.enter_context(tc.psum_pool(name="psum", bufs=8))
+        psum = ctx.enter_context(tc.psum_pool(name="psum", bufs=1))
+        ctx.enter_context(tc.manual_schedule())
 
-        w_rows = const.tile([P, N], BF16, name="w_rows")
-        nc.vector.memset(w_rows[:], 0.0)
-        nc.scalar.dma_start(out=w_rows[0:N, :], in_=w_piece)
-        ones = const.tile([P, P], BF16, name="ones", align_bytes=64)
-        nc.vector.memset(ones[:], 1.0)
-        ident = const.tile([P, P], BF16, name="ident")
-        make_identity(nc, ident[:])
-        ident_f = const.tile([P, P], F32, name="ident_f")
-        make_identity(nc, ident_f[:])
+        taken = []
+
+        def next_bank(dtype):
+            columns = 512 if dtype == F32 else 1024
+            tile = psum.tile([P, columns], dtype, name="bank%d" % (len(taken) % BANKS))
+            taken.append(tile)
+            return tile
+
+        def copy(engine, dst, src):
+            if engine is V:
+                nc.vector.tensor_copy(out=dst, in_=src)
+            else:
+                nc.scalar.copy(out=dst, in_=src)
 
         raw = {}
         g_mix = {}
         g_row = {}
 
         def load_kv(which, n, part=None):
+            if n >= PAIRS:
+                return
             h, j = divmod(n, N)
             if (which, n) not in raw:
-                raw[which, n] = keep.tile([P, 2048], BF16, name="raw_" + which, bufs=5, align_bytes=64)
+                raw[which, n] = keep.tile([P, 2048], BF16, name="raw_" + which, bufs=RAW_BUFS, align_bytes=64)
             src = (k_feat if which == "k" else v)[0, h, j].rearrange("(m b) d -> m (b d)", b=4)
             cols = slice(0, 2048) if part is None else slice(1024 * part, 1024 * part + 1024)
             nc.sync.dma_start(out=raw[which, n][:, cols], in_=src[:, cols])
 
         def load_rows(h, half):
-            if h not in g_row:
-                g_row[h] = keep.tile([P, N, 512], BF16, name="g_row" + str(h), align_bytes=64)
-            i0 = 2 * half
-            nc.sync.dma_start(
-                out=g_row[h][:, i0 : i0 + 2, :], in_=grad_out[0, h].rearrange("i q d -> q i d")[384:512, i0 : i0 + 2, :]
-            )
+            g_row[h, half] = keep.tile([P, 2, 512], BF16, name="g_row%d%d" % (h, half), align_bytes=64)
+            src = grad_out[0, h].rearrange("i q d -> q i d")[384:512, 2 * half : 2 * half + 2, :]
+            nc.sync.dma_start(out=g_row[h, half][:], in_=src)
 
-        def load_mix(h, half):
-            if h not in g_mix:
-                g_mix[h] = keep.tile([P, 12, 512], BF16, name="g_mix" + str(h), align_bytes=64)
+        def load_mix(h, x0, x1):
+            tile = keep.tile([P, x1 - x0, 512], BF16, name="g_mix%d_%d" % (h, x0), align_bytes=64)
+            for x in range(x0, x1):
+                g_mix[h, x] = tile[:, x - x0, :]
             for i in range(N):
                 src = grad_out[0, h, i].rearrange("(x r) d -> r x d", r=32)
-                nc.sync.dma_start(
-                    out=g_mix[h][i:P:4, 6 * half : 6 * half + 6, :], in_=src[:, 6 * half : 6 * half + 6, :]
-                )
+                nc.sync.dma_start(out=tile[i:P:4, :, :], in_=src[:, x0:x1, :])
 
-        load_mix(0, 0)
-        load_rows(0, 0)
-        load_kv("v", 0, 0)
-        load_rows(0, 1)
-        load_mix(0, 1)
-        load_kv("v", 0, 1)
-        load_kv("v", 1)
-        load_kv("k", 0)
-        load_mix(1, 1)
-        load_kv("k", 2)
-        load_kv("k", 1)
-        load_mix(1, 0)
-        load_kv("k", 4)
-        load_kv("v", 4)
-        load_kv("v", 2)
-        load_kv("k", 3)
-        load_kv("v", 3)
-        load_rows(1, 0)
-        load_rows(1, 1)
-
-        warm = const.tile([P, 1], F32, name="warm")
-        nc.vector.memset(warm[:], 0.0)
-        nc.scalar.copy(out=warm[:], in_=warm[:])
+        w_rows = const.tile([P, N], BF16, name="w_rows")
+        ident = const.tile([P, P], F32, name="ident")
+        ones = const.tile([P, P], BF16, name="ones", align_bytes=64)
         eye = const.tile([P, 32], F32, name="eye")
-        nc.vector.tensor_reduce(
-            out=eye[:].rearrange("p (u q e) -> p q u e", u=2, e=2),
-            in_=ident[:].rearrange("p (q u e i) -> p q u e i", u=2, e=2, i=4),
-            axis=mybir.AxisListType.X,
-            op=ADD,
-        )
         spread = const.tile([P, 32, N], BF16, name="spread", align_bytes=64)
-        nc.vector.tensor_copy(out=spread[:], in_=ident[:, 0:N].unsqueeze(1).to_broadcast([P, 32, N]))
         perm = const.tile([P, P], BF16, name="perm", align_bytes=64)
-        nc.vector.tensor_copy(
-            out=perm[:].rearrange("p (u q e) -> p q u e", u=2, e=2),
-            in_=ident[:].rearrange("p (q u e) -> p q u e", u=2, e=2),
-        )
         w_diag = const.tile([P, N, N], BF16, name="w_diag")
-        nc.vector.tensor_tensor(
-            out=w_diag[:],
-            in0=w_rows[:].unsqueeze(1).to_broadcast([P, N, N]),
-            in1=ident[:, 0:N].unsqueeze(2).to_broadcast([P, N, N]),
-            op=MULT,
-        )
-        w_bank = psum.tile([P, 512], F32, name="bank")
-        nc.tensor.matmul(
-            w_bank[:, 0:16], lhsT=ones[:], rhs=w_diag[:].rearrange("p i j -> p (i j)"), start=True, stop=True
-        )
-        nc.tensor.matmul(
-            w_bank[:, 16:20], lhsT=spread[:].rearrange("p r i -> p (r i)"), rhs=w_rows[:], start=True, stop=True
-        )
-        w_f = const.tile([P, 20], F32, name="w_f")
-        nc.vector.tensor_copy(out=w_f[:], in_=w_bank[:, 0:20])
+        w_all = const.tile([P, N * N], F32, name="w_all")
         mixer = const.tile([P, P], BF16, name="mixer", align_bytes=64)
-        nc.vector.tensor_tensor(
-            out=mixer[:].rearrange("p (j r) -> p j r", j=N),
-            in0=eye[:].unsqueeze(1).to_broadcast([P, N, 32]),
-            in1=w_f[:, 16:20].unsqueeze(2).to_broadcast([P, N, 32]),
-            op=MULT,
-        )
 
-        mixed = [keep.tile([P, 4, N, 512], BF16, name="mixed" + str(h), align_bytes=64) for h in range(H)]
-        b_in = {}
+        def patterns():
+            nc.vector.memset(w_rows[:], 0.0)
+            nc.scalar.dma_start(out=w_rows[0:N, :], in_=w_piece)
+            make_identity(nc, ident[:])
+            nc.vector.memset(ones[:], 1.0)
+            nc.scalar.copy(
+                out=perm[:].rearrange("p (u q e) -> p q u e", u=2, e=2),
+                in_=ident[:].rearrange("p (q u e) -> p q u e", u=2, e=2),
+            )
+            nc.vector.tensor_copy(out=spread[:], in_=ident[:, 0:N].unsqueeze(1).to_broadcast([P, 32, N]))
+            nc.vector.tensor_reduce(
+                out=eye[:].rearrange("p (u q e) -> p q u e", u=2, e=2),
+                in_=ident[:].rearrange("p (q u e i) -> p q u e i", u=2, e=2, i=4),
+                axis=mybir.AxisListType.X,
+                op=ADD,
+            )
+
+        def constants():
+            nc.vector.tensor_tensor(
+                out=w_diag[:],
+                in0=w_rows[:].unsqueeze(1).to_broadcast([P, N, N]),
+                in1=ident[:, 0:N].unsqueeze(2).to_broadcast([P, N, N]),
+                op=MULT,
+            )
+            bank = next_bank(F32)
+            nc.tensor.matmul(
+                bank[:, 16:20], lhsT=spread[:].rearrange("p r i -> p (r i)"), rhs=w_rows[:], start=True, stop=True
+            )
+            nc.tensor.matmul(
+                bank[:, 0:16], lhsT=ones[:], rhs=w_diag[:].rearrange("p i j -> p (i j)"), start=True, stop=True
+            )
+            nc.vector.tensor_tensor(
+                out=mixer[:].rearrange("p (j r) -> p j r", j=N),
+                in0=eye[:].unsqueeze(1).to_broadcast([P, N, 32]),
+                in1=bank[:, 16:20].unsqueeze(2).to_broadcast([P, N, 32]),
+                op=MULT,
+            )
+            nc.vector.tensor_copy(out=w_all[:], in_=bank[:, 0:16])
+
+        mixed = [keep.tile([P, 4, N, 512], BF16, name="mixed%d" % h, align_bytes=64) for h in range(H)]
         acc = {}
-        mixed_terms = {}
         row = {}
+        b_in = {}
         a_in = {}
         grouped = {}
         codes = {}
-        on_vector = set("mul-5 mul-6 mul-4 mul-7 rows-0 back-7-0 rows-7 k-0-0 k-7-0 out-6-0-1 out-7-0-0 v-7-0 k-3-0 out-3-1-3 k-3-1 back-5-1 out-5-1-2 v-6-1 k-1-0 rows-4 mul-0 out-1-0-0 back-2-1 out-1-0-3 out-1-1-3 out-1-1-2 out-3-1-1 out-3-0-0 mul-2 out-1-0-1 out-7-1-0".split())
+        results = {}
 
-        def copy_out(dst, src, *key):
-            if "-".join(str(x) for x in key) in on_vector:
-                nc.vector.tensor_copy(out=dst, in_=src)
-            else:
-                nc.scalar.copy(out=dst, in_=src)
-
-        def f32_bank():
-            return psum.tile([P, 512], F32, name="bank")
-
-        def bf16_bank():
-            return psum.tile([P, 1024], BF16, name="bank")
-
-        def mix(n):
-            if n >= PAIRS:
-                return
-            i = mixed_terms.get(n, 0)
-            if i == N:
-                return
-            mixed_terms[n] = i + 1
+        def nmix(n, i, engine=V):
             h, j = divmod(n, N)
-            w_ij = w_f[:, 4 * i + j : 4 * i + j + 1]
-            src = g_row[h][:, i, :].rearrange("m (p t) -> m t p", t=4)
+            w_ij = w_all[:, N * i + j : N * i + j + 1]
+            src = g_row[h, i // 2][:, i % 2, :].rearrange("m (p t) -> m t p", t=4)
             if i == 0:
                 acc[n] = work.tile([P, 4, 128], F32, name="acc", bufs=4)
-                if "mul-" + str(n) in on_vector:
-                    nc.vector.tensor_scalar(out=acc[n][:], in0=src, scalar1=w_ij, scalar2=None, op0=MULT)
-                else:
-                    nc.scalar.activation(
-                        out=acc[n][:], in_=src, func=mybir.ActivationFunctionType.Copy, scale=w_ij
-                    )
+                nc.vector.tensor_scalar(out=acc[n][:], in0=src, scalar1=w_ij, scalar2=None, op0=MULT)
                 return
-            if i == 3:
+            if i == N - 1:
                 row[n] = work.tile([P, 4, 128], BF16, name="row", bufs=4, align_bytes=64)
-            dst = row[n] if i == 3 else acc[n]
+            dst = row[n] if i == N - 1 else acc[n]
             nc.vector.scalar_tensor_tensor(out=dst[:], in0=src, scalar=w_ij, in1=acc[n][:], op0=MULT, op1=ADD)
 
-        def spread_rows(n):
+        def rows(n, engine):
             if n >= PAIRS:
                 return
             h, j = divmod(n, N)
-            bank = bf16_bank()
+            bank = next_bank(BF16)
             for t in range(4):
                 nc.tensor.transpose(bank[:, 128 * t : 128 * t + 128], row[n][:, t, :], perm[:])
             dst = mixed[h][:, :, j, :].rearrange("p t (u q) -> p t u q", u=2)
-            copy_out(dst[:, :, :, 192:256], bank[:, 0:512].rearrange("p (t u q) -> p t u q", t=4, u=2), "rows", n)
+            copy(engine, dst[:, :, :, 192:256], bank[:, 0:512].rearrange("p (t u q) -> p t u q", t=4, u=2))
 
-        def kron(h, x):
-            bank = bf16_bank()
+        def kron(h, x, engine):
+            bank = next_bank(BF16)
             for g in range(2):
                 for t in range(4):
                     c0 = 512 * g + 128 * t
                     nc.tensor.matmul(
-                        bank[:, c0 : c0 + 128],
-                        lhsT=g_mix[h][:, 2 * x + g, t:512:4],
-                        rhs=mixer[:],
-                        start=True,
-                        stop=True,
+                        bank[:, c0 : c0 + 128], lhsT=g_mix[h, 2 * x + g][:, t:512:4], rhs=mixer[:], start=True, stop=True
                     )
             dst = mixed[h][:].rearrange("p t j (u q) -> p (t j u) q", u=2)[:, :, 32 * x : 32 * x + 32]
-            copy_out(
-                dst.rearrange("p a (g y) -> p a g y", g=2), bank[:].rearrange("p (g a y) -> p a g y", g=2, y=16), "mix", h, x
+            copy(
+                engine,
+                dst.rearrange("p a (g y) -> p a g y", g=2),
+                bank[:].rearrange("p (g a y) -> p a g y", g=2, y=16),
             )
 
         def interleave(n):
@@ -209,189 +179,145 @@ def tile_mhla_pa_v_kernel(tc, k_feat, v, w_piece, grad_out, out_0, out_1):
                 in_=mixed[h][:, :, j, :].rearrange("p t (c i) -> p c t i", i=4),
             )
 
-        def turn(which, n, half):
+        def turn(which, n, half, engine):
             if n >= PAIRS:
                 return
             if (which, n) not in grouped:
                 grouped[which, n] = work.tile([P, 2048], BF16, name="grouped_" + which, align_bytes=64)
             words = raw[which, n][:].bitcast(F32)
-            bank = f32_bank()
+            bank = next_bank(F32)
             for b in range(2):
                 for u in range(2):
                     w0 = 256 * (2 * half + b)
-                    nc.tensor.transpose(
-                        bank[:, 256 * b + 128 * u : 256 * b + 128 * u + 128], words[:, w0 + u : w0 + 256 : 2], ident_f[:]
-                    )
+                    c0 = 256 * b + 128 * u
+                    nc.tensor.transpose(bank[:, c0 : c0 + 128], words[:, w0 + u : w0 + 256 : 2], ident[:])
             dst = grouped[which, n][:].bitcast(F32)[:, 512 * half : 512 * half + 512]
-            copy_out(
+            copy(
+                engine,
                 dst.rearrange("p (b m u) -> p b m u", b=2, u=2),
                 bank[:].rearrange("p (b u m) -> p b m u", b=2, u=2),
-                which,
-                n,
-                half,
             )
 
-        def quant(which, n):
-            if n >= PAIRS:
-                return
-            h, j = divmod(n, N)
-            if which == "b":
-                src, fmt = b_in[n][:], E5M2
-            elif which == "a":
-                src, fmt = a_in[n][:], E5M2
-            else:
-                src, fmt = grouped[which, n][:], E4M3
-            depth = 2 if which in "ab" else 5
-            c = work.tile([P, 512], U32, name="codes_" + which, bufs=depth, align_bytes=64)
-            sc = work.tile([P, 512], U8, name="scales_" + which, bufs=depth, align_bytes=64)
-            nc.vector.quantize_mx(out=c[:].bitcast(fmt), scales=sc[:], in_=src)
-            codes[which, n] = (c, sc)
-
-        def back(n, half):
+        def back(n, half, engine):
             if n >= PAIRS:
                 return
             h, j = divmod(n, N)
             if n not in a_in:
                 a_in[n] = work.tile([P, 2048], BF16, name="a_in", align_bytes=64)
             words = mixed[h][:].rearrange("p t j c -> p (t j c)").bitcast(F32)
-            bank = f32_bank()
+            bank = next_bank(F32)
             for tt in range(2):
                 for u in range(2):
                     c0 = 256 * tt + 128 * u
                     w0 = 256 * (N * (2 * half + tt) + j) + 128 * u
-                    nc.tensor.transpose(bank[:, c0 : c0 + 128], words[:, w0 : w0 + 128], ident_f[:])
+                    nc.tensor.transpose(bank[:, c0 : c0 + 128], words[:, w0 : w0 + 128], ident[:])
             dst = a_in[n][:].bitcast(F32)[:, 512 * half : 512 * half + 512]
-            copy_out(
+            copy(
+                engine,
                 dst.rearrange("q (t p u) -> q t p u", t=2, u=2),
                 bank[:].rearrange("q (t u p) -> q t p u", t=2, u=2),
-                "back",
-                n,
-                half,
             )
 
-        results = {}
-
-        def product(n, which, pair):
+        def quant(which, n):
             if n >= PAIRS:
                 return
-            h, j = divmod(n, N)
-            left, right, dram = ("v", "b", out_0) if which == 0 else ("k", "a", out_1)
+            if which == "b":
+                src, fmt = b_in[n], E5M2
+            elif which == "a":
+                src, fmt = a_in[n], E5M2
+            else:
+                src, fmt = grouped[which, n], E4M3
+            c = work.tile([P, 512], U32, name="codes_" + which, bufs=CODE_BUFS, align_bytes=64)
+            sc = work.tile([P, 512], U8, name="scales_" + which, bufs=CODE_BUFS, align_bytes=64)
+            nc.vector.quantize_mx(out=c[:].bitcast(fmt), scales=sc[:], in_=src[:])
+            codes[which, n] = (c, sc)
+
+        def product(n, which, b, engine):
+            left, right = ("v", "b") if which == 0 else ("k", "a")
             lc, ls = codes[left, n]
             rc, rs = codes[right, n]
-            if pair == 0:
-                results[which] = work.tile([P, 4, 512], F32, name="res" + str(which))
-            res = results[which]
-            view = dram[0, h, j].rearrange("(m b) d -> m b d", b=4)
-            for b in range(2 * pair, 2 * pair + 2):
-                bank = f32_bank()
-                cols = slice(128 * b, 128 * b + 128)
-                nc.tensor.matmul_mx(
-                    out=bank[:],
-                    lhsT=lc[:, cols].bitcast(E4M3),
-                    lhsT_scale=ls[:, cols],
-                    rhs=rc[:].bitcast(E5M2),
-                    rhs_scale=rs[:],
-                    start=True,
-                    stop=True,
+            if b == 0:
+                results[which] = work.tile([P, 4, 512], F32, name="res%d" % which, bufs=RES_BUFS)
+            bank = next_bank(F32)
+            cols = slice(128 * b, 128 * b + 128)
+            nc.tensor.matmul_mx(
+                out=bank[:],
+                lhsT=lc[:, cols].bitcast(E4M3),
+                lhsT_scale=ls[:, cols],
+                rhs=rc[:].bitcast(E5M2),
+                rhs_scale=rs[:],
+                start=True,
+                stop=True,
+            )
+            res = results[which][:, b, :]
+            if which == 0:
+                copy(
+                    engine,
+                    res.rearrange("m (q u e) -> m q u e", u=2, e=2),
+                    bank[:].rearrange("m (u q e) -> m q u e", u=2, e=2),
                 )
-                if which == 0:
-                    dst = res[:, b, :].rearrange("m (q u e) -> m q u e", u=2, e=2)
-                    src = bank[:].rearrange("m (u q e) -> m q u e", u=2, e=2)
-                else:
-                    dst = res[:, b, :].rearrange("m (p t) -> m p t", t=4)
-                    src = bank[:].rearrange("m (t p) -> m p t", t=4)
-                copy_out(dst, src, "out", n, which, b)
-                if n == PAIRS - 1 and which == 1:
-                    nc.sync.dma_start(out=view[:, b, :], in_=res[:, b, :])
-            if not (n == PAIRS - 1 and which == 1):
-                nc.sync.dma_start(out=view[:, 2 * pair : 2 * pair + 2, :], in_=res[:, 2 * pair : 2 * pair + 2, :])
+            else:
+                copy(engine, res.rearrange("m (p t) -> m p t", t=4), bank[:].rearrange("m (t p) -> m p t", t=4))
 
-        with tc.manual_schedule():
-            mix(2)
-            mix(3)
-            mix(2)
-            mix(1)
-            kron(0, 1)
-            kron(0, 2)
-            turn("v", 0, 0)
-            kron(0, 3)
-            kron(0, 0)
-            mix(1)
-            mix(0)
-            mix(0)
-            turn("v", 0, 1)
-            mix(2)
-            mix(3)
-            mix(3)
-            mix(1)
-            mix(1)
-            mix(0)
-            kron(0, 5)
-            kron(0, 4)
-            mix(0)
-            quant("v", 0)
-            spread_rows(0)
-            back(0, 0)
-            interleave(0)
-            back(0, 1)
-            spread_rows(1)
-            quant("b", 0)
-            turn("k", 0, 0)
-            quant("a", 0)
-            turn("k", 0, 1)
-            product(0, 0, 0)
-            quant("k", 0)
-            product(0, 0, 1)
-            mix(3)
-            for n in range(3):
-                mix(n + 2)
-                mix(n + 2)
-                turn("v", n + 1, 1)
-                turn("v", n + 1, 0)
-                back(n + 1, 0)
-                interleave(n + 1)
-                product(n, 1, 0)
-                mix(n + 2)
-                quant("b", n + 1)
-                quant("v", n + 1)
-                back(n + 1, 1)
-                turn("k", n + 1, 0)
-                turn("k", n + 1, 1)
-                product(n, 1, 1)
-                mix(n + 2)
-                if n + 5 < PAIRS:
-                    load_kv("v", n + 5)
-                product(n + 1, 0, 0)
-                quant("k", n + 1)
-                quant("a", n + 1)
-                product(n + 1, 0, 1)
-                spread_rows(n + 2)
-                kron(1, 2 * n)
-                if n + 5 < PAIRS:
-                    load_kv("k", n + 5)
-                kron(1, 2 * n + 1)
-            for n in range(3, PAIRS):
-                mix(n + 2)
-                mix(n + 2)
-                turn("v", n + 1, 1)
-                turn("v", n + 1, 0)
-                mix(n + 2)
-                interleave(n + 1)
-                product(n, 1, 0)
-                if n + 5 < PAIRS:
-                    load_kv("k", n + 5)
-                quant("v", n + 1)
-                quant("b", n + 1)
-                turn("k", n + 1, 1)
-                back(n + 1, 0)
-                turn("k", n + 1, 0)
-                mix(n + 2)
-                product(n, 1, 1)
-                back(n + 1, 1)
-                product(n + 1, 0, 0)
-                quant("k", n + 1)
-                quant("a", n + 1)
-                if n + 5 < PAIRS:
-                    load_kv("v", n + 5)
-                spread_rows(n + 2)
-                product(n + 1, 0, 1)
+        def store(n, which, b0, b1):
+            h, j = divmod(n, N)
+            view = (out_0 if which == 0 else out_1)[0, h, j].rearrange("(m b) d -> m b d", b=4)
+            nc.sync.dma_start(out=view[:, b0:b1, :], in_=results[which][:, b0:b1, :])
+
+        patterns()
+        load_kv("v",0,0); load_mix(0,0,2); load_rows(0,0); load_kv("v",0,1); load_mix(0,2,6); load_rows(0,1); load_mix(0,6,12)
+        load_kv("k",0); load_kv("v",1); load_mix(1,0,6); load_kv("k",1); load_rows(1,0); load_kv("v",2); load_rows(1,1); load_mix(1,6,12); load_kv("k",2); load_kv("v",3); load_kv("k",3); load_kv("v",4); load_kv("k",4)
+        constants()
+        turn("v",0,0,V)
+        kron(0,0,S)
+        turn("v",0,1,S)
+        for j in range(4): nmix(j,0,V)
+        kron(0,1,S)
+        for j in range(2): nmix(j,1)
+        quant("v",0)
+        kron(0,2,S)
+        nmix(0,2); nmix(1,2); nmix(0,3); nmix(1,3)
+        kron(0,3,S)
+        nmix(2,1); nmix(3,1); nmix(2,2); nmix(3,2)
+        kron(0,4,S)
+        rows(0,S); rows(1,S)
+        kron(0,5,S)
+        todo=[(2,3),(3,3)]+[(n+j,i) for n in (4,6) for i in range(4) for j in range(2)]
+        def fill(c):
+            for q in range(c):
+                if todo:
+                    n,i=todo.pop(0); nmix(n,i,V)
+
+        turn("k",0,0,S); turn("k",0,1,S)
+        interleave(0)
+        back(0,0,S); back(0,1,S)
+        turn("v",1,0,S)
+        quant("k",0)
+        quant("b",0)
+        kron(1,0,S)
+        for n in range(PAIRS):
+            early = n<3
+            E = S if early else V
+            if n: turn("k",n,0,S); turn("k",n,1,E)
+            quant("a",n)
+            product(n,0,0,S); product(n,0,1,S)
+            if n: quant("k",n)
+            store(n,0,0,2)
+            if n: turn("v",n+1,0,S)
+            interleave(n+1)
+            if early and n: kron(1,2*n,S)
+            fill(2)
+            product(n,0,2,S); product(n,0,3,V)
+            store(n,0,2,4)
+            turn("v",n+1,1,S)
+            quant("b",n+1)
+            fill(2)
+            product(n,1,0,S); product(n,1,1,E)
+            store(n,1,0,2)
+            back(n+1,0,S); back(n+1,1,S); rows(n+2,S)
+            quant("v",n+1)
+            if early: kron(1,2*n+1,S)
+            fill(2)
+            product(n,1,2,S); product(n,1,3,V)
+            store(n,1,2,4)
+            load_kv("v",n+5); load_kv("k",n+5)

@@ -218,7 +218,7 @@ def tile_mhla_pa_v_kernel(tc, k_feat, v, w_piece, grad_out, out_0, out_1):
                 bank[:].rearrange("q (t u p) -> q t p u", t=2, u=2),
             )
 
-        def quant(which, n):
+        def quant(which, n, half=None):
             if n >= PAIRS:
                 return
             if which == "b":
@@ -227,10 +227,13 @@ def tile_mhla_pa_v_kernel(tc, k_feat, v, w_piece, grad_out, out_0, out_1):
                 src, fmt = a_in[n], E5M2
             else:
                 src, fmt = grouped[which, n], E4M3
-            c = work.tile([P, 512], U32, name="codes_" + which, bufs=CODE_BUFS, align_bytes=64)
-            sc = work.tile([P, 512], U8, name="scales_" + which, bufs=CODE_BUFS, align_bytes=64)
-            nc.vector.quantize_mx(out=c[:].bitcast(fmt), scales=sc[:], in_=src[:])
-            codes[which, n] = (c, sc)
+            if (which, n) not in codes:
+                c = work.tile([P, 512], U32, name="codes_" + which, bufs=CODE_BUFS, align_bytes=64)
+                sc = work.tile([P, 512], U8, name="scales_" + which, bufs=CODE_BUFS, align_bytes=64)
+                codes[which, n] = (c, sc)
+            c, sc = codes[which, n]
+            c0, c1 = (0, 512) if half is None else (256 * half, 256 * half + 256)
+            nc.vector.quantize_mx(out=c[:, c0:c1].bitcast(fmt), scales=sc[:, c0:c1], in_=src[:, 4 * c0 : 4 * c1])
 
         def product(n, which, b, engine):
             left, right = ("v", "b") if which == 0 else ("k", "a")
@@ -265,59 +268,67 @@ def tile_mhla_pa_v_kernel(tc, k_feat, v, w_piece, grad_out, out_0, out_1):
             nc.sync.dma_start(out=view[:, b0:b1, :], in_=results[which][:, b0:b1, :])
 
         patterns()
-        load_kv("v",0,0); load_mix(0,0,2); load_rows(0,0); load_kv("v",0,1); load_mix(0,2,6); load_rows(0,1); load_mix(0,6,12)
-        load_kv("k",0); load_kv("v",1); load_mix(1,0,6); load_kv("k",1); load_rows(1,0); load_kv("v",2); load_rows(1,1); load_mix(1,6,12); load_kv("k",2); load_kv("v",3); load_kv("k",3); load_kv("v",4); load_kv("k",4)
-        constants()
-        turn("v",0,0,V)
-        kron(0,0,S)
-        turn("v",0,1,S)
-        for j in range(4): nmix(j,0,V)
-        kron(0,1,S)
-        for j in range(2): nmix(j,1)
-        quant("v",0)
-        kron(0,2,S)
-        nmix(0,2); nmix(1,2); nmix(0,3); nmix(1,3)
-        kron(0,3,S)
-        nmix(2,1); nmix(3,1); nmix(2,2); nmix(3,2)
-        kron(0,4,S)
-        rows(0,S); rows(1,S)
-        kron(0,5,S)
-        todo=[(2,3),(3,3)]+[(n+j,i) for n in (4,6) for i in range(4) for j in range(2)]
+        load_kv("v",0,0); load_mix(0,0,2); load_mix(0,2,6); load_rows(0,0); load_mix(0,6,10); load_rows(0,1); load_mix(0,10,12); load_kv("v",0,1)
+        load_kv("k",0); load_mix(1,0,2); load_kv("v",1); load_mix(1,2,6); load_kv("k",1); load_rows(1,0); load_kv("v",2); load_rows(1,1); load_mix(1,6,12); load_kv("k",2); load_kv("v",3); load_kv("k",3); load_kv("v",4); load_kv("k",4)
+        todo=[(n+j,i) for n in (0,2,4,6) for i in range(4) for j in range(2)]
         def fill(c):
             for q in range(c):
                 if todo:
                     n,i=todo.pop(0); nmix(n,i,V)
-
+        constants()
+        turn("v",0,0,S)
+        for x in range(6): kron(0,x,S)
+        fill(8)
+        rows(0,S)
+        turn("v",0,1,S)
+        fill(4)
         turn("k",0,0,S); turn("k",0,1,S)
         interleave(0)
         back(0,0,S); back(0,1,S)
-        turn("v",1,0,S)
-        quant("k",0)
+        quant("v",0)
         quant("b",0)
         kron(1,0,S)
-        for n in range(PAIRS):
+        quant("k",0)
+
+        for n in range(PAIRS - 1):
             early = n<3
             E = S if early else V
-            if n: turn("k",n,0,S); turn("k",n,1,E)
             quant("a",n)
-            product(n,0,0,S); product(n,0,1,S)
-            if n: quant("k",n)
+            if n: turn("k",n,0,S); turn("k",n,1,V)
+            rows(n+1,S)
+            product(n,0,0,E); product(n,0,1,S)
             store(n,0,0,2)
-            if n: turn("v",n+1,0,S)
+            if n: quant("k",n)
+            product(n,0,2,S)
             interleave(n+1)
-            if early and n: kron(1,2*n,S)
-            fill(2)
-            product(n,0,2,S); product(n,0,3,V)
-            store(n,0,2,4)
+            turn("v",n+1,0,S)
             turn("v",n+1,1,S)
-            quant("b",n+1)
             fill(2)
-            product(n,1,0,S); product(n,1,1,E)
+            if early and n: kron(1,2*n,S)
+            product(n,0,3,S)
+            store(n,0,2,4)
+            product(n,1,0,V); product(n,1,1,S)
             store(n,1,0,2)
-            back(n+1,0,S); back(n+1,1,S); rows(n+2,S)
+            quant("b",n+1)
             quant("v",n+1)
-            if early: kron(1,2*n+1,S)
             fill(2)
-            product(n,1,2,S); product(n,1,3,V)
+            back(n+1,0,S); back(n+1,1,S)
+            if early: kron(1,2*n+1,S)
+            fill(3)
+            product(n,1,2,S); product(n,1,3,E)
             store(n,1,2,4)
             load_kv("v",n+5); load_kv("k",n+5)
+
+        n = PAIRS - 1
+        turn("k",n,0,S)
+        product(n,0,0,S); product(n,0,1,V)
+        store(n,0,0,2)
+        turn("k",n,1,S)
+        quant("a",n)
+        quant("k",n,0)
+        product(n,0,2,S); product(n,0,3,V)
+        store(n,0,2,4)
+        quant("k",n,1)
+        product(n,1,0,S); product(n,1,1,V)
+        store(n,1,0,2)
+        product(n,1,2,S); store(n,1,2,3); product(n,1,3,V); store(n,1,3,4)

@@ -18,6 +18,7 @@ PAIRS = H * N
 FLOPS = 2 * 2 * PAIRS * W * D * D
 BANKS = 8
 RAW_BUFS = 5
+RAW2_BUFS = 2
 RES_BUFS = 2
 CODE_BUFS = 2
 
@@ -55,10 +56,19 @@ def tile_mhla_pa_v_kernel(tc, k_feat, v, w_piece, grad_out, out_0, out_1):
                 return
             h, j = divmod(n, N)
             if (which, n) not in raw:
-                raw[which, n] = keep.tile([P, 2048], BF16, name="raw_" + which, bufs=RAW_BUFS, align_bytes=64)
+                tile = keep.tile([P, 2048], BF16, name="raw_" + which, bufs=RAW_BUFS, align_bytes=64)
+                raw[which, n] = tile[:]
             src = (k_feat if which == "k" else v)[0, h, j].rearrange("(m b) d -> m (b d)", b=4)
             cols = slice(0, 2048) if part is None else slice(1024 * part, 1024 * part + 1024)
             nc.sync.dma_start(out=raw[which, n][:, cols], in_=src[:, cols])
+
+        def load_kv_two(which, n):
+            h, j = divmod(n, N)
+            tile = keep.tile([P, 2, 2048], BF16, name="raw2_" + which, bufs=RAW2_BUFS, align_bytes=64)
+            src = (k_feat if which == "k" else v)[0, h, j : j + 2].rearrange("j (m b) d -> m j (b d)", b=4)
+            nc.sync.dma_start(out=tile[:], in_=src)
+            raw[which, n] = tile[:, 0, :]
+            raw[which, n + 1] = tile[:, 1, :]
 
         def load_rows(h, half):
             g_row[h, half] = keep.tile([P, 2, 512], BF16, name="g_row%d%d" % (h, half), align_bytes=64)
@@ -78,7 +88,6 @@ def tile_mhla_pa_v_kernel(tc, k_feat, v, w_piece, grad_out, out_0, out_1):
         ones = const.tile([P, P], BF16, name="ones", align_bytes=64)
         eye = const.tile([P, 32], F32, name="eye")
         spread = const.tile([P, 32, N], BF16, name="spread", align_bytes=64)
-        perm = const.tile([P, P], BF16, name="perm", align_bytes=64)
         w_diag = const.tile([P, N, N], BF16, name="w_diag")
         w_all = const.tile([P, N * N], F32, name="w_all")
         mixer = const.tile([P, P], BF16, name="mixer", align_bytes=64)
@@ -88,11 +97,7 @@ def tile_mhla_pa_v_kernel(tc, k_feat, v, w_piece, grad_out, out_0, out_1):
             nc.scalar.dma_start(out=w_rows[0:N, :], in_=w_piece)
             make_identity(nc, ident[:])
             nc.vector.memset(ones[:], 1.0)
-            nc.scalar.copy(
-                out=perm[:].rearrange("p (u q e) -> p q u e", u=2, e=2),
-                in_=ident[:].rearrange("p (q u e) -> p q u e", u=2, e=2),
-            )
-            nc.vector.tensor_copy(out=spread[:], in_=ident[:, 0:N].unsqueeze(1).to_broadcast([P, 32, N]))
+            nc.scalar.copy(out=spread[:], in_=ident[:, 0:N].unsqueeze(1).to_broadcast([P, 32, N]))
             nc.vector.tensor_reduce(
                 out=eye[:].rearrange("p (u q e) -> p q u e", u=2, e=2),
                 in_=ident[:].rearrange("p (q u e i) -> p q u e i", u=2, e=2, i=4),
@@ -131,28 +136,41 @@ def tile_mhla_pa_v_kernel(tc, k_feat, v, w_piece, grad_out, out_0, out_1):
         codes = {}
         results = {}
 
+        def b_tile(n):
+            if n not in b_in:
+                b_in[n] = work.tile([P, 2048], BF16, name="b_in", align_bytes=64)
+            return b_in[n]
+
         def nmix(n, i, engine=V):
             h, j = divmod(n, N)
             w_ij = w_all[:, N * i + j : N * i + j + 1]
-            src = g_row[h, i // 2][:, i % 2, :].rearrange("m (p t) -> m t p", t=4)
+            src = g_row[h, i // 2][:, i % 2, :]
             if i == 0:
-                acc[n] = work.tile([P, 4, 128], F32, name="acc", bufs=4)
+                acc[n] = work.tile([P, 512], F32, name="acc", bufs=4)
                 nc.vector.tensor_scalar(out=acc[n][:], in0=src, scalar1=w_ij, scalar2=None, op0=MULT)
                 return
             if i == N - 1:
-                row[n] = work.tile([P, 4, 128], BF16, name="row", bufs=4, align_bytes=64)
+                row[n] = work.tile([P, 512], BF16, name="row", bufs=4, align_bytes=64)
             dst = row[n] if i == N - 1 else acc[n]
             nc.vector.scalar_tensor_tensor(out=dst[:], in0=src, scalar=w_ij, in1=acc[n][:], op0=MULT, op1=ADD)
 
         def rows(n, engine):
             if n >= PAIRS:
                 return
+            words = row[n][:].bitcast(F32)
+            bank = next_bank(F32)
+            for w in range(2):
+                nc.tensor.transpose(bank[:, 128 * w : 128 * w + 128], words[:, w:256:2], ident[:])
+            dst = b_tile(n)[:].bitcast(F32).rearrange("p (u q e w) -> p u q e w", u=2, e=2, w=2)
+            copy(engine, dst[:, :, 96:128, :, :], bank[:, 0:256].rearrange("p (w q u e) -> p u q e w", w=2, u=2, e=2))
+
+        def deinterleave(n):
+            if n >= PAIRS:
+                return
             h, j = divmod(n, N)
-            bank = next_bank(BF16)
-            for t in range(4):
-                nc.tensor.transpose(bank[:, 128 * t : 128 * t + 128], row[n][:, t, :], perm[:])
-            dst = mixed[h][:, :, j, :].rearrange("p t (u q) -> p t u q", u=2)
-            copy(engine, dst[:, :, :, 192:256], bank[:, 0:512].rearrange("p (t u q) -> p t u q", t=4, u=2))
+            dst = mixed[h][:, :, j, :].rearrange("p t (u c i) -> p u c t i", u=2, i=8)
+            src = b_tile(n)[:].rearrange("p (u c i t) -> p u c t i", u=2, i=8, t=4)
+            nc.vector.tensor_copy(out=dst[:, :, 24:32, :, :], in_=src[:, :, 24:32, :, :])
 
         def kron(h, x, engine):
             bank = next_bank(BF16)
@@ -173,18 +191,16 @@ def tile_mhla_pa_v_kernel(tc, k_feat, v, w_piece, grad_out, out_0, out_1):
             if n >= PAIRS:
                 return
             h, j = divmod(n, N)
-            b_in[n] = work.tile([P, 2048], BF16, name="b_in", align_bytes=64)
-            nc.vector.tensor_copy(
-                out=b_in[n][:].rearrange("p (c i t) -> p c t i", i=4, t=4),
-                in_=mixed[h][:, :, j, :].rearrange("p t (c i) -> p c t i", i=4),
-            )
+            dst = b_tile(n)[:].rearrange("p (u c i t) -> p u c t i", u=2, i=4, t=4)
+            src = mixed[h][:, :, j, :].rearrange("p t (u c i) -> p u c t i", u=2, i=4)
+            nc.vector.tensor_copy(out=dst[:, :, 0:48, :, :], in_=src[:, :, 0:48, :, :])
 
         def turn(which, n, half, engine):
             if n >= PAIRS:
                 return
             if (which, n) not in grouped:
                 grouped[which, n] = work.tile([P, 2048], BF16, name="grouped_" + which, align_bytes=64)
-            words = raw[which, n][:].bitcast(F32)
+            words = raw[which, n].bitcast(F32)
             bank = next_bank(F32)
             for b in range(2):
                 for u in range(2):
@@ -283,6 +299,7 @@ def tile_mhla_pa_v_kernel(tc, k_feat, v, w_piece, grad_out, out_0, out_1):
         turn("v",0,1,S)
         fill(4)
         turn("k",0,0,S); turn("k",0,1,S)
+        deinterleave(0)
         interleave(0)
         back(0,0,S); back(0,1,S)
         quant("v",0)
@@ -300,6 +317,7 @@ def tile_mhla_pa_v_kernel(tc, k_feat, v, w_piece, grad_out, out_0, out_1):
             store(n,0,0,2)
             if n: quant("k",n)
             product(n,0,2,S)
+            deinterleave(n+1)
             interleave(n+1)
             turn("v",n+1,0,S)
             turn("v",n+1,1,S)

@@ -19,7 +19,7 @@ FLOPS = 2 * 2 * PAIRS * W * D * D
 BANKS = 8
 RAW_BUFS = 5
 RAW2_BUFS = 2
-RES_BUFS = 2
+RES_BUFS = 3
 CODE_BUFS = 2
 
 
@@ -147,7 +147,10 @@ def tile_mhla_pa_v_kernel(tc, k_feat, v, w_piece, grad_out, out_0, out_1):
             src = g_row[h, i // 2][:, i % 2, :]
             if i == 0:
                 acc[n] = work.tile([P, 512], F32, name="acc", bufs=4)
-                nc.vector.tensor_scalar(out=acc[n][:], in0=src, scalar1=w_ij, scalar2=None, op0=MULT)
+                if engine is V:
+                    nc.vector.tensor_scalar(out=acc[n][:], in0=src, scalar1=w_ij, scalar2=None, op0=MULT)
+                else:
+                    nc.scalar.activation(out=acc[n][:], in_=src, func=mybir.ActivationFunctionType.Copy, scale=w_ij)
                 return
             if i == N - 1:
                 row[n] = work.tile([P, 512], BF16, name="row", bufs=4, align_bytes=64)
@@ -180,20 +183,21 @@ def tile_mhla_pa_v_kernel(tc, k_feat, v, w_piece, grad_out, out_0, out_1):
                     nc.tensor.matmul(
                         bank[:, c0 : c0 + 128], lhsT=g_mix[h, 2 * x + g][:, t:512:4], rhs=mixer[:], start=True, stop=True
                     )
-            dst = mixed[h][:].rearrange("p t j (u q) -> p (t j u) q", u=2)[:, :, 32 * x : 32 * x + 32]
+            words = mixed[h][:].rearrange("p t j c -> p (t j c)").bitcast(F32)
+            dst = words.rearrange("p (a q) -> p a q", q=128)[:, :, 16 * x : 16 * x + 16]
             copy(
                 engine,
                 dst.rearrange("p a (g y) -> p a g y", g=2),
-                bank[:].rearrange("p (g a y) -> p a g y", g=2, y=16),
+                bank[:].bitcast(F32).rearrange("p (g a y) -> p a g y", g=2, y=8),
             )
 
-        def interleave(n):
+        def interleave(n, engine=V, x0=0, x1=6):
             if n >= PAIRS:
                 return
             h, j = divmod(n, N)
             dst = b_tile(n)[:].rearrange("p (u c i t) -> p u c t i", u=2, i=4, t=4)
             src = mixed[h][:, :, j, :].rearrange("p t (u c i) -> p u c t i", u=2, i=4)
-            nc.vector.tensor_copy(out=dst[:, :, 0:48, :, :], in_=src[:, :, 0:48, :, :])
+            engine.tensor_copy(out=dst[:, :, 8 * x0 : 8 * x1, :, :], in_=src[:, :, 8 * x0 : 8 * x1, :, :])
 
         def turn(which, n, half, engine):
             if n >= PAIRS:
@@ -284,57 +288,65 @@ def tile_mhla_pa_v_kernel(tc, k_feat, v, w_piece, grad_out, out_0, out_1):
             nc.sync.dma_start(out=view[:, b0:b1, :], in_=results[which][:, b0:b1, :])
 
         patterns()
-        load_kv("v",0,0); load_mix(0,0,2); load_mix(0,2,6); load_rows(0,0); load_mix(0,6,10); load_rows(0,1); load_mix(0,10,12); load_kv("v",0,1)
-        load_kv("k",0); load_mix(1,0,2); load_kv("v",1); load_mix(1,2,6); load_kv("k",1); load_rows(1,0); load_kv("v",2); load_rows(1,1); load_mix(1,6,12); load_kv("k",2); load_kv("v",3); load_kv("k",3); load_kv("v",4); load_kv("k",4)
+        load_rows(0,0); load_mix(0,0,2); load_kv("v",0,0); load_rows(0,1); load_mix(0,2,6); load_kv("v",0,1); load_mix(0,6,12)
+        load_kv("k",0); load_kv("v",1); load_mix(1,0,4); load_rows(1,0); load_kv("k",1); load_rows(1,1); load_kv("v",2); load_mix(1,4,12); load_kv("k",2); load_kv("v",3); load_kv("k",3); load_kv("v",4); load_kv("k",4)
         todo=[(n+j,i) for n in (0,2,4,6) for i in range(4) for j in range(2)]
-        def fill(c):
+        def fill(c, first=V):
             for q in range(c):
                 if todo:
-                    n,i=todo.pop(0); nmix(n,i,V)
+                    n,i=todo.pop(0); nmix(n,i,first if i==0 else V)
         constants()
+        fill(2)
+        nmix(2,0,S); nmix(3,0,S); todo.remove((2,0)); todo.remove((3,0))
+        kron(0,0,S)
         turn("v",0,0,S)
-        for x in range(6): kron(0,x,S)
-        fill(8)
+        fill(6)
+        kron(0,1,S); kron(0,2,S)
         rows(0,S)
         turn("v",0,1,S)
-        fill(4)
-        turn("k",0,0,S); turn("k",0,1,S)
+        fill(2)
         deinterleave(0)
-        interleave(0)
-        back(0,0,S); back(0,1,S)
+        interleave(0,V,0,3)
+        kron(0,3,S); kron(0,4,S); kron(0,5,S)
         quant("v",0)
+        fill(2)
+        rows(1,S)
+        turn("k",0,0,S); turn("k",0,1,S)
+        interleave(0,V,3,6)
+        back(0,0,S); back(0,1,S)
+        fill(1)
         quant("b",0)
+        turn("v",1,0,S); turn("v",1,1,S)
         kron(1,0,S)
         quant("k",0)
+        fill(1)
 
         for n in range(PAIRS - 1):
             early = n<3
             E = S if early else V
             quant("a",n)
-            if n: turn("k",n,0,S); turn("k",n,1,V)
-            rows(n+1,S)
-            product(n,0,0,E); product(n,0,1,S)
-            store(n,0,0,2)
+            if n: turn("k",n,0,S); turn("k",n,1,E); rows(n+1,S)
+            product(n,0,0,V); product(n,0,1,S)
+            if n>=5: store(n,0,0,2)
             if n: quant("k",n)
             product(n,0,2,S)
             deinterleave(n+1)
             interleave(n+1)
-            turn("v",n+1,0,S)
-            turn("v",n+1,1,S)
+            if n: turn("v",n+1,0,S); turn("v",n+1,1,S)
             fill(2)
             if early and n: kron(1,2*n,S)
             product(n,0,3,S)
-            store(n,0,2,4)
-            product(n,1,0,V); product(n,1,1,S)
-            store(n,1,0,2)
+            store(n,0,2 if n>=5 else 0,4)
+            product(n,1,0,E); product(n,1,1,S)
+            if n>=5: store(n,1,0,2)
             quant("b",n+1)
             quant("v",n+1)
             fill(2)
             back(n+1,0,S); back(n+1,1,S)
             if early: kron(1,2*n+1,S)
-            fill(3)
-            product(n,1,2,S); product(n,1,3,E)
-            store(n,1,2,4)
+            product(n,1,2,S); product(n,1,3,V)
+            fill(2)
+            store(n,1,2 if n>=5 else 0,4)
             load_kv("v",n+5); load_kv("k",n+5)
 
         n = PAIRS - 1

@@ -93,8 +93,8 @@ def tile_mhla_pa_v_kernel(tc, k_feat, v, w_piece, grad_out, out_0, out_1):
         mixer = const.tile([P, P], BF16, name="mixer", align_bytes=64)
 
         def patterns():
-            nc.vector.memset(w_rows[:], 0.0)
-            nc.scalar.dma_start(out=w_rows[0:N, :], in_=w_piece)
+            nc.gpsimd.memset(w_rows[:], 0.0)
+            nc.sync.dma_start(out=w_rows[0:N, :], in_=w_piece)
             make_identity(nc, ident[:])
             nc.vector.memset(ones[:], 1.0)
             nc.scalar.copy(out=spread[:], in_=ident[:, 0:N].unsqueeze(1).to_broadcast([P, 32, N]))
@@ -282,10 +282,10 @@ def tile_mhla_pa_v_kernel(tc, k_feat, v, w_piece, grad_out, out_0, out_1):
             else:
                 copy(engine, res.rearrange("m (p t) -> m p t", t=4), bank[:].rearrange("m (t p) -> m p t", t=4))
 
-        def store(n, which, b0, b1):
+        def store(n, which, b0, b1, queue=nc.sync):
             h, j = divmod(n, N)
             view = (out_0 if which == 0 else out_1)[0, h, j].rearrange("(m b) d -> m b d", b=4)
-            nc.sync.dma_start(out=view[:, b0:b1, :], in_=results[which][:, b0:b1, :])
+            queue.dma_start(out=view[:, b0:b1, :], in_=results[which][:, b0:b1, :])
 
         patterns()
         load_rows(0,0); load_mix(0,0,2); load_kv("v",0,0); load_rows(0,1); load_mix(0,2,6); load_kv("v",0,1); load_mix(0,6,12)
@@ -326,19 +326,19 @@ def tile_mhla_pa_v_kernel(tc, k_feat, v, w_piece, grad_out, out_0, out_1):
             E = S if early else V
             quant("a",n)
             if n: turn("k",n,0,S); turn("k",n,1,E); rows(n+1,S)
-            product(n,0,0,V); product(n,0,1,S)
-            if n>=5: store(n,0,0,2)
+            product(n,0,0,E); product(n,0,1,S)
+            if n>=6: store(n,0,0,2)
             if n: quant("k",n)
-            product(n,0,2,S)
+            if n: turn("v",n+1,0,S)
             deinterleave(n+1)
             interleave(n+1)
-            if n: turn("v",n+1,0,S); turn("v",n+1,1,S)
-            fill(2)
             if early and n: kron(1,2*n,S)
-            product(n,0,3,S)
-            store(n,0,2 if n>=5 else 0,4)
-            product(n,1,0,E); product(n,1,1,S)
-            if n>=5: store(n,1,0,2)
+            product(n,0,2,S); product(n,0,3,S)
+            store(n,0,2 if n>=6 else 0,4)
+            if n: turn("v",n+1,1,S)
+            fill(2)
+            product(n,1,0,V); product(n,1,1,S)
+            if n>=6: store(n,1,0,2)
             quant("b",n+1)
             quant("v",n+1)
             fill(2)
@@ -346,17 +346,17 @@ def tile_mhla_pa_v_kernel(tc, k_feat, v, w_piece, grad_out, out_0, out_1):
             if early: kron(1,2*n+1,S)
             product(n,1,2,S); product(n,1,3,V)
             fill(2)
-            store(n,1,2 if n>=5 else 0,4)
+            store(n,1,2 if n>=6 else 0,4)
             load_kv("v",n+5); load_kv("k",n+5)
 
         n = PAIRS - 1
+        quant("a",n)
         turn("k",n,0,S)
-        product(n,0,0,S); product(n,0,1,V)
+        product(n,0,0,V); product(n,0,1,S)
         store(n,0,0,2)
         turn("k",n,1,S)
-        quant("a",n)
         quant("k",n,0)
-        product(n,0,2,S); product(n,0,3,V)
+        product(n,0,2,V); product(n,0,3,S)
         store(n,0,2,4)
         quant("k",n,1)
         product(n,1,0,S); product(n,1,1,V)

@@ -17,8 +17,9 @@ P = 128
 PAIRS = H * N
 FLOPS = 2 * 2 * PAIRS * W * D * D
 BANKS = 8
+HALF = 1
+ACC_BUFS = 4
 RAW_BUFS = 5
-RAW2_BUFS = 2
 RES_BUFS = 3
 CODE_BUFS = 2
 
@@ -62,18 +63,10 @@ def tile_mhla_pa_v_kernel(tc, k_feat, v, w_piece, grad_out, out_0, out_1):
             cols = slice(0, 2048) if part is None else slice(1024 * part, 1024 * part + 1024)
             nc.sync.dma_start(out=raw[which, n][:, cols], in_=src[:, cols])
 
-        def load_kv_two(which, n):
-            h, j = divmod(n, N)
-            tile = keep.tile([P, 2, 2048], BF16, name="raw2_" + which, bufs=RAW2_BUFS, align_bytes=64)
-            src = (k_feat if which == "k" else v)[0, h, j : j + 2].rearrange("j (m b) d -> m j (b d)", b=4)
-            nc.sync.dma_start(out=tile[:], in_=src)
-            raw[which, n] = tile[:, 0, :]
-            raw[which, n + 1] = tile[:, 1, :]
-
-        def load_rows(h, half):
-            g_row[h, half] = keep.tile([P, 2, 512], BF16, name="g_row%d%d" % (h, half), align_bytes=64)
-            src = grad_out[0, h].rearrange("i q d -> q i d")[384:512, 2 * half : 2 * half + 2, :]
-            nc.sync.dma_start(out=g_row[h, half][:], in_=src)
+        def load_rows(i0, i1):
+            for i in range(i0, i1):
+                g_row[i] = keep.tile([P, 1024], BF16, name="g_row%d" % i, align_bytes=64)
+                nc.sync.dma_start(out=g_row[i][:], in_=grad_out[0, 0, i, 256:512, :].rearrange("(r e) d -> r (e d)", e=2))
 
         def load_mix(h, x0, x1):
             tile = keep.tile([P, x1 - x0, 512], BF16, name="g_mix%d_%d" % (h, x0), align_bytes=64)
@@ -93,8 +86,8 @@ def tile_mhla_pa_v_kernel(tc, k_feat, v, w_piece, grad_out, out_0, out_1):
         mixer = const.tile([P, P], BF16, name="mixer", align_bytes=64)
 
         def patterns():
-            nc.gpsimd.memset(w_rows[:], 0.0)
-            nc.sync.dma_start(out=w_rows[0:N, :], in_=w_piece)
+            nc.vector.memset(w_rows[:], 0.0)
+            nc.scalar.dma_start(out=w_rows[0:N, :], in_=w_piece)
             make_identity(nc, ident[:])
             nc.vector.memset(ones[:], 1.0)
             nc.scalar.copy(out=spread[:], in_=ident[:, 0:N].unsqueeze(1).to_broadcast([P, 32, N]))
@@ -144,36 +137,37 @@ def tile_mhla_pa_v_kernel(tc, k_feat, v, w_piece, grad_out, out_0, out_1):
         def nmix(n, i, engine=V):
             h, j = divmod(n, N)
             w_ij = w_all[:, N * i + j : N * i + j + 1]
-            src = g_row[h, i // 2][:, i % 2, :]
+            src = g_row[i][:]
             if i == 0:
-                acc[n] = work.tile([P, 512], F32, name="acc", bufs=4)
+                acc[n] = work.tile([P, 1024], F32, name="acc", bufs=ACC_BUFS)
                 if engine is V:
                     nc.vector.tensor_scalar(out=acc[n][:], in0=src, scalar1=w_ij, scalar2=None, op0=MULT)
                 else:
                     nc.scalar.activation(out=acc[n][:], in_=src, func=mybir.ActivationFunctionType.Copy, scale=w_ij)
                 return
             if i == N - 1:
-                row[n] = work.tile([P, 512], BF16, name="row", bufs=4, align_bytes=64)
+                row[n] = work.tile([P, 1024], BF16, name="row", bufs=3, align_bytes=64)
             dst = row[n] if i == N - 1 else acc[n]
             nc.vector.scalar_tensor_tensor(out=dst[:], in0=src, scalar=w_ij, in1=acc[n][:], op0=MULT, op1=ADD)
 
         def rows(n, engine):
-            if n >= PAIRS:
+            if n >= N:
                 return
             words = row[n][:].bitcast(F32)
             bank = next_bank(F32)
-            for w in range(2):
-                nc.tensor.transpose(bank[:, 128 * w : 128 * w + 128], words[:, w:256:2], ident[:])
+            for e in range(2):
+                for w in range(2):
+                    c0 = 256 * e + 128 * w
+                    nc.tensor.transpose(bank[:, c0 : c0 + 128], words[:, 256 * e + w : 256 * e + 256 : 2], ident[:])
             dst = b_tile(n)[:].bitcast(F32).rearrange("p (u q e w) -> p u q e w", u=2, e=2, w=2)
-            copy(engine, dst[:, :, 96:128, :, :], bank[:, 0:256].rearrange("p (w q u e) -> p u q e w", w=2, u=2, e=2))
+            copy(engine, dst[:, :, 64:128, :, :], bank[:].rearrange("p (e w q u) -> p u q e w", e=2, w=2, u=2))
 
         def deinterleave(n):
-            if n >= PAIRS:
+            if n >= N:
                 return
-            h, j = divmod(n, N)
-            dst = mixed[h][:, :, j, :].rearrange("p t (u c i) -> p u c t i", u=2, i=8)
+            dst = mixed[0][:, :, n, :].rearrange("p t (u c i) -> p u c t i", u=2, i=8)
             src = b_tile(n)[:].rearrange("p (u c i t) -> p u c t i", u=2, i=8, t=4)
-            nc.vector.tensor_copy(out=dst[:, :, 24:32, :, :], in_=src[:, :, 24:32, :, :])
+            nc.vector.tensor_copy(out=dst[:, :, 16:32, :, :], in_=src[:, :, 16:32, :, :])
 
         def kron(h, x, engine):
             bank = next_bank(BF16)
@@ -191,13 +185,14 @@ def tile_mhla_pa_v_kernel(tc, k_feat, v, w_piece, grad_out, out_0, out_1):
                 bank[:].bitcast(F32).rearrange("p (g a y) -> p a g y", g=2, y=8),
             )
 
-        def interleave(n, engine=V, x0=0, x1=6):
+        def interleave(n):
             if n >= PAIRS:
                 return
             h, j = divmod(n, N)
             dst = b_tile(n)[:].rearrange("p (u c i t) -> p u c t i", u=2, i=4, t=4)
             src = mixed[h][:, :, j, :].rearrange("p t (u c i) -> p u c t i", u=2, i=4)
-            engine.tensor_copy(out=dst[:, :, 8 * x0 : 8 * x1, :, :], in_=src[:, :, 8 * x0 : 8 * x1, :, :])
+            c1 = 32 if h == 0 else 64
+            nc.vector.tensor_copy(out=dst[:, :, 0:c1, :, :], in_=src[:, :, 0:c1, :, :])
 
         def turn(which, n, half, engine):
             if n >= PAIRS:
@@ -288,64 +283,64 @@ def tile_mhla_pa_v_kernel(tc, k_feat, v, w_piece, grad_out, out_0, out_1):
             queue.dma_start(out=view[:, b0:b1, :], in_=results[which][:, b0:b1, :])
 
         patterns()
-        load_rows(0,0); load_mix(0,0,2); load_kv("v",0,0); load_rows(0,1); load_mix(0,2,6); load_kv("v",0,1); load_mix(0,6,12)
-        load_kv("k",0); load_kv("v",1); load_mix(1,0,4); load_rows(1,0); load_kv("k",1); load_rows(1,1); load_kv("v",2); load_mix(1,4,12); load_kv("k",2); load_kv("v",3); load_kv("k",3); load_kv("v",4); load_kv("k",4)
-        todo=[(n+j,i) for n in (0,2,4,6) for i in range(4) for j in range(2)]
-        def fill(c, first=V):
+        load_rows(0,1); load_mix(0,0,4); load_rows(1,2); load_kv("v",0); load_rows(2,3); load_rows(3,4); load_mix(0,4,8)
+        load_kv("k",0); load_mix(1,0,6); load_kv("v",1); load_kv("k",1); load_mix(1,6,16); load_kv("v",2); load_kv("k",2); load_kv("v",3); load_kv("k",3); load_kv("v",4); load_kv("k",4)
+        mixes=list(range(8))
+        def more(engine):
+            if mixes: kron(1,mixes.pop(0),engine)
+        todo=[(j,i) for j in (2,3) for i in (1,2,3)]
+        def fill(c):
             for q in range(c):
-                if todo:
-                    n,i=todo.pop(0); nmix(n,i,first if i==0 else V)
+                if todo: nmix(*todo.pop(0))
         constants()
-        fill(2)
-        nmix(2,0,S); nmix(3,0,S); todo.remove((2,0)); todo.remove((3,0))
-        kron(0,0,S)
-        turn("v",0,0,S)
-        fill(6)
-        kron(0,1,S); kron(0,2,S)
+        nmix(0,0,V)
+        for j in (1,2,3): nmix(j,0,S)
+        kron(0,0,S); kron(0,1,S)
+        for i in (1,2,3):
+            for j in (0,1): nmix(j,i)
+        turn("v",0,0,S); turn("v",0,1,S)
+        kron(0,2,S); kron(0,3,S)
         rows(0,S)
-        turn("v",0,1,S)
-        fill(2)
-        deinterleave(0)
-        interleave(0,V,0,3)
-        kron(0,3,S); kron(0,4,S); kron(0,5,S)
-        quant("v",0)
-        fill(2)
-        rows(1,S)
         turn("k",0,0,S); turn("k",0,1,S)
-        interleave(0,V,3,6)
+        rows(1,S)
+        quant("v",0)
+        fill(1)
+        deinterleave(0)
+        interleave(0)
+        more(S)
+        turn("v",1,0,S); turn("v",1,1,S)
         back(0,0,S); back(0,1,S)
         fill(1)
         quant("b",0)
-        turn("v",1,0,S); turn("v",1,1,S)
-        kron(1,0,S)
+        more(S)
         quant("k",0)
         fill(1)
-
         for n in range(PAIRS - 1):
-            early = n<3
-            E = S if early else V
+            E = S if n<1 else V
             quant("a",n)
-            if n: turn("k",n,0,S); turn("k",n,1,E); rows(n+1,S)
+            if n: turn("k",n,0,S); turn("k",n,1,E)
             product(n,0,0,E); product(n,0,1,S)
             if n>=6: store(n,0,0,2)
             if n: quant("k",n)
-            if n: turn("v",n+1,0,S)
+            product(n,0,2,S)
+            more(S)
+            if n==1: more(S)
             deinterleave(n+1)
             interleave(n+1)
-            if early and n: kron(1,2*n,S)
-            product(n,0,2,S); product(n,0,3,S)
+            if n: turn("v",n+1,0,S); turn("v",n+1,1,S)
+            fill(1)
+            product(n,0,3,S)
             store(n,0,2 if n>=6 else 0,4)
-            if n: turn("v",n+1,1,S)
-            fill(2)
-            product(n,1,0,V); product(n,1,1,S)
+            product(n,1,0,V if n else S); product(n,1,1,S)
             if n>=6: store(n,1,0,2)
+            more(S)
             quant("b",n+1)
+            fill(1)
             quant("v",n+1)
-            fill(2)
-            back(n+1,0,S); back(n+1,1,S)
-            if early: kron(1,2*n+1,S)
+            fill(0)
+            back(n+1,0,S); back(n+1,1,S); rows(n+2,S)
             product(n,1,2,S); product(n,1,3,V)
-            fill(2)
+            fill(1)
             store(n,1,2 if n>=6 else 0,4)
             load_kv("v",n+5); load_kv("k",n+5)
 
@@ -361,4 +356,4 @@ def tile_mhla_pa_v_kernel(tc, k_feat, v, w_piece, grad_out, out_0, out_1):
         quant("k",n,1)
         product(n,1,0,S); product(n,1,1,V)
         store(n,1,0,2)
-        product(n,1,2,S); store(n,1,2,3); product(n,1,3,V); store(n,1,3,4)
+        product(n,1,2,S); product(n,1,3,V); store(n,1,2,4)

@@ -17,11 +17,8 @@ P = 128
 PAIRS = H * N
 FLOPS = 2 * 2 * PAIRS * W * D * D
 BANKS = 8
-HALF = 1
-ACC_BUFS = 4
-RAW_BUFS = 5
-RES_BUFS = 3
-CODE_BUFS = 2
+AHEAD = 5
+RESULT_BUFS = 3
 
 
 def tile_mhla_pa_v_kernel(tc, k_feat, v, w_piece, grad_out, out_0, out_1):
@@ -48,30 +45,24 @@ def tile_mhla_pa_v_kernel(tc, k_feat, v, w_piece, grad_out, out_0, out_1):
             else:
                 nc.scalar.copy(out=dst, in_=src)
 
-        raw = {}
-        g_mix = {}
-        g_row = {}
+        tokens = {}
+        g_rows = {}
+        g_groups = {}
 
-        def load_kv(which, n, part=None):
-            if n >= PAIRS:
-                return
+        def load_tokens(which, n):
             h, j = divmod(n, N)
-            if (which, n) not in raw:
-                tile = keep.tile([P, 2048], BF16, name="raw_" + which, bufs=RAW_BUFS, align_bytes=64)
-                raw[which, n] = tile[:]
+            tokens[which, n] = keep.tile([P, 2048], BF16, name="raw_" + which, bufs=AHEAD, align_bytes=256)
             src = (k_feat if which == "k" else v)[0, h, j].rearrange("(m b) d -> m (b d)", b=4)
-            cols = slice(0, 2048) if part is None else slice(1024 * part, 1024 * part + 1024)
-            nc.sync.dma_start(out=raw[which, n][:, cols], in_=src[:, cols])
+            nc.sync.dma_start(out=tokens[which, n][:], in_=src)
 
-        def load_rows(i0, i1):
-            for i in range(i0, i1):
-                g_row[i] = keep.tile([P, 1024], BF16, name="g_row%d" % i, align_bytes=64)
-                nc.sync.dma_start(out=g_row[i][:], in_=grad_out[0, 0, i, 256:512, :].rearrange("(r e) d -> r (e d)", e=2))
+        def load_rows(i):
+            g_rows[i] = keep.tile([P, 1024], BF16, name="g_row%d" % i, align_bytes=256)
+            nc.sync.dma_start(out=g_rows[i][:], in_=grad_out[0, 0, i, 256:512, :].rearrange("(r e) d -> r (e d)", e=2))
 
-        def load_mix(h, x0, x1):
-            tile = keep.tile([P, x1 - x0, 512], BF16, name="g_mix%d_%d" % (h, x0), align_bytes=64)
+        def load_groups(h, x0, x1):
+            tile = keep.tile([P, x1 - x0, 512], BF16, name="g_mix%d_%d" % (h, x0), align_bytes=256)
             for x in range(x0, x1):
-                g_mix[h, x] = tile[:, x - x0, :]
+                g_groups[h, x] = tile[:, x - x0, :]
             for i in range(N):
                 src = grad_out[0, h, i].rearrange("(x r) d -> r x d", r=32)
                 nc.sync.dma_start(out=tile[i:P:4, :, :], in_=src[:, x0:x1, :])
@@ -86,8 +77,8 @@ def tile_mhla_pa_v_kernel(tc, k_feat, v, w_piece, grad_out, out_0, out_1):
         mixer = const.tile([P, P], BF16, name="mixer", align_bytes=64)
 
         def patterns():
-            nc.vector.memset(w_rows[:], 0.0)
-            nc.scalar.dma_start(out=w_rows[0:N, :], in_=w_piece)
+            nc.gpsimd.memset(w_rows[:], 0.0)
+            nc.sync.dma_start(out=w_rows[0:N, :], in_=w_piece)
             make_identity(nc, ident[:])
             nc.vector.memset(ones[:], 1.0)
             nc.scalar.copy(out=spread[:], in_=ident[:, 0:N].unsqueeze(1).to_broadcast([P, 32, N]))
@@ -98,7 +89,7 @@ def tile_mhla_pa_v_kernel(tc, k_feat, v, w_piece, grad_out, out_0, out_1):
                 op=ADD,
             )
 
-        def constants():
+        def weights():
             nc.vector.tensor_tensor(
                 out=w_diag[:],
                 in0=w_rows[:].unsqueeze(1).to_broadcast([P, N, N]),
@@ -120,12 +111,12 @@ def tile_mhla_pa_v_kernel(tc, k_feat, v, w_piece, grad_out, out_0, out_1):
             )
             nc.vector.tensor_copy(out=w_all[:], in_=bank[:, 0:16])
 
-        mixed = [keep.tile([P, 4, N, 512], BF16, name="mixed%d" % h, align_bytes=64) for h in range(H)]
-        acc = {}
-        row = {}
+        state = [keep.tile([P, 4, N, 512], BF16, name="mixed%d" % h, align_bytes=64) for h in range(H)]
+        sums = {}
+        mixed_rows = {}
         b_in = {}
         a_in = {}
-        grouped = {}
+        turned = {}
         codes = {}
         results = {}
 
@@ -134,120 +125,113 @@ def tile_mhla_pa_v_kernel(tc, k_feat, v, w_piece, grad_out, out_0, out_1):
                 b_in[n] = work.tile([P, 2048], BF16, name="b_in", align_bytes=64)
             return b_in[n]
 
-        def nmix(n, i, engine=V):
-            h, j = divmod(n, N)
+        def mix_term(j, i, engine=V):
             w_ij = w_all[:, N * i + j : N * i + j + 1]
-            src = g_row[i][:]
             if i == 0:
-                acc[n] = work.tile([P, 1024], F32, name="acc", bufs=ACC_BUFS)
+                sums[j] = work.tile([P, 1024], F32, name="acc", bufs=N)
                 if engine is V:
-                    nc.vector.tensor_scalar(out=acc[n][:], in0=src, scalar1=w_ij, scalar2=None, op0=MULT)
+                    nc.vector.tensor_scalar(out=sums[j][:], in0=g_rows[i][:], scalar1=w_ij, scalar2=None, op0=MULT)
                 else:
-                    nc.scalar.activation(out=acc[n][:], in_=src, func=mybir.ActivationFunctionType.Copy, scale=w_ij)
+                    nc.scalar.activation(
+                        out=sums[j][:], in_=g_rows[i][:], func=mybir.ActivationFunctionType.Copy, scale=w_ij
+                    )
                 return
             if i == N - 1:
-                row[n] = work.tile([P, 1024], BF16, name="row", bufs=3, align_bytes=64)
-            dst = row[n] if i == N - 1 else acc[n]
-            nc.vector.scalar_tensor_tensor(out=dst[:], in0=src, scalar=w_ij, in1=acc[n][:], op0=MULT, op1=ADD)
+                mixed_rows[j] = work.tile([P, 1024], BF16, name="row", bufs=N - 1, align_bytes=64)
+            dst = mixed_rows[j] if i == N - 1 else sums[j]
+            nc.vector.scalar_tensor_tensor(
+                out=dst[:], in0=g_rows[i][:], scalar=w_ij, in1=sums[j][:], op0=MULT, op1=ADD
+            )
 
-        def rows(n, engine):
-            if n >= N:
-                return
-            words = row[n][:].bitcast(F32)
+        def rows_to_b(j):
+            words = mixed_rows[j][:].bitcast(F32)
             bank = next_bank(F32)
             for e in range(2):
                 for w in range(2):
                     c0 = 256 * e + 128 * w
                     nc.tensor.transpose(bank[:, c0 : c0 + 128], words[:, 256 * e + w : 256 * e + 256 : 2], ident[:])
-            dst = b_tile(n)[:].bitcast(F32).rearrange("p (u q e w) -> p u q e w", u=2, e=2, w=2)
-            copy(engine, dst[:, :, 64:128, :, :], bank[:].rearrange("p (e w q u) -> p u q e w", e=2, w=2, u=2))
+            dst = b_tile(j)[:].bitcast(F32).rearrange("p (u q e w) -> p u q e w", u=2, e=2, w=2)
+            copy(S, dst[:, :, 64:128, :, :], bank[:].rearrange("p (e w q u) -> p u q e w", e=2, w=2, u=2))
 
-        def deinterleave(n):
-            if n >= N:
-                return
-            dst = mixed[0][:, :, n, :].rearrange("p t (u c i) -> p u c t i", u=2, i=8)
-            src = b_tile(n)[:].rearrange("p (u c i t) -> p u c t i", u=2, i=8, t=4)
+        def b_to_state(j):
+            dst = state[0][:, :, j, :].rearrange("p t (u c i) -> p u c t i", u=2, i=8)
+            src = b_tile(j)[:].rearrange("p (u c i t) -> p u c t i", u=2, i=8, t=4)
             nc.vector.tensor_copy(out=dst[:, :, 16:32, :, :], in_=src[:, :, 16:32, :, :])
 
-        def kron(h, x, engine):
+        def mix_groups(h, x):
             bank = next_bank(BF16)
             for g in range(2):
                 for t in range(4):
                     c0 = 512 * g + 128 * t
                     nc.tensor.matmul(
-                        bank[:, c0 : c0 + 128], lhsT=g_mix[h, 2 * x + g][:, t:512:4], rhs=mixer[:], start=True, stop=True
+                        bank[:, c0 : c0 + 128],
+                        lhsT=g_groups[h, 2 * x + g][:, t:512:4],
+                        rhs=mixer[:],
+                        start=True,
+                        stop=True,
                     )
-            words = mixed[h][:].rearrange("p t j c -> p (t j c)").bitcast(F32)
+            words = state[h][:].rearrange("p t j c -> p (t j c)").bitcast(F32)
             dst = words.rearrange("p (a q) -> p a q", q=128)[:, :, 16 * x : 16 * x + 16]
             copy(
-                engine,
+                S,
                 dst.rearrange("p a (g y) -> p a g y", g=2),
                 bank[:].bitcast(F32).rearrange("p (g a y) -> p a g y", g=2, y=8),
             )
 
-        def interleave(n):
-            if n >= PAIRS:
-                return
+        def state_to_b(n):
             h, j = divmod(n, N)
             dst = b_tile(n)[:].rearrange("p (u c i t) -> p u c t i", u=2, i=4, t=4)
-            src = mixed[h][:, :, j, :].rearrange("p t (u c i) -> p u c t i", u=2, i=4)
+            src = state[h][:, :, j, :].rearrange("p t (u c i) -> p u c t i", u=2, i=4)
             c1 = 32 if h == 0 else 64
             nc.vector.tensor_copy(out=dst[:, :, 0:c1, :, :], in_=src[:, :, 0:c1, :, :])
 
+        def state_to_a(n):
+            h, j = divmod(n, N)
+            a_in[n] = work.tile([P, 2048], BF16, name="a_in", align_bytes=64)
+            words = state[h][:].rearrange("p t j c -> p (t j c)").bitcast(F32)
+            for half in range(2):
+                bank = next_bank(F32)
+                for t in range(2):
+                    for u in range(2):
+                        c0 = 256 * t + 128 * u
+                        w0 = 256 * (N * (2 * half + t) + j) + 128 * u
+                        nc.tensor.transpose(bank[:, c0 : c0 + 128], words[:, w0 : w0 + 128], ident[:])
+                dst = a_in[n][:].bitcast(F32)[:, 512 * half : 512 * half + 512]
+                copy(
+                    S,
+                    dst.rearrange("q (t p u) -> q t p u", t=2, u=2),
+                    bank[:].rearrange("q (t u p) -> q t p u", t=2, u=2),
+                )
+
         def turn(which, n, half, engine):
-            if n >= PAIRS:
-                return
-            if (which, n) not in grouped:
-                grouped[which, n] = work.tile([P, 2048], BF16, name="grouped_" + which, align_bytes=64)
-            words = raw[which, n].bitcast(F32)
+            if half == 0:
+                turned[which, n] = work.tile([P, 2048], BF16, name="grouped_" + which, align_bytes=64)
+            words = tokens[which, n][:].bitcast(F32)
             bank = next_bank(F32)
             for b in range(2):
                 for u in range(2):
                     w0 = 256 * (2 * half + b)
                     c0 = 256 * b + 128 * u
                     nc.tensor.transpose(bank[:, c0 : c0 + 128], words[:, w0 + u : w0 + 256 : 2], ident[:])
-            dst = grouped[which, n][:].bitcast(F32)[:, 512 * half : 512 * half + 512]
+            dst = turned[which, n][:].bitcast(F32)[:, 512 * half : 512 * half + 512]
             copy(
                 engine,
                 dst.rearrange("p (b m u) -> p b m u", b=2, u=2),
                 bank[:].rearrange("p (b u m) -> p b m u", b=2, u=2),
             )
 
-        def back(n, half, engine):
-            if n >= PAIRS:
-                return
-            h, j = divmod(n, N)
-            if n not in a_in:
-                a_in[n] = work.tile([P, 2048], BF16, name="a_in", align_bytes=64)
-            words = mixed[h][:].rearrange("p t j c -> p (t j c)").bitcast(F32)
-            bank = next_bank(F32)
-            for tt in range(2):
-                for u in range(2):
-                    c0 = 256 * tt + 128 * u
-                    w0 = 256 * (N * (2 * half + tt) + j) + 128 * u
-                    nc.tensor.transpose(bank[:, c0 : c0 + 128], words[:, w0 : w0 + 128], ident[:])
-            dst = a_in[n][:].bitcast(F32)[:, 512 * half : 512 * half + 512]
-            copy(
-                engine,
-                dst.rearrange("q (t p u) -> q t p u", t=2, u=2),
-                bank[:].rearrange("q (t u p) -> q t p u", t=2, u=2),
-            )
-
-        def quant(which, n, half=None):
-            if n >= PAIRS:
-                return
+        def quantise(which, n, c0=0, c1=512):
             if which == "b":
                 src, fmt = b_in[n], E5M2
             elif which == "a":
                 src, fmt = a_in[n], E5M2
             else:
-                src, fmt = grouped[which, n], E4M3
-            if (which, n) not in codes:
-                c = work.tile([P, 512], U32, name="codes_" + which, bufs=CODE_BUFS, align_bytes=64)
-                sc = work.tile([P, 512], U8, name="scales_" + which, bufs=CODE_BUFS, align_bytes=64)
+                src, fmt = turned[which, n], E4M3
+            if c0 == 0:
+                c = work.tile([P, 512], U32, name="codes_" + which, align_bytes=64)
+                sc = work.tile([P, 512], U8, name="scales_" + which, align_bytes=64)
                 codes[which, n] = (c, sc)
             c, sc = codes[which, n]
-            c0, c1 = (0, 512) if half is None else (256 * half, 256 * half + 256)
             nc.vector.quantize_mx(out=c[:, c0:c1].bitcast(fmt), scales=sc[:, c0:c1], in_=src[:, 4 * c0 : 4 * c1])
 
         def product(n, which, b, engine):
@@ -255,7 +239,7 @@ def tile_mhla_pa_v_kernel(tc, k_feat, v, w_piece, grad_out, out_0, out_1):
             lc, ls = codes[left, n]
             rc, rs = codes[right, n]
             if b == 0:
-                results[which] = work.tile([P, 4, 512], F32, name="res%d" % which, bufs=RES_BUFS)
+                results[which] = work.tile([P, 4, 512], F32, name="res%d" % which, bufs=RESULT_BUFS, align_bytes=256)
             bank = next_bank(F32)
             cols = slice(128 * b, 128 * b + 128)
             nc.tensor.matmul_mx(
@@ -277,83 +261,125 @@ def tile_mhla_pa_v_kernel(tc, k_feat, v, w_piece, grad_out, out_0, out_1):
             else:
                 copy(engine, res.rearrange("m (p t) -> m p t", t=4), bank[:].rearrange("m (t p) -> m p t", t=4))
 
-        def store(n, which, b0, b1, queue=nc.sync):
+        def store(n, which, b0, b1):
             h, j = divmod(n, N)
             view = (out_0 if which == 0 else out_1)[0, h, j].rearrange("(m b) d -> m b d", b=4)
-            queue.dma_start(out=view[:, b0:b1, :], in_=results[which][:, b0:b1, :])
+            nc.sync.dma_start(out=view[:, b0:b1, :], in_=results[which][:, b0:b1, :])
+
+        banks_left = list(range(8))
+        terms_left = [(j, i) for j in (2, 3) for i in (1, 2, 3)]
+
+        def next_groups():
+            if banks_left:
+                mix_groups(1, banks_left.pop(0))
+
+        def next_term():
+            if terms_left:
+                mix_term(*terms_left.pop(0))
 
         patterns()
-        load_rows(0,1); load_mix(0,0,4); load_rows(1,2); load_kv("v",0); load_rows(2,3); load_rows(3,4); load_mix(0,4,8)
-        load_kv("k",0); load_mix(1,0,6); load_kv("v",1); load_kv("k",1); load_mix(1,6,16); load_kv("v",2); load_kv("k",2); load_kv("v",3); load_kv("k",3); load_kv("v",4); load_kv("k",4)
-        mixes=list(range(8))
-        def more(engine):
-            if mixes: kron(1,mixes.pop(0),engine)
-        todo=[(j,i) for j in (2,3) for i in (1,2,3)]
-        def fill(c):
-            for q in range(c):
-                if todo: nmix(*todo.pop(0))
-        constants()
-        nmix(0,0,V)
-        for j in (1,2,3): nmix(j,0,S)
-        kron(0,0,S); kron(0,1,S)
-        for i in (1,2,3):
-            for j in (0,1): nmix(j,i)
-        turn("v",0,0,S); turn("v",0,1,S)
-        kron(0,2,S); kron(0,3,S)
-        rows(0,S)
-        turn("k",0,0,S); turn("k",0,1,S)
-        rows(1,S)
-        quant("v",0)
-        fill(1)
-        deinterleave(0)
-        interleave(0)
-        more(S)
-        turn("v",1,0,S); turn("v",1,1,S)
-        back(0,0,S); back(0,1,S)
-        fill(1)
-        quant("b",0)
-        more(S)
-        quant("k",0)
-        fill(1)
+        load_rows(0)
+        load_groups(0, 0, 4)
+        load_rows(1)
+        load_tokens("v", 0)
+        load_rows(2)
+        load_groups(0, 4, 8)
+        load_rows(3)
+        load_tokens("k", 0)
+        load_groups(1, 0, 6)
+        load_tokens("v", 1)
+        load_tokens("k", 1)
+        load_groups(1, 6, 16)
+        for n in range(2, AHEAD):
+            load_tokens("v", n)
+            load_tokens("k", n)
+
+        weights()
+        for j in range(N):
+            mix_term(j, 0, V if j < 2 else S)
+        mix_groups(0, 0)
+        mix_groups(0, 1)
+        for i in range(1, N):
+            for j in range(2):
+                mix_term(j, i)
+        turn("v", 0, 0, S)
+        turn("v", 0, 1, S)
+        mix_groups(0, 2)
+        mix_groups(0, 3)
+        rows_to_b(0)
+        turn("k", 0, 0, S)
+        turn("k", 0, 1, S)
+        rows_to_b(1)
+        quantise("v", 0)
+        next_term()
+        b_to_state(0)
+        state_to_b(0)
+        next_groups()
+        turn("v", 1, 0, S)
+        turn("v", 1, 1, S)
+        state_to_a(0)
+        next_term()
+        quantise("b", 0)
+        next_groups()
+        quantise("k", 0)
+        next_term()
+
         for n in range(PAIRS - 1):
-            E = S if n<1 else V
-            quant("a",n)
-            if n: turn("k",n,0,S); turn("k",n,1,E)
-            product(n,0,0,E); product(n,0,1,S)
-            if n>=6: store(n,0,0,2)
-            if n: quant("k",n)
-            product(n,0,2,S)
-            more(S)
-            if n==1: more(S)
-            deinterleave(n+1)
-            interleave(n+1)
-            if n: turn("v",n+1,0,S); turn("v",n+1,1,S)
-            fill(1)
-            product(n,0,3,S)
-            store(n,0,2 if n>=6 else 0,4)
-            product(n,1,0,V if n else S); product(n,1,1,S)
-            if n>=6: store(n,1,0,2)
-            more(S)
-            quant("b",n+1)
-            fill(1)
-            quant("v",n+1)
-            fill(0)
-            back(n+1,0,S); back(n+1,1,S); rows(n+2,S)
-            product(n,1,2,S); product(n,1,3,V)
-            fill(1)
-            store(n,1,2 if n>=6 else 0,4)
-            load_kv("v",n+5); load_kv("k",n+5)
+            helper = V if n > 0 else S
+            halves = n == PAIRS - 2
+            quantise("a", n)
+            if n > 0:
+                turn("k", n, 0, S)
+                turn("k", n, 1, V)
+            product(n, 0, 0, helper)
+            product(n, 0, 1, S)
+            if halves:
+                store(n, 0, 0, 2)
+            if n > 0:
+                quantise("k", n)
+            product(n, 0, 2, S)
+            next_groups()
+            if n == 1:
+                next_groups()
+            if n + 1 < N:
+                b_to_state(n + 1)
+            state_to_b(n + 1)
+            if n > 0:
+                turn("v", n + 1, 0, S)
+                turn("v", n + 1, 1, S)
+            next_term()
+            product(n, 0, 3, S)
+            store(n, 0, 2 if halves else 0, 4)
+            product(n, 1, 0, helper)
+            product(n, 1, 1, S)
+            if halves:
+                store(n, 1, 0, 2)
+            next_groups()
+            quantise("b", n + 1)
+            next_term()
+            quantise("v", n + 1)
+            state_to_a(n + 1)
+            if n + 2 < N:
+                rows_to_b(n + 2)
+            product(n, 1, 2, S)
+            product(n, 1, 3, V)
+            next_term()
+            store(n, 1, 2 if halves else 0, 4)
+            if n + AHEAD < PAIRS:
+                load_tokens("v", n + AHEAD)
+                load_tokens("k", n + AHEAD)
 
         n = PAIRS - 1
-        quant("a",n)
-        turn("k",n,0,S)
-        product(n,0,0,V); product(n,0,1,S)
-        store(n,0,0,2)
-        turn("k",n,1,S)
-        quant("k",n,0)
-        product(n,0,2,V); product(n,0,3,S)
-        store(n,0,2,4)
-        quant("k",n,1)
-        product(n,1,0,S); product(n,1,1,V)
-        store(n,1,0,2)
-        product(n,1,2,S); product(n,1,3,V); store(n,1,2,4)
+        quantise("a", n)
+        for half in range(2):
+            turn("k", n, half, S)
+            if half == 1:
+                quantise("k", n, 0, 256)
+            product(n, 0, 2 * half, V)
+            product(n, 0, 2 * half + 1, S)
+            store(n, 0, 2 * half, 2 * half + 2)
+        quantise("k", n, 256, 512)
+        for half in range(2):
+            product(n, 1, 2 * half, S)
+            product(n, 1, 2 * half + 1, V)
+            store(n, 1, 2 * half, 2 * half + 2)

@@ -17,7 +17,8 @@ P = 128
 PAIRS = H * N
 FLOPS = 2 * 2 * PAIRS * W * D * D
 BANKS = 8
-AHEAD = 5
+TOKEN_BUFS = 5
+CODE_BUFS = 2
 RESULT_BUFS = 3
 
 
@@ -51,7 +52,7 @@ def tile_mhla_pa_v_kernel(tc, k_feat, v, w_piece, grad_out, out_0, out_1):
 
         def load_tokens(which, n):
             h, j = divmod(n, N)
-            tokens[which, n] = keep.tile([P, 2048], BF16, name="raw_" + which, bufs=AHEAD, align_bytes=256)
+            tokens[which, n] = keep.tile([P, 2048], BF16, name="raw_" + which, bufs=TOKEN_BUFS, align_bytes=256)
             src = (k_feat if which == "k" else v)[0, h, j].rearrange("(m b) d -> m (b d)", b=4)
             nc.sync.dma_start(out=tokens[which, n][:], in_=src)
 
@@ -69,10 +70,8 @@ def tile_mhla_pa_v_kernel(tc, k_feat, v, w_piece, grad_out, out_0, out_1):
 
         w_rows = const.tile([P, N], BF16, name="w_rows")
         ident = const.tile([P, P], F32, name="ident")
-        ones = const.tile([P, P], BF16, name="ones", align_bytes=64)
         eye = const.tile([P, 32], F32, name="eye")
         spread = const.tile([P, 32, N], BF16, name="spread", align_bytes=64)
-        w_diag = const.tile([P, N, N], BF16, name="w_diag")
         w_all = const.tile([P, N * N], F32, name="w_all")
         mixer = const.tile([P, P], BF16, name="mixer", align_bytes=64)
 
@@ -80,7 +79,6 @@ def tile_mhla_pa_v_kernel(tc, k_feat, v, w_piece, grad_out, out_0, out_1):
             nc.gpsimd.memset(w_rows[:], 0.0)
             nc.sync.dma_start(out=w_rows[0:N, :], in_=w_piece)
             make_identity(nc, ident[:])
-            nc.vector.memset(ones[:], 1.0)
             nc.scalar.copy(out=spread[:], in_=ident[:, 0:N].unsqueeze(1).to_broadcast([P, 32, N]))
             nc.vector.tensor_reduce(
                 out=eye[:].rearrange("p (u q e) -> p q u e", u=2, e=2),
@@ -89,27 +87,29 @@ def tile_mhla_pa_v_kernel(tc, k_feat, v, w_piece, grad_out, out_0, out_1):
                 op=ADD,
             )
 
+        w_bank = next_bank(F32)
+
         def weights():
-            nc.vector.tensor_tensor(
-                out=w_diag[:],
-                in0=w_rows[:].unsqueeze(1).to_broadcast([P, N, N]),
-                in1=ident[:, 0:N].unsqueeze(2).to_broadcast([P, N, N]),
-                op=MULT,
-            )
-            bank = next_bank(F32)
+            for j in range(N):
+                nc.tensor.matmul(
+                    w_bank[:, N * j : N * j + N],
+                    lhsT=w_rows[:, j : j + 1].to_broadcast([P, P]),
+                    rhs=spread[:, 0, :],
+                    start=True,
+                    stop=True,
+                )
             nc.tensor.matmul(
-                bank[:, 16:20], lhsT=spread[:].rearrange("p r i -> p (r i)"), rhs=w_rows[:], start=True, stop=True
+                w_bank[:, 16:20], lhsT=spread[:].rearrange("p r i -> p (r i)"), rhs=w_rows[:], start=True, stop=True
             )
-            nc.tensor.matmul(
-                bank[:, 0:16], lhsT=ones[:], rhs=w_diag[:].rearrange("p i j -> p (i j)"), start=True, stop=True
-            )
+            nc.vector.tensor_copy(out=w_all[:], in_=w_bank[:, 0:16])
+
+        def build_mixer():
             nc.vector.tensor_tensor(
                 out=mixer[:].rearrange("p (j r) -> p j r", j=N),
                 in0=eye[:].unsqueeze(1).to_broadcast([P, N, 32]),
-                in1=bank[:, 16:20].unsqueeze(2).to_broadcast([P, N, 32]),
+                in1=w_bank[:, 16:20].unsqueeze(2).to_broadcast([P, N, 32]),
                 op=MULT,
             )
-            nc.vector.tensor_copy(out=w_all[:], in_=bank[:, 0:16])
 
         state = [keep.tile([P, 4, N, 512], BF16, name="mixed%d" % h, align_bytes=64) for h in range(H)]
         sums = {}
@@ -126,7 +126,7 @@ def tile_mhla_pa_v_kernel(tc, k_feat, v, w_piece, grad_out, out_0, out_1):
             return b_in[n]
 
         def mix_term(j, i, engine=V):
-            w_ij = w_all[:, N * i + j : N * i + j + 1]
+            w_ij = w_all[:, N * j + i : N * j + i + 1]
             if i == 0:
                 sums[j] = work.tile([P, 1024], F32, name="acc", bufs=N)
                 if engine is V:
@@ -143,7 +143,7 @@ def tile_mhla_pa_v_kernel(tc, k_feat, v, w_piece, grad_out, out_0, out_1):
                 out=dst[:], in0=g_rows[i][:], scalar=w_ij, in1=sums[j][:], op0=MULT, op1=ADD
             )
 
-        def rows_to_b(j):
+        def rows_to_b(j, engine):
             words = mixed_rows[j][:].bitcast(F32)
             bank = next_bank(F32)
             for e in range(2):
@@ -151,14 +151,14 @@ def tile_mhla_pa_v_kernel(tc, k_feat, v, w_piece, grad_out, out_0, out_1):
                     c0 = 256 * e + 128 * w
                     nc.tensor.transpose(bank[:, c0 : c0 + 128], words[:, 256 * e + w : 256 * e + 256 : 2], ident[:])
             dst = b_tile(j)[:].bitcast(F32).rearrange("p (u q e w) -> p u q e w", u=2, e=2, w=2)
-            copy(S, dst[:, :, 64:128, :, :], bank[:].rearrange("p (e w q u) -> p u q e w", e=2, w=2, u=2))
+            copy(engine, dst[:, :, 64:128, :, :], bank[:].rearrange("p (e w q u) -> p u q e w", e=2, w=2, u=2))
 
         def b_to_state(j):
             dst = state[0][:, :, j, :].rearrange("p t (u c i) -> p u c t i", u=2, i=8)
             src = b_tile(j)[:].rearrange("p (u c i t) -> p u c t i", u=2, i=8, t=4)
             nc.vector.tensor_copy(out=dst[:, :, 16:32, :, :], in_=src[:, :, 16:32, :, :])
 
-        def mix_groups(h, x):
+        def mix_groups(h, x, engine):
             bank = next_bank(BF16)
             for g in range(2):
                 for t in range(4):
@@ -173,35 +173,34 @@ def tile_mhla_pa_v_kernel(tc, k_feat, v, w_piece, grad_out, out_0, out_1):
             words = state[h][:].rearrange("p t j c -> p (t j c)").bitcast(F32)
             dst = words.rearrange("p (a q) -> p a q", q=128)[:, :, 16 * x : 16 * x + 16]
             copy(
-                S,
+                engine,
                 dst.rearrange("p a (g y) -> p a g y", g=2),
                 bank[:].bitcast(F32).rearrange("p (g a y) -> p a g y", g=2, y=8),
             )
 
-        def state_to_b(n):
+        def state_to_b(n, c0, c1):
             h, j = divmod(n, N)
             dst = b_tile(n)[:].rearrange("p (u c i t) -> p u c t i", u=2, i=4, t=4)
             src = state[h][:, :, j, :].rearrange("p t (u c i) -> p u c t i", u=2, i=4)
-            c1 = 32 if h == 0 else 64
-            nc.vector.tensor_copy(out=dst[:, :, 0:c1, :, :], in_=src[:, :, 0:c1, :, :])
+            nc.vector.tensor_copy(out=dst[:, :, c0:c1, :, :], in_=src[:, :, c0:c1, :, :])
 
-        def state_to_a(n):
+        def state_to_a(n, half, engine):
             h, j = divmod(n, N)
-            a_in[n] = work.tile([P, 2048], BF16, name="a_in", align_bytes=64)
+            if half == 0:
+                a_in[n] = work.tile([P, 2048], BF16, name="a_in", align_bytes=64)
             words = state[h][:].rearrange("p t j c -> p (t j c)").bitcast(F32)
-            for half in range(2):
-                bank = next_bank(F32)
-                for t in range(2):
-                    for u in range(2):
-                        c0 = 256 * t + 128 * u
-                        w0 = 256 * (N * (2 * half + t) + j) + 128 * u
-                        nc.tensor.transpose(bank[:, c0 : c0 + 128], words[:, w0 : w0 + 128], ident[:])
-                dst = a_in[n][:].bitcast(F32)[:, 512 * half : 512 * half + 512]
-                copy(
-                    S,
-                    dst.rearrange("q (t p u) -> q t p u", t=2, u=2),
-                    bank[:].rearrange("q (t u p) -> q t p u", t=2, u=2),
-                )
+            bank = next_bank(F32)
+            for t in range(2):
+                for u in range(2):
+                    c0 = 256 * t + 128 * u
+                    w0 = 256 * (N * (2 * half + t) + j) + 128 * u
+                    nc.tensor.transpose(bank[:, c0 : c0 + 128], words[:, w0 : w0 + 128], ident[:])
+            dst = a_in[n][:].bitcast(F32)[:, 512 * half : 512 * half + 512]
+            copy(
+                engine,
+                dst.rearrange("q (t p u) -> q t p u", t=2, u=2),
+                bank[:].rearrange("q (t u p) -> q t p u", t=2, u=2),
+            )
 
         def turn(which, n, half, engine):
             if half == 0:
@@ -228,8 +227,8 @@ def tile_mhla_pa_v_kernel(tc, k_feat, v, w_piece, grad_out, out_0, out_1):
             else:
                 src, fmt = turned[which, n], E4M3
             if c0 == 0:
-                c = work.tile([P, 512], U32, name="codes_" + which, align_bytes=64)
-                sc = work.tile([P, 512], U8, name="scales_" + which, align_bytes=64)
+                c = work.tile([P, 512], U32, name="codes_" + which, bufs=CODE_BUFS, align_bytes=64)
+                sc = work.tile([P, 512], U8, name="scales_" + which, bufs=CODE_BUFS, align_bytes=64)
                 codes[which, n] = (c, sc)
             c, sc = codes[which, n]
             nc.vector.quantize_mx(out=c[:, c0:c1].bitcast(fmt), scales=sc[:, c0:c1], in_=src[:, 4 * c0 : 4 * c1])
@@ -266,23 +265,12 @@ def tile_mhla_pa_v_kernel(tc, k_feat, v, w_piece, grad_out, out_0, out_1):
             view = (out_0 if which == 0 else out_1)[0, h, j].rearrange("(m b) d -> m b d", b=4)
             nc.sync.dma_start(out=view[:, b0:b1, :], in_=results[which][:, b0:b1, :])
 
-        banks_left = list(range(8))
-        terms_left = [(j, i) for j in (2, 3) for i in (1, 2, 3)]
-
-        def next_groups():
-            if banks_left:
-                mix_groups(1, banks_left.pop(0))
-
-        def next_term():
-            if terms_left:
-                mix_term(*terms_left.pop(0))
-
         patterns()
         load_rows(0)
-        load_groups(0, 0, 4)
         load_rows(1)
-        load_tokens("v", 0)
+        load_groups(0, 0, 4)
         load_rows(2)
+        load_tokens("v", 0)
         load_groups(0, 4, 8)
         load_rows(3)
         load_tokens("k", 0)
@@ -290,96 +278,226 @@ def tile_mhla_pa_v_kernel(tc, k_feat, v, w_piece, grad_out, out_0, out_1):
         load_tokens("v", 1)
         load_tokens("k", 1)
         load_groups(1, 6, 16)
-        for n in range(2, AHEAD):
-            load_tokens("v", n)
-            load_tokens("k", n)
-
+        load_tokens("v", 2)
+        load_tokens("k", 2)
+        load_tokens("v", 3)
+        load_tokens("k", 3)
+        load_tokens("v", 4)
+        load_tokens("k", 4)
         weights()
-        for j in range(N):
-            mix_term(j, 0, V if j < 2 else S)
-        mix_groups(0, 0)
-        mix_groups(0, 1)
-        for i in range(1, N):
-            for j in range(2):
-                mix_term(j, i)
+        build_mixer()
+        mix_term(0, 0, V)
+        mix_term(1, 0, S)
+        mix_term(2, 0, S)
+        mix_term(3, 0, S)
+        mix_groups(0, 0, S)
+        mix_groups(0, 1, S)
+        mix_term(0, 1)
+        mix_term(1, 1)
+        mix_term(0, 2)
+        mix_term(1, 2)
+        mix_term(0, 3)
+        mix_term(1, 3)
         turn("v", 0, 0, S)
         turn("v", 0, 1, S)
-        mix_groups(0, 2)
-        mix_groups(0, 3)
-        rows_to_b(0)
+        mix_groups(0, 2, S)
+        mix_groups(0, 3, S)
+        rows_to_b(0, S)
         turn("k", 0, 0, S)
         turn("k", 0, 1, S)
-        rows_to_b(1)
+        rows_to_b(1, S)
         quantise("v", 0)
-        next_term()
+        mix_term(2, 1)
         b_to_state(0)
-        state_to_b(0)
-        next_groups()
+        state_to_b(0, 0, 32)
+        mix_groups(1, 0, S)
         turn("v", 1, 0, S)
         turn("v", 1, 1, S)
-        state_to_a(0)
-        next_term()
+        state_to_a(0, 0, S)
+        state_to_a(0, 1, S)
+        mix_term(2, 2)
         quantise("b", 0)
-        next_groups()
+        mix_groups(1, 1, S)
         quantise("k", 0)
-        next_term()
-
-        for n in range(PAIRS - 1):
-            helper = V if n > 0 else S
-            halves = n == PAIRS - 2
-            quantise("a", n)
-            if n > 0:
-                turn("k", n, 0, S)
-                turn("k", n, 1, V)
-            product(n, 0, 0, helper)
-            product(n, 0, 1, S)
-            if halves:
-                store(n, 0, 0, 2)
-            if n > 0:
-                quantise("k", n)
-            product(n, 0, 2, S)
-            next_groups()
-            if n == 1:
-                next_groups()
-            if n + 1 < N:
-                b_to_state(n + 1)
-            state_to_b(n + 1)
-            if n > 0:
-                turn("v", n + 1, 0, S)
-                turn("v", n + 1, 1, S)
-            next_term()
-            product(n, 0, 3, S)
-            store(n, 0, 2 if halves else 0, 4)
-            product(n, 1, 0, helper)
-            product(n, 1, 1, S)
-            if halves:
-                store(n, 1, 0, 2)
-            next_groups()
-            quantise("b", n + 1)
-            next_term()
-            quantise("v", n + 1)
-            state_to_a(n + 1)
-            if n + 2 < N:
-                rows_to_b(n + 2)
-            product(n, 1, 2, S)
-            product(n, 1, 3, V)
-            next_term()
-            store(n, 1, 2 if halves else 0, 4)
-            if n + AHEAD < PAIRS:
-                load_tokens("v", n + AHEAD)
-                load_tokens("k", n + AHEAD)
-
-        n = PAIRS - 1
-        quantise("a", n)
-        for half in range(2):
-            turn("k", n, half, S)
-            if half == 1:
-                quantise("k", n, 0, 256)
-            product(n, 0, 2 * half, V)
-            product(n, 0, 2 * half + 1, S)
-            store(n, 0, 2 * half, 2 * half + 2)
-        quantise("k", n, 256, 512)
-        for half in range(2):
-            product(n, 1, 2 * half, S)
-            product(n, 1, 2 * half + 1, V)
-            store(n, 1, 2 * half, 2 * half + 2)
+        mix_term(2, 3)
+        quantise("a", 0)
+        product(0, 0, 0, S)
+        product(0, 0, 1, S)
+        product(0, 0, 2, S)
+        mix_groups(1, 2, S)
+        b_to_state(1)
+        state_to_b(1, 0, 32)
+        mix_term(3, 1)
+        product(0, 0, 3, S)
+        load_tokens("v", 5)
+        load_tokens("k", 5)
+        store(0, 0, 0, 4)
+        product(0, 1, 0, S)
+        product(0, 1, 1, S)
+        mix_groups(1, 3, S)
+        quantise("b", 1)
+        mix_term(3, 2)
+        quantise("v", 1)
+        state_to_a(1, 0, S)
+        state_to_a(1, 1, S)
+        rows_to_b(2, S)
+        product(0, 1, 2, S)
+        product(0, 1, 3, V)
+        mix_term(3, 3)
+        store(0, 1, 0, 4)
+        quantise("a", 1)
+        turn("k", 1, 0, S)
+        turn("k", 1, 1, V)
+        product(1, 0, 0, V)
+        product(1, 0, 1, S)
+        quantise("k", 1)
+        product(1, 0, 2, S)
+        mix_groups(1, 4, S)
+        mix_groups(1, 5, S)
+        b_to_state(2)
+        state_to_b(2, 0, 32)
+        turn("v", 2, 0, S)
+        turn("v", 2, 1, S)
+        load_tokens("v", 6)
+        product(1, 0, 3, S)
+        store(1, 0, 0, 4)
+        product(1, 1, 0, V)
+        product(1, 1, 1, S)
+        mix_groups(1, 6, V)
+        quantise("b", 2)
+        quantise("v", 2)
+        state_to_a(2, 0, S)
+        state_to_a(2, 1, S)
+        rows_to_b(3, S)
+        product(1, 1, 2, S)
+        product(1, 1, 3, V)
+        load_tokens("k", 6)
+        store(1, 1, 0, 4)
+        quantise("a", 2)
+        turn("k", 2, 0, S)
+        turn("k", 2, 1, V)
+        product(2, 0, 0, V)
+        product(2, 0, 1, S)
+        quantise("k", 2)
+        product(2, 0, 2, S)
+        mix_groups(1, 7, V)
+        b_to_state(3)
+        state_to_b(3, 0, 32)
+        turn("v", 3, 0, S)
+        turn("v", 3, 1, S)
+        load_tokens("v", 7)
+        product(2, 0, 3, S)
+        store(2, 0, 0, 4)
+        product(2, 1, 0, V)
+        product(2, 1, 1, S)
+        quantise("b", 3)
+        quantise("v", 3)
+        state_to_a(3, 0, S)
+        state_to_a(3, 1, S)
+        product(2, 1, 2, S)
+        product(2, 1, 3, V)
+        load_tokens("k", 7)
+        store(2, 1, 0, 4)
+        quantise("a", 3)
+        turn("k", 3, 0, S)
+        turn("k", 3, 1, V)
+        product(3, 0, 0, V)
+        product(3, 0, 1, S)
+        quantise("k", 3)
+        product(3, 0, 2, S)
+        state_to_b(4, 0, 64)
+        turn("v", 4, 0, S)
+        turn("v", 4, 1, S)
+        product(3, 0, 3, S)
+        store(3, 0, 0, 4)
+        product(3, 1, 0, V)
+        product(3, 1, 1, S)
+        quantise("b", 4)
+        quantise("v", 4)
+        state_to_a(4, 0, S)
+        state_to_a(4, 1, S)
+        product(3, 1, 2, S)
+        product(3, 1, 3, V)
+        store(3, 1, 0, 4)
+        quantise("a", 4)
+        turn("k", 4, 0, S)
+        turn("k", 4, 1, V)
+        product(4, 0, 0, V)
+        product(4, 0, 1, S)
+        quantise("k", 4)
+        product(4, 0, 2, S)
+        state_to_b(5, 0, 64)
+        turn("v", 5, 0, S)
+        turn("v", 5, 1, S)
+        product(4, 0, 3, S)
+        store(4, 0, 0, 4)
+        product(4, 1, 0, V)
+        product(4, 1, 1, S)
+        quantise("b", 5)
+        quantise("v", 5)
+        state_to_a(5, 0, S)
+        state_to_a(5, 1, S)
+        product(4, 1, 2, S)
+        product(4, 1, 3, V)
+        store(4, 1, 0, 4)
+        quantise("a", 5)
+        turn("k", 5, 0, S)
+        turn("k", 5, 1, V)
+        product(5, 0, 0, V)
+        product(5, 0, 1, S)
+        quantise("k", 5)
+        product(5, 0, 2, S)
+        state_to_b(6, 0, 64)
+        turn("v", 6, 0, S)
+        turn("v", 6, 1, S)
+        product(5, 0, 3, S)
+        store(5, 0, 0, 4)
+        product(5, 1, 0, V)
+        product(5, 1, 1, S)
+        quantise("b", 6)
+        quantise("v", 6)
+        state_to_a(6, 0, S)
+        state_to_a(6, 1, S)
+        product(5, 1, 2, S)
+        product(5, 1, 3, V)
+        store(5, 1, 0, 4)
+        quantise("a", 6)
+        turn("k", 6, 0, S)
+        turn("k", 6, 1, V)
+        product(6, 0, 0, V)
+        product(6, 0, 1, S)
+        store(6, 0, 0, 2)
+        quantise("k", 6)
+        product(6, 0, 2, S)
+        state_to_b(7, 0, 64)
+        turn("v", 7, 0, S)
+        turn("v", 7, 1, S)
+        product(6, 0, 3, S)
+        store(6, 0, 2, 4)
+        product(6, 1, 0, V)
+        product(6, 1, 1, S)
+        store(6, 1, 0, 2)
+        quantise("b", 7)
+        quantise("v", 7)
+        state_to_a(7, 0, S)
+        state_to_a(7, 1, S)
+        product(6, 1, 2, S)
+        product(6, 1, 3, V)
+        store(6, 1, 2, 4)
+        quantise("a", 7)
+        turn("k", 7, 0, S)
+        product(7, 0, 0, V)
+        product(7, 0, 1, S)
+        store(7, 0, 0, 2)
+        turn("k", 7, 1, S)
+        quantise("k", 7, 0, 256)
+        product(7, 0, 2, V)
+        product(7, 0, 3, S)
+        store(7, 0, 2, 4)
+        quantise("k", 7, 256, 512)
+        product(7, 1, 0, S)
+        product(7, 1, 1, V)
+        store(7, 1, 0, 2)
+        product(7, 1, 2, S)
+        product(7, 1, 3, V)
+        store(7, 1, 2, 4)

@@ -329,8 +329,6 @@ def tile_mhla_pa_v_kernel(tc, k_feat, v, w_piece, grad_out, out_0, out_1):
         state_to_b(1, 0, 32)
         mix_term(3, 1)
         product(0, 0, 3, S)
-        load_tokens("v", 5)
-        load_tokens("k", 5)
         store(0, 0, 0, 4)
         product(0, 1, 0, S)
         product(0, 1, 1, S)
@@ -345,6 +343,8 @@ def tile_mhla_pa_v_kernel(tc, k_feat, v, w_piece, grad_out, out_0, out_1):
         product(0, 1, 3, V)
         mix_term(3, 3)
         store(0, 1, 0, 4)
+        load_tokens("v", 5)
+        load_tokens("k", 5)
         quantise("a", 1)
         turn("k", 1, 0, S)
         turn("k", 1, 1, V)
@@ -358,7 +358,6 @@ def tile_mhla_pa_v_kernel(tc, k_feat, v, w_piece, grad_out, out_0, out_1):
         state_to_b(2, 0, 32)
         turn("v", 2, 0, S)
         turn("v", 2, 1, S)
-        load_tokens("v", 6)
         product(1, 0, 3, S)
         store(1, 0, 0, 4)
         product(1, 1, 0, V)
@@ -371,8 +370,9 @@ def tile_mhla_pa_v_kernel(tc, k_feat, v, w_piece, grad_out, out_0, out_1):
         rows_to_b(3, S)
         product(1, 1, 2, S)
         product(1, 1, 3, V)
-        load_tokens("k", 6)
         store(1, 1, 0, 4)
+        load_tokens("v", 6)
+        load_tokens("k", 6)
         quantise("a", 2)
         turn("k", 2, 0, S)
         turn("k", 2, 1, V)
@@ -385,7 +385,6 @@ def tile_mhla_pa_v_kernel(tc, k_feat, v, w_piece, grad_out, out_0, out_1):
         state_to_b(3, 0, 32)
         turn("v", 3, 0, S)
         turn("v", 3, 1, S)
-        load_tokens("v", 7)
         product(2, 0, 3, S)
         store(2, 0, 0, 4)
         product(2, 1, 0, V)
@@ -396,8 +395,9 @@ def tile_mhla_pa_v_kernel(tc, k_feat, v, w_piece, grad_out, out_0, out_1):
         state_to_a(3, 1, S)
         product(2, 1, 2, S)
         product(2, 1, 3, V)
-        load_tokens("k", 7)
         store(2, 1, 0, 4)
+        load_tokens("v", 7)
+        load_tokens("k", 7)
         quantise("a", 3)
         turn("k", 3, 0, S)
         turn("k", 3, 1, V)

@@ -17,8 +17,7 @@ P = 128
 PAIRS = H * N
 FLOPS = 2 * 2 * PAIRS * W * D * D
 BANKS = 8
-TOKEN_BUFS = 5
-CODE_BUFS = 2
+AHEAD = 5
 RESULT_BUFS = 3
 
 
@@ -52,7 +51,7 @@ def tile_mhla_pa_v_kernel(tc, k_feat, v, w_piece, grad_out, out_0, out_1):
 
         def load_tokens(which, n):
             h, j = divmod(n, N)
-            tokens[which, n] = keep.tile([P, 2048], BF16, name="raw_" + which, bufs=TOKEN_BUFS, align_bytes=256)
+            tokens[which, n] = keep.tile([P, 2048], BF16, name="raw_" + which, bufs=AHEAD, align_bytes=256)
             src = (k_feat if which == "k" else v)[0, h, j].rearrange("(m b) d -> m (b d)", b=4)
             nc.sync.dma_start(out=tokens[which, n][:], in_=src)
 
@@ -87,27 +86,24 @@ def tile_mhla_pa_v_kernel(tc, k_feat, v, w_piece, grad_out, out_0, out_1):
                 op=ADD,
             )
 
-        w_bank = next_bank(F32)
-
         def weights():
+            bank = next_bank(F32)
             for j in range(N):
                 nc.tensor.matmul(
-                    w_bank[:, N * j : N * j + N],
+                    bank[:, N * j : N * j + N],
                     lhsT=w_rows[:, j : j + 1].to_broadcast([P, P]),
                     rhs=spread[:, 0, :],
                     start=True,
                     stop=True,
                 )
             nc.tensor.matmul(
-                w_bank[:, 16:20], lhsT=spread[:].rearrange("p r i -> p (r i)"), rhs=w_rows[:], start=True, stop=True
+                bank[:, 16:20], lhsT=spread[:].rearrange("p r i -> p (r i)"), rhs=w_rows[:], start=True, stop=True
             )
-            nc.vector.tensor_copy(out=w_all[:], in_=w_bank[:, 0:16])
-
-        def build_mixer():
+            nc.vector.tensor_copy(out=w_all[:], in_=bank[:, 0:16])
             nc.vector.tensor_tensor(
                 out=mixer[:].rearrange("p (j r) -> p j r", j=N),
                 in0=eye[:].unsqueeze(1).to_broadcast([P, N, 32]),
-                in1=w_bank[:, 16:20].unsqueeze(2).to_broadcast([P, N, 32]),
+                in1=bank[:, 16:20].unsqueeze(2).to_broadcast([P, N, 32]),
                 op=MULT,
             )
 
@@ -143,7 +139,7 @@ def tile_mhla_pa_v_kernel(tc, k_feat, v, w_piece, grad_out, out_0, out_1):
                 out=dst[:], in0=g_rows[i][:], scalar=w_ij, in1=sums[j][:], op0=MULT, op1=ADD
             )
 
-        def rows_to_b(j, engine):
+        def rows_to_b(j):
             words = mixed_rows[j][:].bitcast(F32)
             bank = next_bank(F32)
             for e in range(2):
@@ -151,14 +147,14 @@ def tile_mhla_pa_v_kernel(tc, k_feat, v, w_piece, grad_out, out_0, out_1):
                     c0 = 256 * e + 128 * w
                     nc.tensor.transpose(bank[:, c0 : c0 + 128], words[:, 256 * e + w : 256 * e + 256 : 2], ident[:])
             dst = b_tile(j)[:].bitcast(F32).rearrange("p (u q e w) -> p u q e w", u=2, e=2, w=2)
-            copy(engine, dst[:, :, 64:128, :, :], bank[:].rearrange("p (e w q u) -> p u q e w", e=2, w=2, u=2))
+            copy(S, dst[:, :, 64:128, :, :], bank[:].rearrange("p (e w q u) -> p u q e w", e=2, w=2, u=2))
 
         def b_to_state(j):
             dst = state[0][:, :, j, :].rearrange("p t (u c i) -> p u c t i", u=2, i=8)
             src = b_tile(j)[:].rearrange("p (u c i t) -> p u c t i", u=2, i=8, t=4)
             nc.vector.tensor_copy(out=dst[:, :, 16:32, :, :], in_=src[:, :, 16:32, :, :])
 
-        def mix_groups(h, x, engine):
+        def mix_groups(h, x, engine=S):
             bank = next_bank(BF16)
             for g in range(2):
                 for t in range(4):
@@ -178,29 +174,30 @@ def tile_mhla_pa_v_kernel(tc, k_feat, v, w_piece, grad_out, out_0, out_1):
                 bank[:].bitcast(F32).rearrange("p (g a y) -> p a g y", g=2, y=8),
             )
 
-        def state_to_b(n, c0, c1):
+        def state_to_b(n):
             h, j = divmod(n, N)
             dst = b_tile(n)[:].rearrange("p (u c i t) -> p u c t i", u=2, i=4, t=4)
             src = state[h][:, :, j, :].rearrange("p t (u c i) -> p u c t i", u=2, i=4)
-            nc.vector.tensor_copy(out=dst[:, :, c0:c1, :, :], in_=src[:, :, c0:c1, :, :])
+            c1 = 32 if h == 0 else 64
+            nc.vector.tensor_copy(out=dst[:, :, 0:c1, :, :], in_=src[:, :, 0:c1, :, :])
 
-        def state_to_a(n, half, engine):
+        def state_to_a(n):
             h, j = divmod(n, N)
-            if half == 0:
-                a_in[n] = work.tile([P, 2048], BF16, name="a_in", align_bytes=64)
+            a_in[n] = work.tile([P, 2048], BF16, name="a_in", align_bytes=64)
             words = state[h][:].rearrange("p t j c -> p (t j c)").bitcast(F32)
-            bank = next_bank(F32)
-            for t in range(2):
-                for u in range(2):
-                    c0 = 256 * t + 128 * u
-                    w0 = 256 * (N * (2 * half + t) + j) + 128 * u
-                    nc.tensor.transpose(bank[:, c0 : c0 + 128], words[:, w0 : w0 + 128], ident[:])
-            dst = a_in[n][:].bitcast(F32)[:, 512 * half : 512 * half + 512]
-            copy(
-                engine,
-                dst.rearrange("q (t p u) -> q t p u", t=2, u=2),
-                bank[:].rearrange("q (t u p) -> q t p u", t=2, u=2),
-            )
+            for half in range(2):
+                bank = next_bank(F32)
+                for t in range(2):
+                    for u in range(2):
+                        c0 = 256 * t + 128 * u
+                        w0 = 256 * (N * (2 * half + t) + j) + 128 * u
+                        nc.tensor.transpose(bank[:, c0 : c0 + 128], words[:, w0 : w0 + 128], ident[:])
+                dst = a_in[n][:].bitcast(F32)[:, 512 * half : 512 * half + 512]
+                copy(
+                    S,
+                    dst.rearrange("q (t p u) -> q t p u", t=2, u=2),
+                    bank[:].rearrange("q (t u p) -> q t p u", t=2, u=2),
+                )
 
         def turn(which, n, half, engine):
             if half == 0:
@@ -227,8 +224,8 @@ def tile_mhla_pa_v_kernel(tc, k_feat, v, w_piece, grad_out, out_0, out_1):
             else:
                 src, fmt = turned[which, n], E4M3
             if c0 == 0:
-                c = work.tile([P, 512], U32, name="codes_" + which, bufs=CODE_BUFS, align_bytes=64)
-                sc = work.tile([P, 512], U8, name="scales_" + which, bufs=CODE_BUFS, align_bytes=64)
+                c = work.tile([P, 512], U32, name="codes_" + which, align_bytes=64)
+                sc = work.tile([P, 512], U8, name="scales_" + which, align_bytes=64)
                 codes[which, n] = (c, sc)
             c, sc = codes[which, n]
             nc.vector.quantize_mx(out=c[:, c0:c1].bitcast(fmt), scales=sc[:, c0:c1], in_=src[:, 4 * c0 : 4 * c1])
@@ -265,6 +262,17 @@ def tile_mhla_pa_v_kernel(tc, k_feat, v, w_piece, grad_out, out_0, out_1):
             view = (out_0 if which == 0 else out_1)[0, h, j].rearrange("(m b) d -> m b d", b=4)
             nc.sync.dma_start(out=view[:, b0:b1, :], in_=results[which][:, b0:b1, :])
 
+        banks_left = list(range(8))
+        terms_left = [(j, i) for j in (2, 3) for i in (1, 2, 3)]
+
+        def next_groups(engine=S):
+            if banks_left:
+                mix_groups(1, banks_left.pop(0), engine)
+
+        def next_term():
+            if terms_left:
+                mix_term(*terms_left.pop(0))
+
         patterns()
         load_rows(0)
         load_rows(1)
@@ -278,226 +286,96 @@ def tile_mhla_pa_v_kernel(tc, k_feat, v, w_piece, grad_out, out_0, out_1):
         load_tokens("v", 1)
         load_tokens("k", 1)
         load_groups(1, 6, 16)
-        load_tokens("v", 2)
-        load_tokens("k", 2)
-        load_tokens("v", 3)
-        load_tokens("k", 3)
-        load_tokens("v", 4)
-        load_tokens("k", 4)
+        for n in range(2, AHEAD):
+            load_tokens("v", n)
+            load_tokens("k", n)
+
         weights()
-        build_mixer()
-        mix_term(0, 0, V)
-        mix_term(1, 0, S)
-        mix_term(2, 0, S)
-        mix_term(3, 0, S)
-        mix_groups(0, 0, S)
-        mix_groups(0, 1, S)
-        mix_term(0, 1)
-        mix_term(1, 1)
-        mix_term(0, 2)
-        mix_term(1, 2)
-        mix_term(0, 3)
-        mix_term(1, 3)
+        for j in range(N):
+            mix_term(j, 0, V if j == 0 else S)
+        mix_groups(0, 0)
+        mix_groups(0, 1)
+        for i in range(1, N):
+            for j in range(2):
+                mix_term(j, i)
         turn("v", 0, 0, S)
         turn("v", 0, 1, S)
-        mix_groups(0, 2, S)
-        mix_groups(0, 3, S)
-        rows_to_b(0, S)
+        mix_groups(0, 2)
+        mix_groups(0, 3)
+        rows_to_b(0)
         turn("k", 0, 0, S)
         turn("k", 0, 1, S)
-        rows_to_b(1, S)
+        rows_to_b(1)
         quantise("v", 0)
-        mix_term(2, 1)
+        next_term()
         b_to_state(0)
-        state_to_b(0, 0, 32)
-        mix_groups(1, 0, S)
+        state_to_b(0)
+        next_groups()
         turn("v", 1, 0, S)
         turn("v", 1, 1, S)
-        state_to_a(0, 0, S)
-        state_to_a(0, 1, S)
-        mix_term(2, 2)
+        state_to_a(0)
+        next_term()
         quantise("b", 0)
-        mix_groups(1, 1, S)
+        next_groups()
         quantise("k", 0)
-        mix_term(2, 3)
-        quantise("a", 0)
-        product(0, 0, 0, S)
-        product(0, 0, 1, S)
-        product(0, 0, 2, S)
-        mix_groups(1, 2, S)
-        b_to_state(1)
-        state_to_b(1, 0, 32)
-        mix_term(3, 1)
-        product(0, 0, 3, S)
-        store(0, 0, 0, 4)
-        product(0, 1, 0, S)
-        product(0, 1, 1, S)
-        mix_groups(1, 3, S)
-        quantise("b", 1)
-        mix_term(3, 2)
-        quantise("v", 1)
-        state_to_a(1, 0, S)
-        state_to_a(1, 1, S)
-        rows_to_b(2, S)
-        product(0, 1, 2, S)
-        product(0, 1, 3, V)
-        mix_term(3, 3)
-        store(0, 1, 0, 4)
-        load_tokens("v", 5)
-        load_tokens("k", 5)
-        quantise("a", 1)
-        turn("k", 1, 0, S)
-        turn("k", 1, 1, V)
-        product(1, 0, 0, V)
-        product(1, 0, 1, S)
-        quantise("k", 1)
-        product(1, 0, 2, S)
-        mix_groups(1, 4, S)
-        mix_groups(1, 5, S)
-        b_to_state(2)
-        state_to_b(2, 0, 32)
-        turn("v", 2, 0, S)
-        turn("v", 2, 1, S)
-        product(1, 0, 3, S)
-        store(1, 0, 0, 4)
-        product(1, 1, 0, V)
-        product(1, 1, 1, S)
-        mix_groups(1, 6, V)
-        quantise("b", 2)
-        quantise("v", 2)
-        state_to_a(2, 0, S)
-        state_to_a(2, 1, S)
-        rows_to_b(3, S)
-        product(1, 1, 2, S)
-        product(1, 1, 3, V)
-        store(1, 1, 0, 4)
-        load_tokens("v", 6)
-        load_tokens("k", 6)
-        quantise("a", 2)
-        turn("k", 2, 0, S)
-        turn("k", 2, 1, V)
-        product(2, 0, 0, V)
-        product(2, 0, 1, S)
-        quantise("k", 2)
-        product(2, 0, 2, S)
-        mix_groups(1, 7, V)
-        b_to_state(3)
-        state_to_b(3, 0, 32)
-        turn("v", 3, 0, S)
-        turn("v", 3, 1, S)
-        product(2, 0, 3, S)
-        store(2, 0, 0, 4)
-        product(2, 1, 0, V)
-        product(2, 1, 1, S)
-        quantise("b", 3)
-        quantise("v", 3)
-        state_to_a(3, 0, S)
-        state_to_a(3, 1, S)
-        product(2, 1, 2, S)
-        product(2, 1, 3, V)
-        store(2, 1, 0, 4)
-        load_tokens("v", 7)
-        load_tokens("k", 7)
-        quantise("a", 3)
-        turn("k", 3, 0, S)
-        turn("k", 3, 1, V)
-        product(3, 0, 0, V)
-        product(3, 0, 1, S)
-        quantise("k", 3)
-        product(3, 0, 2, S)
-        state_to_b(4, 0, 64)
-        turn("v", 4, 0, S)
-        turn("v", 4, 1, S)
-        product(3, 0, 3, S)
-        store(3, 0, 0, 4)
-        product(3, 1, 0, V)
-        product(3, 1, 1, S)
-        quantise("b", 4)
-        quantise("v", 4)
-        state_to_a(4, 0, S)
-        state_to_a(4, 1, S)
-        product(3, 1, 2, S)
-        product(3, 1, 3, V)
-        store(3, 1, 0, 4)
-        quantise("a", 4)
-        turn("k", 4, 0, S)
-        turn("k", 4, 1, V)
-        product(4, 0, 0, V)
-        product(4, 0, 1, S)
-        quantise("k", 4)
-        product(4, 0, 2, S)
-        state_to_b(5, 0, 64)
-        turn("v", 5, 0, S)
-        turn("v", 5, 1, S)
-        product(4, 0, 3, S)
-        store(4, 0, 0, 4)
-        product(4, 1, 0, V)
-        product(4, 1, 1, S)
-        quantise("b", 5)
-        quantise("v", 5)
-        state_to_a(5, 0, S)
-        state_to_a(5, 1, S)
-        product(4, 1, 2, S)
-        product(4, 1, 3, V)
-        store(4, 1, 0, 4)
-        quantise("a", 5)
-        turn("k", 5, 0, S)
-        turn("k", 5, 1, V)
-        product(5, 0, 0, V)
-        product(5, 0, 1, S)
-        quantise("k", 5)
-        product(5, 0, 2, S)
-        state_to_b(6, 0, 64)
-        turn("v", 6, 0, S)
-        turn("v", 6, 1, S)
-        product(5, 0, 3, S)
-        store(5, 0, 0, 4)
-        product(5, 1, 0, V)
-        product(5, 1, 1, S)
-        quantise("b", 6)
-        quantise("v", 6)
-        state_to_a(6, 0, S)
-        state_to_a(6, 1, S)
-        product(5, 1, 2, S)
-        product(5, 1, 3, V)
-        store(5, 1, 0, 4)
-        quantise("a", 6)
-        turn("k", 6, 0, S)
-        turn("k", 6, 1, V)
-        product(6, 0, 0, V)
-        product(6, 0, 1, S)
-        store(6, 0, 0, 2)
-        quantise("k", 6)
-        product(6, 0, 2, S)
-        state_to_b(7, 0, 64)
-        turn("v", 7, 0, S)
-        turn("v", 7, 1, S)
-        product(6, 0, 3, S)
-        store(6, 0, 2, 4)
-        product(6, 1, 0, V)
-        product(6, 1, 1, S)
-        store(6, 1, 0, 2)
-        quantise("b", 7)
-        quantise("v", 7)
-        state_to_a(7, 0, S)
-        state_to_a(7, 1, S)
-        product(6, 1, 2, S)
-        product(6, 1, 3, V)
-        store(6, 1, 2, 4)
-        quantise("a", 7)
-        turn("k", 7, 0, S)
-        product(7, 0, 0, V)
-        product(7, 0, 1, S)
-        store(7, 0, 0, 2)
-        turn("k", 7, 1, S)
-        quantise("k", 7, 0, 256)
-        product(7, 0, 2, V)
-        product(7, 0, 3, S)
-        store(7, 0, 2, 4)
-        quantise("k", 7, 256, 512)
-        product(7, 1, 0, S)
-        product(7, 1, 1, V)
-        store(7, 1, 0, 2)
-        product(7, 1, 2, S)
-        product(7, 1, 3, V)
-        store(7, 1, 2, 4)
+        next_term()
+
+        for n in range(PAIRS - 1):
+            helper = V if n > 0 else S
+            halves = n == PAIRS - 2
+            quantise("a", n)
+            if n > 0:
+                turn("k", n, 0, S)
+                turn("k", n, 1, V)
+            product(n, 0, 0, helper)
+            product(n, 0, 1, S)
+            if halves:
+                store(n, 0, 0, 2)
+            if n > 0:
+                quantise("k", n)
+            product(n, 0, 2, S)
+            next_groups()
+            if n == 1:
+                next_groups()
+            if n + 1 < N:
+                b_to_state(n + 1)
+            state_to_b(n + 1)
+            if n > 0:
+                turn("v", n + 1, 0, S)
+                turn("v", n + 1, 1, S)
+            next_term()
+            product(n, 0, 3, S)
+            store(n, 0, 2 if halves else 0, 4)
+            product(n, 1, 0, helper)
+            product(n, 1, 1, S)
+            if halves:
+                store(n, 1, 0, 2)
+            next_groups(helper)
+            quantise("b", n + 1)
+            next_term()
+            quantise("v", n + 1)
+            state_to_a(n + 1)
+            if n + 2 < N:
+                rows_to_b(n + 2)
+            product(n, 1, 2, S)
+            product(n, 1, 3, V)
+            next_term()
+            store(n, 1, 2 if halves else 0, 4)
+            if n + AHEAD < PAIRS:
+                load_tokens("v", n + AHEAD)
+                load_tokens("k", n + AHEAD)
+
+        n = PAIRS - 1
+        quantise("a", n)
+        for half in range(2):
+            turn("k", n, half, S)
+            if half == 1:
+                quantise("k", n, 0, 256)
+            product(n, 0, 2 * half, V)
+            product(n, 0, 2 * half + 1, S)
+            store(n, 0, 2 * half, 2 * half + 2)
+        quantise("k", n, 256, 512)
+        for half in range(2):
+            product(n, 1, 2 * half, S)
+            product(n, 1, 2 * half + 1, V)
+            store(n, 1, 2 * half, 2 * half + 2)

@@ -276,11 +276,11 @@ def tile_mhla_pa_v_kernel(tc, k_feat, v, w_piece, grad_out, out_0, out_1):
         patterns()
         load_rows(0)
         load_rows(1)
-        load_groups(0, 0, 4)
         load_rows(2)
         load_tokens("v", 0)
-        load_groups(0, 4, 8)
+        load_groups(0, 0, 4)
         load_rows(3)
+        load_groups(0, 4, 8)
         load_tokens("k", 0)
         load_groups(1, 0, 6)
         load_tokens("v", 1)
@@ -293,13 +293,13 @@ def tile_mhla_pa_v_kernel(tc, k_feat, v, w_piece, grad_out, out_0, out_1):
         weights()
         for j in range(N):
             mix_term(j, 0, V if j == 0 else S)
-        mix_groups(0, 0)
-        mix_groups(0, 1)
         for i in range(1, N):
             for j in range(2):
                 mix_term(j, i)
         turn("v", 0, 0, S)
         turn("v", 0, 1, S)
+        mix_groups(0, 0)
+        mix_groups(0, 1)
         mix_groups(0, 2)
         mix_groups(0, 3)
         rows_to_b(0)
@@ -322,7 +322,8 @@ def tile_mhla_pa_v_kernel(tc, k_feat, v, w_piece, grad_out, out_0, out_1):
 
         for n in range(PAIRS - 1):
             helper = V if n > 0 else S
-            halves = n == PAIRS - 2
+            halves = n >= 6
+            early = n >= 5
             quantise("a", n)
             if n > 0:
                 turn("k", n, 0, S)
@@ -334,6 +335,9 @@ def tile_mhla_pa_v_kernel(tc, k_feat, v, w_piece, grad_out, out_0, out_1):
             if n > 0:
                 quantise("k", n)
             product(n, 0, 2, S)
+            if early:
+                product(n, 0, 3, S)
+                store(n, 0, 2 if halves else 0, 4)
             next_groups()
             if n == 1:
                 next_groups()
@@ -344,8 +348,9 @@ def tile_mhla_pa_v_kernel(tc, k_feat, v, w_piece, grad_out, out_0, out_1):
                 turn("v", n + 1, 0, S)
                 turn("v", n + 1, 1, S)
             next_term()
-            product(n, 0, 3, S)
-            store(n, 0, 2 if halves else 0, 4)
+            if not early:
+                product(n, 0, 3, S)
+                store(n, 0, 2 if halves else 0, 4)
             product(n, 1, 0, helper)
             product(n, 1, 1, S)
             if halves:
@@ -354,13 +359,16 @@ def tile_mhla_pa_v_kernel(tc, k_feat, v, w_piece, grad_out, out_0, out_1):
             quantise("b", n + 1)
             next_term()
             quantise("v", n + 1)
-            state_to_a(n + 1)
+            if n < 7:
+                state_to_a(n + 1)
             if n + 2 < N:
                 rows_to_b(n + 2)
             product(n, 1, 2, S)
             product(n, 1, 3, V)
             next_term()
             store(n, 1, 2 if halves else 0, 4)
+            if n >= 7:
+                state_to_a(n + 1)
             if n + AHEAD < PAIRS:
                 load_tokens("v", n + AHEAD)
                 load_tokens("k", n + AHEAD)

@@ -364,7 +364,7 @@ def tile_mhla_pa_v_kernel(tc, k_feat, v, w_piece, grad_out, out_0, out_1):
             if n + 2 < N:
                 rows_to_b(n + 2)
             product(n, 1, 2, S)
-            product(n, 1, 3, V)
+            product(n, 1, 3, S if n == 4 else V)
             next_term()
             store(n, 1, 2 if halves else 0, 4)
             if n >= 7:

@@ -327,7 +327,7 @@ def tile_mhla_pa_v_kernel(tc, k_feat, v, w_piece, grad_out, out_0, out_1):
             quantise("a", n)
             if n > 0:
                 turn("k", n, 0, S)
-                turn("k", n, 1, V)
+                turn("k", n, 1, S if n in (1, 4) else V)
             product(n, 0, 0, helper)
             product(n, 0, 1, S)
             if halves:
@@ -364,7 +364,7 @@ def tile_mhla_pa_v_kernel(tc, k_feat, v, w_piece, grad_out, out_0, out_1):
             if n + 2 < N:
                 rows_to_b(n + 2)
             product(n, 1, 2, S)
-            product(n, 1, 3, S if n == 4 else V)
+            product(n, 1, 3, V)
             next_term()
             store(n, 1, 2 if halves else 0, 4)
             if n >= 7:

@@ -323,11 +323,12 @@ def tile_mhla_pa_v_kernel(tc, k_feat, v, w_piece, grad_out, out_0, out_1):
         for n in range(PAIRS - 1):
             helper = V if n > 0 else S
             halves = n >= 6
+            halves_1 = n >= 5
             early = n >= 5
             quantise("a", n)
             if n > 0:
                 turn("k", n, 0, S)
-                turn("k", n, 1, S if n in (1, 4) else V)
+                turn("k", n, 1, S if n in (1, 4, 6) else V)
             product(n, 0, 0, helper)
             product(n, 0, 1, S)
             if halves:
@@ -353,7 +354,7 @@ def tile_mhla_pa_v_kernel(tc, k_feat, v, w_piece, grad_out, out_0, out_1):
                 store(n, 0, 2 if halves else 0, 4)
             product(n, 1, 0, helper)
             product(n, 1, 1, S)
-            if halves:
+            if halves_1:
                 store(n, 1, 0, 2)
             next_groups(helper)
             quantise("b", n + 1)
@@ -366,7 +367,7 @@ def tile_mhla_pa_v_kernel(tc, k_feat, v, w_piece, grad_out, out_0, out_1):
             product(n, 1, 2, S)
             product(n, 1, 3, V)
             next_term()
-            store(n, 1, 2 if halves else 0, 4)
+            store(n, 1, 2 if halves_1 else 0, 4)
             if n >= 7:
                 state_to_a(n + 1)
             if n + AHEAD < PAIRS:

@@ -17,7 +17,7 @@ P = 128
 PAIRS = H * N
 FLOPS = 2 * 2 * PAIRS * W * D * D
 BANKS = 8
-AHEAD = 5
+RAW_WINDOWS = 3
 RESULT_BUFS = 3
 
 
@@ -49,11 +49,15 @@ def tile_mhla_pa_v_kernel(tc, k_feat, v, w_piece, grad_out, out_0, out_1):
         g_rows = {}
         g_groups = {}
 
-        def load_tokens(which, n):
-            h, j = divmod(n, N)
-            tokens[which, n] = keep.tile([P, 2048], BF16, name="raw_" + which, bufs=AHEAD, align_bytes=256)
-            src = (k_feat if which == "k" else v)[0, h, j].rearrange("(m b) d -> m (b d)", b=4)
-            nc.sync.dma_start(out=tokens[which, n][:], in_=src)
+        def load_tokens(which, n, windows, tile=None, place=0):
+            if tile is None:
+                tile = keep.tile([P, 2048 * RAW_WINDOWS], BF16, name="raw_" + which, bufs=2, align_bytes=256)
+            for w in range(windows):
+                tokens[which, n + w] = tile[:, 2048 * (place + w) : 2048 * (place + w + 1)]
+            src = (k_feat if which == "k" else v)[0].rearrange("h j (m b) d -> m (h j) (b d)", b=4)
+            dst = tile[:, 2048 * place : 2048 * (place + windows)].rearrange("p (w c) -> p w c", w=windows)
+            nc.sync.dma_start(out=dst, in_=src[:, n : n + windows, :])
+            return tile
 
         def load_rows(i):
             g_rows[i] = keep.tile([P, 1024], BF16, name="g_row%d" % i, align_bytes=256)
@@ -277,18 +281,18 @@ def tile_mhla_pa_v_kernel(tc, k_feat, v, w_piece, grad_out, out_0, out_1):
         load_rows(0)
         load_rows(1)
         load_rows(2)
-        load_tokens("v", 0)
+        first_v = load_tokens("v", 0, 1)
         load_groups(0, 0, 4)
         load_rows(3)
         load_groups(0, 4, 8)
-        load_tokens("k", 0)
+        first_k = load_tokens("k", 0, 1)
         load_groups(1, 0, 6)
-        load_tokens("v", 1)
-        load_tokens("k", 1)
+        load_tokens("v", 1, 1, first_v, 1)
+        load_tokens("k", 1, 1, first_k, 1)
         load_groups(1, 6, 16)
-        for n in range(2, AHEAD):
-            load_tokens("v", n)
-            load_tokens("k", n)
+        load_tokens("v", 2, 3)
+        load_tokens("k", 2, 3)
+        late_loads = ["v", "k"]
 
         weights()
         for j in range(N):
@@ -323,7 +327,6 @@ def tile_mhla_pa_v_kernel(tc, k_feat, v, w_piece, grad_out, out_0, out_1):
         for n in range(PAIRS - 1):
             helper = V if n > 0 else S
             halves = n >= 6
-            halves_1 = n >= 5
             early = n >= 5
             quantise("a", n)
             if n > 0:
@@ -354,7 +357,7 @@ def tile_mhla_pa_v_kernel(tc, k_feat, v, w_piece, grad_out, out_0, out_1):
                 store(n, 0, 2 if halves else 0, 4)
             product(n, 1, 0, helper)
             product(n, 1, 1, S)
-            if halves_1:
+            if halves:
                 store(n, 1, 0, 2)
             next_groups(helper)
             quantise("b", n + 1)
@@ -367,12 +370,11 @@ def tile_mhla_pa_v_kernel(tc, k_feat, v, w_piece, grad_out, out_0, out_1):
             product(n, 1, 2, S)
             product(n, 1, 3, V)
             next_term()
-            store(n, 1, 2 if halves_1 else 0, 4)
+            store(n, 1, 2 if halves else 0, 4)
             if n >= 7:
                 state_to_a(n + 1)
-            if n + AHEAD < PAIRS:
-                load_tokens("v", n + AHEAD)
-                load_tokens("k", n + AHEAD)
+            if late_loads:
+                load_tokens(late_loads.pop(0), 5, 3)
 
         n = PAIRS - 1
         quantise("a", n)

@@ -286,10 +286,9 @@ def tile_mhla_pa_v_kernel(tc, k_feat, v, w_piece, grad_out, out_0, out_1):
         load_rows(3)
         load_groups(0, 4, 8)
         first_k = load_tokens("k", 0, 1)
-        load_groups(1, 0, 6)
         load_tokens("v", 1, 1, first_v, 1)
         load_tokens("k", 1, 1, first_k, 1)
-        load_groups(1, 6, 16)
+        load_groups(1, 0, 16)
         load_tokens("v", 2, 3)
         load_tokens("k", 2, 3)
         late_loads = ["v", "k"]
@@ -314,22 +313,26 @@ def tile_mhla_pa_v_kernel(tc, k_feat, v, w_piece, grad_out, out_0, out_1):
         next_term()
         b_to_state(0)
         state_to_b(0)
-        next_groups()
         turn("v", 1, 0, S)
         turn("v", 1, 1, S)
         state_to_a(0)
         next_term()
         quantise("b", 0)
-        next_groups()
+        turn("k", 1, 0, S)
+        turn("k", 1, 1, S)
         quantise("k", 0)
         next_term()
 
         for n in range(PAIRS - 1):
             helper = V if n > 0 else S
             halves = n >= 6
+            halves_1 = n >= 5
             early = n >= 5
             quantise("a", n)
-            if n > 0:
+            if n == 1:
+                next_groups()
+                next_groups()
+            if n > 1:
                 turn("k", n, 0, S)
                 turn("k", n, 1, S if n in (1, 4, 6) else V)
             product(n, 0, 0, helper)
@@ -342,7 +345,8 @@ def tile_mhla_pa_v_kernel(tc, k_feat, v, w_piece, grad_out, out_0, out_1):
             if early:
                 product(n, 0, 3, S)
                 store(n, 0, 2 if halves else 0, 4)
-            next_groups()
+            if n > 0:
+                next_groups()
             if n == 1:
                 next_groups()
             if n + 1 < N:
@@ -357,9 +361,11 @@ def tile_mhla_pa_v_kernel(tc, k_feat, v, w_piece, grad_out, out_0, out_1):
                 store(n, 0, 2 if halves else 0, 4)
             product(n, 1, 0, helper)
             product(n, 1, 1, S)
-            if halves:
+            if halves_1:
                 store(n, 1, 0, 2)
             next_groups(helper)
+            if n == 0:
+                next_groups()
             quantise("b", n + 1)
             next_term()
             quantise("v", n + 1)
@@ -370,7 +376,7 @@ def tile_mhla_pa_v_kernel(tc, k_feat, v, w_piece, grad_out, out_0, out_1):
             product(n, 1, 2, S)
             product(n, 1, 3, V)
             next_term()
-            store(n, 1, 2 if halves else 0, 4)
+            store(n, 1, 2 if halves_1 else 0, 4)
             if n >= 7:
                 state_to_a(n + 1)
             if late_loads:

@@ -71,18 +71,25 @@ def tile_mhla_pa_v_kernel(tc, k_feat, v, w_piece, grad_out, out_0, out_1):
                 src = grad_out[0, h, i].rearrange("(x r) d -> r x d", r=32)
                 nc.sync.dma_start(out=tile[i:P:4, :, :], in_=src[:, x0:x1, :])
 
+        def load_head(h):
+            tile = keep.tile([P, 16, 512], BF16, name="g_mix%d" % h, align_bytes=256)
+            for x in range(16):
+                g_groups[h, x] = tile[:, x, :]
+            nc.sync.dma_start(out=tile[:], in_=grad_out[0, h].rearrange("i (x r) d -> r (i x) d", r=32))
+
         w_rows = const.tile([P, N], BF16, name="w_rows")
         ident = const.tile([P, P], F32, name="ident")
         eye = const.tile([P, 32], F32, name="eye")
-        spread = const.tile([P, 32, N], BF16, name="spread", align_bytes=64)
+        spread = const.tile([P, N, 32], BF16, name="spread", align_bytes=64)
         w_all = const.tile([P, N * N], F32, name="w_all")
         mixer = const.tile([P, P], BF16, name="mixer", align_bytes=64)
 
         def patterns():
-            nc.gpsimd.memset(w_rows[:], 0.0)
-            nc.sync.dma_start(out=w_rows[0:N, :], in_=w_piece)
+            nc.sync.dma_start(out=w_rows[0:32, :], in_=w_piece.partition_broadcast(8))
+            nc.gpsimd.memset(w_rows[32:64, :], 0.0)
+            nc.gpsimd.memset(w_rows[64:P, :], 0.0)
             make_identity(nc, ident[:])
-            nc.scalar.copy(out=spread[:], in_=ident[:, 0:N].unsqueeze(1).to_broadcast([P, 32, N]))
+            nc.scalar.copy(out=spread[:], in_=ident[:, 0:32].unsqueeze(1).to_broadcast([P, N, 32]))
             nc.vector.tensor_reduce(
                 out=eye[:].rearrange("p (u q e) -> p q u e", u=2, e=2),
                 in_=ident[:].rearrange("p (q u e i) -> p q u e i", u=2, e=2, i=4),
@@ -96,7 +103,7 @@ def tile_mhla_pa_v_kernel(tc, k_feat, v, w_piece, grad_out, out_0, out_1):
                 nc.tensor.matmul(
                     bank[:, N * j : N * j + N],
                     lhsT=w_rows[:, j : j + 1].to_broadcast([P, P]),
-                    rhs=spread[:, 0, :],
+                    rhs=spread[:, 0, 0:N],
                     start=True,
                     stop=True,
                 )
@@ -288,7 +295,7 @@ def tile_mhla_pa_v_kernel(tc, k_feat, v, w_piece, grad_out, out_0, out_1):
         first_k = load_tokens("k", 0, 1)
         load_tokens("v", 1, 1, first_v, 1)
         load_tokens("k", 1, 1, first_k, 1)
-        load_groups(1, 0, 16)
+        load_head(1)
         load_tokens("v", 2, 3)
         load_tokens("k", 2, 3)
         late_loads = ["v", "k"]

@@ -17,6 +17,8 @@ P = 128
 PAIRS = H * N
 FLOPS = 2 * 2 * PAIRS * W * D * D
 BANKS = 8
+HELD = 3
+GROUPS = 16
 RAW_WINDOWS = 3
 RESULT_BUFS = 3
 
@@ -31,13 +33,13 @@ def tile_mhla_pa_v_kernel(tc, k_feat, v, w_piece, grad_out, out_0, out_1):
         psum = ctx.enter_context(tc.psum_pool(name="psum", bufs=1))
         ctx.enter_context(tc.manual_schedule())
 
-        taken = []
+        ring = list(range(BANKS - HELD))
 
-        def next_bank(dtype):
-            columns = 512 if dtype == F32 else 1024
-            tile = psum.tile([P, columns], dtype, name="bank%d" % (len(taken) % BANKS))
-            taken.append(tile)
-            return tile
+        def next_bank(dtype, slot=None):
+            if slot is None:
+                slot = ring.pop(0)
+                ring.append(slot)
+            return psum.tile([P, 512 if dtype == F32 else 1024], dtype, name="bank%d" % slot)
 
         def copy(engine, dst, src):
             if engine is V:
@@ -46,7 +48,6 @@ def tile_mhla_pa_v_kernel(tc, k_feat, v, w_piece, grad_out, out_0, out_1):
                 nc.scalar.copy(out=dst, in_=src)
 
         tokens = {}
-        g_rows = {}
         g_groups = {}
 
         def load_tokens(which, n, windows, tile=None, place=0):
@@ -59,23 +60,17 @@ def tile_mhla_pa_v_kernel(tc, k_feat, v, w_piece, grad_out, out_0, out_1):
             nc.sync.dma_start(out=dst, in_=src[:, n : n + windows, :])
             return tile
 
-        def load_rows(i):
-            g_rows[i] = keep.tile([P, 1024], BF16, name="g_row%d" % i, align_bytes=256)
-            nc.sync.dma_start(out=g_rows[i][:], in_=grad_out[0, 0, i, 256:512, :].rearrange("(r e) d -> r (e d)", e=2))
+        def load_group(x):
+            tile = keep.tile([P, 512], BF16, name="g_one%d" % x, align_bytes=256)
+            g_groups[0, x] = tile[:, :]
+            nc.sync.dma_start(out=tile[:], in_=grad_out[0, 0, :, 32 * x : 32 * x + 32, :].rearrange("i r d -> r i d"))
 
-        def load_groups(h, x0, x1):
-            tile = keep.tile([P, x1 - x0, 512], BF16, name="g_mix%d_%d" % (h, x0), align_bytes=256)
-            for x in range(x0, x1):
-                g_groups[h, x] = tile[:, x - x0, :]
-            for i in range(N):
-                src = grad_out[0, h, i].rearrange("(x r) d -> r x d", r=32)
-                nc.sync.dma_start(out=tile[i:P:4, :, :], in_=src[:, x0:x1, :])
-
-        def load_head(h):
-            tile = keep.tile([P, 16, 512], BF16, name="g_mix%d" % h, align_bytes=256)
-            for x in range(16):
-                g_groups[h, x] = tile[:, x, :]
-            nc.sync.dma_start(out=tile[:], in_=grad_out[0, h].rearrange("i (x r) d -> r (i x) d", r=32))
+        def load_every(h, x0, step):
+            tile = keep.tile([P, GROUPS // step, 512], BF16, name="g_every%d_%d" % (h, x0), align_bytes=256)
+            for x in range(x0, GROUPS, step):
+                g_groups[h, x] = tile[:, x // step, :]
+            src = grad_out[0, h].rearrange("i (x r) d -> r (i x) d", r=32)
+            nc.sync.dma_start(out=tile[:], in_=src[:, x0 : N * GROUPS : step, :])
 
         w_rows = const.tile([P, N], BF16, name="w_rows")
         ident = const.tile([P, P], F32, name="ident")
@@ -83,12 +78,17 @@ def tile_mhla_pa_v_kernel(tc, k_feat, v, w_piece, grad_out, out_0, out_1):
         spread = const.tile([P, N, 32], BF16, name="spread", align_bytes=64)
         w_all = const.tile([P, N * N], F32, name="w_all")
         mixer = const.tile([P, P], BF16, name="mixer", align_bytes=64)
+        sorter = const.tile([P, P], BF16, name="sorter", align_bytes=64)
 
         def patterns():
             nc.sync.dma_start(out=w_rows[0:32, :], in_=w_piece.partition_broadcast(8))
             nc.gpsimd.memset(w_rows[32:64, :], 0.0)
             nc.gpsimd.memset(w_rows[64:P, :], 0.0)
             make_identity(nc, ident[:])
+            nc.vector.tensor_copy(
+                out=sorter[:].rearrange("p (i u q e) -> p i u q e", i=N, u=2, e=2),
+                in_=ident[:].rearrange("p (q u e i) -> p i u q e", u=2, e=2, i=N),
+            )
             nc.scalar.copy(out=spread[:], in_=ident[:, 0:32].unsqueeze(1).to_broadcast([P, N, 32]))
             nc.vector.tensor_reduce(
                 out=eye[:].rearrange("p (u q e) -> p q u e", u=2, e=2),
@@ -118,97 +118,100 @@ def tile_mhla_pa_v_kernel(tc, k_feat, v, w_piece, grad_out, out_0, out_1):
                 op=MULT,
             )
 
-        state = [keep.tile([P, 4, N, 512], BF16, name="mixed%d" % h, align_bytes=64) for h in range(H)]
+        state = [keep.tile([P, N * 2048], BF16, name="mixed%d" % h, align_bytes=64) for h in range(H)]
+        raw = {}
         sums = {}
-        mixed_rows = {}
         b_in = {}
         a_in = {}
         turned = {}
         codes = {}
         results = {}
 
-        def b_tile(n):
-            if n not in b_in:
-                b_in[n] = work.tile([P, 2048], BF16, name="b_in", align_bytes=64)
-            return b_in[n]
+        def turn_groups(x0, count, run):
+            bank = next_bank(BF16, BANKS - HELD + len(raw) % HELD)
+            view = bank[:, 0 : 512 * count].rearrange("p (i t u g y) -> p i t u g y", i=N, t=4, u=2, g=count)
+            for g in range(count):
+                for t in range(4):
+                    nc.tensor.transpose(view[:, :, t, :, g, :], g_groups[0, x0 + g][:, t:512:4], sorter[:])
+            raw[x0] = (view.rearrange("p i t u g y -> p i (t u) (g y)")[:, :, :, 0:run], run)
 
-        def mix_term(j, i, engine=V):
+        def mix_term(x0, j, i, engine=V):
+            terms, run = raw[x0]
             w_ij = w_all[:, N * j + i : N * j + i + 1]
             if i == 0:
-                sums[j] = work.tile([P, 1024], F32, name="acc", bufs=N)
-                if engine is V:
-                    nc.vector.tensor_scalar(out=sums[j][:], in0=g_rows[i][:], scalar1=w_ij, scalar2=None, op0=MULT)
-                else:
-                    nc.scalar.activation(
-                        out=sums[j][:], in_=g_rows[i][:], func=mybir.ActivationFunctionType.Copy, scale=w_ij
-                    )
-                return
-            if i == N - 1:
-                mixed_rows[j] = work.tile([P, 1024], BF16, name="row", bufs=N - 1, align_bytes=64)
-            dst = mixed_rows[j] if i == N - 1 else sums[j]
-            nc.vector.scalar_tensor_tensor(
-                out=dst[:], in0=g_rows[i][:], scalar=w_ij, in1=sums[j][:], op0=MULT, op1=ADD
-            )
+                sums[x0, j] = work.tile([P, 256], F32, name="acc", bufs=2 * N)
+            acc = sums[x0, j][:, 0 : 8 * run].rearrange("p (a c) -> p a c", a=8)
+            if i == 0 and engine is V:
+                nc.vector.tensor_scalar(out=acc, in0=terms[:, i], scalar1=w_ij, scalar2=None, op0=MULT)
+            elif i == 0:
+                nc.scalar.activation(out=acc, in_=terms[:, i], func=mybir.ActivationFunctionType.Copy, scale=w_ij)
+            else:
+                window = state[0][:, 2048 * j : 2048 * (j + 1)].rearrange("p (a c) -> p a c", a=8)
+                dst = acc if i < N - 1 else window[:, :, 16 * x0 : 16 * x0 + run]
+                nc.vector.scalar_tensor_tensor(out=dst, in0=terms[:, i], scalar=w_ij, in1=acc, op0=MULT, op1=ADD)
 
-        def rows_to_b(j):
-            words = mixed_rows[j][:].bitcast(F32)
-            bank = next_bank(F32)
-            for e in range(2):
-                for w in range(2):
-                    c0 = 256 * e + 128 * w
-                    nc.tensor.transpose(bank[:, c0 : c0 + 128], words[:, 256 * e + w : 256 * e + 256 : 2], ident[:])
-            dst = b_tile(j)[:].bitcast(F32).rearrange("p (u q e w) -> p u q e w", u=2, e=2, w=2)
-            copy(S, dst[:, :, 64:128, :, :], bank[:].rearrange("p (e w q u) -> p u q e w", e=2, w=2, u=2))
+        def first_terms(x0, engine):
+            for j in range(N):
+                mix_term(x0, j, 0, engine)
 
-        def b_to_state(j):
-            dst = state[0][:, :, j, :].rearrange("p t (u c i) -> p u c t i", u=2, i=8)
-            src = b_tile(j)[:].rearrange("p (u c i t) -> p u c t i", u=2, i=8, t=4)
-            nc.vector.tensor_copy(out=dst[:, :, 16:32, :, :], in_=src[:, :, 16:32, :, :])
+        def later_terms(x0):
+            for i in range(1, N):
+                for j in range(N):
+                    mix_term(x0, j, i)
 
-        def mix_groups(h, x, engine=S):
+        def mix_groups(h, x0, count, engine=S, step=1):
             bank = next_bank(BF16)
-            for g in range(2):
+            view = bank[:, 0 : 512 * count].rearrange("p (g j t c) -> p g j t c", g=count, j=N, t=4)
+            for g in range(count):
                 for t in range(4):
-                    c0 = 512 * g + 128 * t
-                    nc.tensor.matmul(
-                        bank[:, c0 : c0 + 128],
-                        lhsT=g_groups[h, 2 * x + g][:, t:512:4],
-                        rhs=mixer[:],
-                        start=True,
-                        stop=True,
-                    )
-            words = state[h][:].rearrange("p t j c -> p (t j c)").bitcast(F32)
-            dst = words.rearrange("p (a q) -> p a q", q=128)[:, :, 16 * x : 16 * x + 16]
+                    rows = g_groups[h, x0 + step * g]
+                    nc.tensor.matmul(view[:, g, :, t, :], lhsT=rows[:, t:512:4], rhs=mixer[:], start=True, stop=True)
+            dst = state[h][:].bitcast(F32).rearrange("p (a x y) -> p a x y", x=GROUPS, y=8)
             copy(
                 engine,
-                dst.rearrange("p a (g y) -> p a g y", g=2),
-                bank[:].bitcast(F32).rearrange("p (g a y) -> p a g y", g=2, y=8),
+                dst[:, :, x0 : x0 + step * (count - 1) + 1 : step, :],
+                bank[:, 0 : 512 * count].bitcast(F32).rearrange("p (g a y) -> p a g y", g=count, y=8),
             )
+
+        def mix_group_and_half(x, y):
+            bank = next_bank(BF16)
+            whole = bank[:, 0:512].rearrange("p (j t c) -> p j t c", j=N, t=4)
+            half = bank[:, 512:768].rearrange("p (j t u c) -> p j t u c", j=N, t=4, u=2)
+            upper = mixer[:].rearrange("p (j u c) -> p j u c", j=N, u=2)[:, :, :, 8:16]
+            for t in range(4):
+                nc.tensor.matmul(whole[:, :, t, :], lhsT=g_groups[0, x][:, t:512:4], rhs=mixer[:], start=True, stop=True)
+            for t in range(4):
+                nc.tensor.matmul(half[:, :, t, :, :], lhsT=g_groups[0, y][:, t:512:4], rhs=upper, start=True, stop=True)
+            dst = state[0][:].bitcast(F32).rearrange("p (a q) -> p a q", q=128)
+            copy(S, dst[:, :, 8 * x : 8 * x + 8], bank[:, 0:512].bitcast(F32).rearrange("p (a y) -> p a y", y=8))
+            copy(S, dst[:, :, 8 * y + 4 : 8 * y + 8], bank[:, 512:768].bitcast(F32).rearrange("p (a y) -> p a y", y=4))
 
         def state_to_b(n):
             h, j = divmod(n, N)
-            dst = b_tile(n)[:].rearrange("p (u c i t) -> p u c t i", u=2, i=4, t=4)
-            src = state[h][:, :, j, :].rearrange("p t (u c i) -> p u c t i", u=2, i=4)
-            c1 = 32 if h == 0 else 64
-            nc.vector.tensor_copy(out=dst[:, :, 0:c1, :, :], in_=src[:, :, 0:c1, :, :])
+            b_in[n] = work.tile([P, 2048], BF16, name="b_in", align_bytes=64)
+            dst = b_in[n][:].rearrange("p (c i t) -> p c t i", i=4, t=4)
+            src = state[h][:, 2048 * j : 2048 * (j + 1)].rearrange("p (t c i) -> p c t i", t=4, i=4)
+            nc.vector.tensor_copy(out=dst, in_=src)
 
-        def state_to_a(n):
+        def state_to_a(n, half, engines):
             h, j = divmod(n, N)
-            a_in[n] = work.tile([P, 2048], BF16, name="a_in", align_bytes=64)
-            words = state[h][:].rearrange("p t j c -> p (t j c)").bitcast(F32)
-            for half in range(2):
-                bank = next_bank(F32)
+            if half == 0:
+                a_in[n] = work.tile([P, 2048], BF16, name="a_in", align_bytes=64)
+            words = state[h][:].bitcast(F32)
+            bank = next_bank(F32)
+            for t in range(2):
+                for u in range(2):
+                    c0 = 256 * t + 128 * u
+                    w0 = 1024 * j + 512 * half + c0
+                    nc.tensor.transpose(bank[:, c0 : c0 + 128], words[:, w0 : w0 + 128], ident[:])
+            dst = a_in[n][:].bitcast(F32)[:, 512 * half : 512 * half + 512]
+            dst = dst.rearrange("q (t p u) -> q t p u", t=2, u=2)
+            src = bank[:].rearrange("q (t u p) -> q t p u", t=2, u=2)
+            if len(engines) == 1:
+                copy(engines[0], dst, src)
+            else:
                 for t in range(2):
-                    for u in range(2):
-                        c0 = 256 * t + 128 * u
-                        w0 = 256 * (N * (2 * half + t) + j) + 128 * u
-                        nc.tensor.transpose(bank[:, c0 : c0 + 128], words[:, w0 : w0 + 128], ident[:])
-                dst = a_in[n][:].bitcast(F32)[:, 512 * half : 512 * half + 512]
-                copy(
-                    S,
-                    dst.rearrange("q (t p u) -> q t p u", t=2, u=2),
-                    bank[:].rearrange("q (t u p) -> q t p u", t=2, u=2),
-                )
+                    copy(engines[t], dst[:, t, :, :], src[:, t, :, :])
 
         def turn(which, n, half, engine):
             if half == 0:
@@ -273,133 +276,107 @@ def tile_mhla_pa_v_kernel(tc, k_feat, v, w_piece, grad_out, out_0, out_1):
             view = (out_0 if which == 0 else out_1)[0, h, j].rearrange("(m b) d -> m b d", b=4)
             nc.sync.dma_start(out=view[:, b0:b1, :], in_=results[which][:, b0:b1, :])
 
-        banks_left = list(range(8))
-        terms_left = [(j, i) for j in (2, 3) for i in (1, 2, 3)]
-
-        def next_groups(engine=S):
-            if banks_left:
-                mix_groups(1, banks_left.pop(0), engine)
-
-        def next_term():
-            if terms_left:
-                mix_term(*terms_left.pop(0))
-
         patterns()
-        load_rows(0)
-        load_rows(1)
-        load_rows(2)
+        load_group(0)
+        load_group(4)
+        load_group(5)
         first_v = load_tokens("v", 0, 1)
-        load_groups(0, 0, 4)
-        load_rows(3)
-        load_groups(0, 4, 8)
+        load_every(0, 2, 4)
+        load_group(8)
+        load_group(9)
         first_k = load_tokens("k", 0, 1)
+        load_every(0, 3, 4)
+        load_group(12)
+        load_group(13)
+        load_group(1)
         load_tokens("v", 1, 1, first_v, 1)
         load_tokens("k", 1, 1, first_k, 1)
-        load_head(1)
+        load_every(1, 0, 2)
+        load_every(1, 1, 2)
         load_tokens("v", 2, 3)
         load_tokens("k", 2, 3)
         late_loads = ["v", "k"]
 
+        banks_left = [x + odd for odd in range(2) for x in range(0, GROUPS, 4)]
+
+        def next_groups(count, engine=S):
+            for x in range(count):
+                mix_groups(1, banks_left.pop(0), 2, engine, 2)
+
         weights()
-        for j in range(N):
-            mix_term(j, 0, V if j == 0 else S)
-        for i in range(1, N):
-            for j in range(2):
-                mix_term(j, i)
+        turn_groups(0, 1, 16)
+        first_terms(0, V)
+        turn_groups(4, 2, 32)
+        first_terms(4, S)
+        later_terms(0)
         turn("v", 0, 0, S)
         turn("v", 0, 1, S)
-        mix_groups(0, 0)
-        mix_groups(0, 1)
-        mix_groups(0, 2)
-        mix_groups(0, 3)
-        rows_to_b(0)
+        mix_groups(0, 2, 2, S, 4)
+        mix_groups(0, 10, 2, S, 4)
+        turn_groups(8, 2, 32)
+        first_terms(8, S)
+        later_terms(4)
         turn("k", 0, 0, S)
         turn("k", 0, 1, S)
-        rows_to_b(1)
-        quantise("v", 0)
-        next_term()
-        b_to_state(0)
-        state_to_b(0)
+        mix_groups(0, 3, 2, S, 4)
+        mix_groups(0, 11, 2, S, 4)
+        turn_groups(12, 2, 24)
+        first_terms(12, S)
+        later_terms(8)
+        mix_group_and_half(1, 13)
+        later_terms(12)
         turn("v", 1, 0, S)
         turn("v", 1, 1, S)
-        state_to_a(0)
-        next_term()
-        quantise("b", 0)
+        ring.extend([6, 7])
         turn("k", 1, 0, S)
         turn("k", 1, 1, S)
+        next_groups(1)
+        ring.append(5)
+        state_to_b(0)
+        state_to_a(0, 0, [S])
+        state_to_a(0, 1, [S])
+        next_groups(3)
+        quantise("v", 0)
+        quantise("b", 0)
         quantise("k", 0)
-        next_term()
 
-        for n in range(PAIRS - 1):
-            helper = V if n > 0 else S
-            halves = n >= 6
-            halves_1 = n >= 5
-            early = n >= 5
+        for n in range(PAIRS):
+            m = n + 1
+            more = m < PAIRS
+            halves = n >= 7
             quantise("a", n)
-            if n == 1:
-                next_groups()
-                next_groups()
             if n > 1:
                 turn("k", n, 0, S)
-                turn("k", n, 1, S if n in (1, 4, 6) else V)
-            product(n, 0, 0, helper)
-            product(n, 0, 1, S)
-            if halves:
-                store(n, 0, 0, 2)
-            if n > 0:
-                quantise("k", n)
-            product(n, 0, 2, S)
-            if early:
-                product(n, 0, 3, S)
-                store(n, 0, 2 if halves else 0, 4)
-            if n > 0:
-                next_groups()
-            if n == 1:
-                next_groups()
-            if n + 1 < N:
-                b_to_state(n + 1)
-            state_to_b(n + 1)
-            if n > 0:
-                turn("v", n + 1, 0, S)
-                turn("v", n + 1, 1, S)
-            next_term()
-            if not early:
-                product(n, 0, 3, S)
-                store(n, 0, 2 if halves else 0, 4)
-            product(n, 1, 0, helper)
-            product(n, 1, 1, S)
-            if halves_1:
-                store(n, 1, 0, 2)
-            next_groups(helper)
-            if n == 0:
-                next_groups()
-            quantise("b", n + 1)
-            next_term()
-            quantise("v", n + 1)
-            if n < 7:
-                state_to_a(n + 1)
-            if n + 2 < N:
-                rows_to_b(n + 2)
-            product(n, 1, 2, S)
-            product(n, 1, 3, V)
-            next_term()
-            store(n, 1, 2 if halves_1 else 0, 4)
-            if n >= 7:
-                state_to_a(n + 1)
+                if not more:
+                    quantise("k", n, 0, 256)
+                turn("k", n, 1, S)
+            if more:
+                state_to_b(m)
+                if n > 0:
+                    quantise("k", n)
+            else:
+                quantise("k", n, 256, 512)
+            for b in range(4):
+                product(n, 0, b, V if b == 3 or (b == 1 and not more) else S)
+                if halves and b == 1:
+                    store(n, 0, 0, 2)
+            store(n, 0, 2 if halves else 0, 4)
+            if n < 3:
+                next_groups((2, 1, 0)[n])
+            if more:
+                if n > 0:
+                    turn("v", m, 0, S)
+                    turn("v", m, 1, S)
+                quantise("b", m)
+                state_to_a(m, 0, [S])
+                state_to_a(m, 1, [V, S])
+                quantise("v", m)
+            for b in range(4):
+                product(n, 1, b, V if b % 2 == 1 else S)
+                if n >= 6 and b == 1:
+                    store(n, 1, 0, 2)
+            store(n, 1, 2 if n >= 6 else 0, 4)
+            if n < 3:
+                next_groups((1, 0, 0)[n], S)
             if late_loads:
                 load_tokens(late_loads.pop(0), 5, 3)
-
-        n = PAIRS - 1
-        quantise("a", n)
-        for half in range(2):
-            turn("k", n, half, S)
-            if half == 1:
-                quantise("k", n, 0, 256)
-            product(n, 0, 2 * half, V)
-            product(n, 0, 2 * half + 1, S)
-            store(n, 0, 2 * half, 2 * half + 2)
-        quantise("k", n, 256, 512)
-        for half in range(2):
-            product(n, 1, 2 * half, S)
-            product(n, 1, 2 * half + 1, V)
-            store(n, 1, 2 * half, 2 * half + 2)

@@ -78,7 +78,7 @@ def tile_mhla_pa_v_kernel(tc, k_feat, v, w_piece, grad_out, out_0, out_1):
         spread = const.tile([P, N, 32], BF16, name="spread", align_bytes=64)
         w_all = const.tile([P, N * N], F32, name="w_all")
         mixer = const.tile([P, P], BF16, name="mixer", align_bytes=64)
-        sorter = const.tile([P, P], BF16, name="sorter", align_bytes=64)
+        sorter = const.tile([P, P], F32, name="sorter")
 
         def patterns():
             nc.sync.dma_start(out=w_rows[0:32, :], in_=w_piece.partition_broadcast(8))
@@ -127,27 +127,29 @@ def tile_mhla_pa_v_kernel(tc, k_feat, v, w_piece, grad_out, out_0, out_1):
         codes = {}
         results = {}
 
-        def turn_groups(x0, count, run):
-            bank = next_bank(BF16, BANKS - HELD + len(raw) % HELD)
-            view = bank[:, 0 : 512 * count].rearrange("p (i t u g y) -> p i t u g y", i=N, t=4, u=2, g=count)
+        def turn_groups(x0, count):
+            bank = next_bank(F32, BANKS - HELD + len(raw) % HELD)
+            view = bank[:, 0 : 256 * count].rearrange("p (i w u g y) -> p i w u g y", i=N, w=2, u=2, g=count)
             for g in range(count):
-                for t in range(4):
-                    nc.tensor.transpose(view[:, :, t, :, g, :], g_groups[0, x0 + g][:, t:512:4], sorter[:])
-            raw[x0] = (view.rearrange("p i t u g y -> p i (t u) (g y)")[:, :, :, 0:run], run)
+                words = g_groups[0, x0 + g].bitcast(F32)
+                for w in range(2):
+                    nc.tensor.transpose(view[:, :, w, :, g, :], words[:, w:256:2], sorter[:])
+            halves = bank[:, 0 : 256 * count].bitcast(BF16).rearrange("p (i c f) -> p i f c", i=N, f=2)
+            raw[x0] = (halves.rearrange("p i f (a y) -> p i f a y", a=4), 16 * count)
 
         def mix_term(x0, j, i, engine=V):
             terms, run = raw[x0]
             w_ij = w_all[:, N * j + i : N * j + i + 1]
             if i == 0:
                 sums[x0, j] = work.tile([P, 256], F32, name="acc", bufs=2 * N)
-            acc = sums[x0, j][:, 0 : 8 * run].rearrange("p (a c) -> p a c", a=8)
+            acc = sums[x0, j][:, 0 : 8 * run].rearrange("p (f a y) -> p f a y", f=2, a=4)
             if i == 0 and engine is V:
                 nc.vector.tensor_scalar(out=acc, in0=terms[:, i], scalar1=w_ij, scalar2=None, op0=MULT)
             elif i == 0:
                 nc.scalar.activation(out=acc, in_=terms[:, i], func=mybir.ActivationFunctionType.Copy, scale=w_ij)
             else:
-                window = state[0][:, 2048 * j : 2048 * (j + 1)].rearrange("p (a c) -> p a c", a=8)
-                dst = acc if i < N - 1 else window[:, :, 16 * x0 : 16 * x0 + run]
+                window = state[0][:, 2048 * j : 2048 * (j + 1)].rearrange("p (f a c) -> p f a c", f=2, a=4)
+                dst = acc if i < N - 1 else window[:, :, :, 16 * x0 : 16 * x0 + run]
                 nc.vector.scalar_tensor_tensor(out=dst, in0=terms[:, i], scalar=w_ij, in1=acc, op0=MULT, op1=ADD)
 
         def first_terms(x0, engine):
@@ -161,11 +163,12 @@ def tile_mhla_pa_v_kernel(tc, k_feat, v, w_piece, grad_out, out_0, out_1):
 
         def mix_groups(h, x0, count, engine=S, step=1):
             bank = next_bank(BF16)
-            view = bank[:, 0 : 512 * count].rearrange("p (g j t c) -> p g j t c", g=count, j=N, t=4)
+            view = bank[:, 0 : 512 * count].rearrange("p (g j f w c) -> p g j f w c", g=count, j=N, f=2, w=2)
             for g in range(count):
                 for t in range(4):
                     rows = g_groups[h, x0 + step * g]
-                    nc.tensor.matmul(view[:, g, :, t, :], lhsT=rows[:, t:512:4], rhs=mixer[:], start=True, stop=True)
+                    out = view[:, g, :, t % 2, t // 2, :]
+                    nc.tensor.matmul(out, lhsT=rows[:, t:512:4], rhs=mixer[:], start=True, stop=True)
             dst = state[h][:].bitcast(F32).rearrange("p (a x y) -> p a x y", x=GROUPS, y=8)
             copy(
                 engine,
@@ -173,24 +176,11 @@ def tile_mhla_pa_v_kernel(tc, k_feat, v, w_piece, grad_out, out_0, out_1):
                 bank[:, 0 : 512 * count].bitcast(F32).rearrange("p (g a y) -> p a g y", g=count, y=8),
             )
 
-        def mix_group_and_half(x, y):
-            bank = next_bank(BF16)
-            whole = bank[:, 0:512].rearrange("p (j t c) -> p j t c", j=N, t=4)
-            half = bank[:, 512:768].rearrange("p (j t u c) -> p j t u c", j=N, t=4, u=2)
-            upper = mixer[:].rearrange("p (j u c) -> p j u c", j=N, u=2)[:, :, :, 8:16]
-            for t in range(4):
-                nc.tensor.matmul(whole[:, :, t, :], lhsT=g_groups[0, x][:, t:512:4], rhs=mixer[:], start=True, stop=True)
-            for t in range(4):
-                nc.tensor.matmul(half[:, :, t, :, :], lhsT=g_groups[0, y][:, t:512:4], rhs=upper, start=True, stop=True)
-            dst = state[0][:].bitcast(F32).rearrange("p (a q) -> p a q", q=128)
-            copy(S, dst[:, :, 8 * x : 8 * x + 8], bank[:, 0:512].bitcast(F32).rearrange("p (a y) -> p a y", y=8))
-            copy(S, dst[:, :, 8 * y + 4 : 8 * y + 8], bank[:, 512:768].bitcast(F32).rearrange("p (a y) -> p a y", y=4))
-
         def state_to_b(n):
             h, j = divmod(n, N)
             b_in[n] = work.tile([P, 2048], BF16, name="b_in", align_bytes=64)
-            dst = b_in[n][:].rearrange("p (c i t) -> p c t i", i=4, t=4)
-            src = state[h][:, 2048 * j : 2048 * (j + 1)].rearrange("p (t c i) -> p c t i", t=4, i=4)
+            dst = b_in[n][:].rearrange("p (c i w f) -> p c w f i", i=4, w=2, f=2)
+            src = state[h][:, 2048 * j : 2048 * (j + 1)].rearrange("p (f w c i) -> p c w f i", f=2, w=2, i=4)
             nc.vector.tensor_copy(out=dst, in_=src)
 
         def state_to_a(n, half, engines):
@@ -269,7 +259,11 @@ def tile_mhla_pa_v_kernel(tc, k_feat, v, w_piece, grad_out, out_0, out_1):
                     bank[:].rearrange("m (u q e) -> m q u e", u=2, e=2),
                 )
             else:
-                copy(engine, res.rearrange("m (p t) -> m p t", t=4), bank[:].rearrange("m (t p) -> m p t", t=4))
+                copy(
+                    engine,
+                    res.rearrange("m (p w f) -> m p w f", w=2, f=2),
+                    bank[:].rearrange("m (f w p) -> m p w f", f=2, w=2),
+                )
 
         def store(n, which, b0, b1):
             h, j = divmod(n, N)
@@ -295,7 +289,7 @@ def tile_mhla_pa_v_kernel(tc, k_feat, v, w_piece, grad_out, out_0, out_1):
         load_every(1, 1, 2)
         load_tokens("v", 2, 3)
         load_tokens("k", 2, 3)
-        late_loads = ["v", "k"]
+        late_loads = ["k"]
 
         banks_left = [x + odd for odd in range(2) for x in range(0, GROUPS, 4)]
 
@@ -304,33 +298,34 @@ def tile_mhla_pa_v_kernel(tc, k_feat, v, w_piece, grad_out, out_0, out_1):
                 mix_groups(1, banks_left.pop(0), 2, engine, 2)
 
         weights()
-        turn_groups(0, 1, 16)
+        turn_groups(0, 1)
         first_terms(0, V)
-        turn_groups(4, 2, 32)
+        turn_groups(4, 2)
         first_terms(4, S)
         later_terms(0)
         turn("v", 0, 0, S)
         turn("v", 0, 1, S)
         mix_groups(0, 2, 2, S, 4)
-        mix_groups(0, 10, 2, S, 4)
-        turn_groups(8, 2, 32)
+        turn_groups(8, 2)
         first_terms(8, S)
+        mix_groups(0, 10, 2, S, 4)
         later_terms(4)
         turn("k", 0, 0, S)
         turn("k", 0, 1, S)
         mix_groups(0, 3, 2, S, 4)
         mix_groups(0, 11, 2, S, 4)
-        turn_groups(12, 2, 24)
+        turn_groups(12, 2)
         first_terms(12, S)
         later_terms(8)
-        mix_group_and_half(1, 13)
+        mix_groups(0, 1, 1)
         later_terms(12)
         turn("v", 1, 0, S)
         turn("v", 1, 1, S)
+        load_tokens("v", 5, 3)
         ring.extend([6, 7])
         turn("k", 1, 0, S)
         turn("k", 1, 1, S)
-        next_groups(1)
+        next_groups(2)
         ring.append(5)
         state_to_b(0)
         state_to_a(0, 0, [S])
@@ -340,43 +335,61 @@ def tile_mhla_pa_v_kernel(tc, k_feat, v, w_piece, grad_out, out_0, out_1):
         quantise("b", 0)
         quantise("k", 0)
 
-        for n in range(PAIRS):
+        for n in range(PAIRS - 1):
             m = n + 1
-            more = m < PAIRS
-            halves = n >= 7
+            halves = n >= 6
+            halves_1 = n >= 5
+            early = n >= 5
             quantise("a", n)
             if n > 1:
                 turn("k", n, 0, S)
-                if not more:
-                    quantise("k", n, 0, 256)
-                turn("k", n, 1, S)
-            if more:
-                state_to_b(m)
-                if n > 0:
-                    quantise("k", n)
-            else:
-                quantise("k", n, 256, 512)
-            for b in range(4):
-                product(n, 0, b, V if b == 3 or (b == 1 and not more) else S)
-                if halves and b == 1:
-                    store(n, 0, 0, 2)
-            store(n, 0, 2 if halves else 0, 4)
+                turn("k", n, 1, S if n in (4, 6) else V)
+            product(n, 0, 0, V)
+            product(n, 0, 1, S)
+            if halves:
+                store(n, 0, 0, 2)
+            if n > 0:
+                quantise("k", n)
+            product(n, 0, 2, S)
+            if early:
+                product(n, 0, 3, S)
+                store(n, 0, 2 if halves else 0, 4)
             if n < 3:
-                next_groups((2, 1, 0)[n])
-            if more:
-                if n > 0:
-                    turn("v", m, 0, S)
-                    turn("v", m, 1, S)
-                quantise("b", m)
-                state_to_a(m, 0, [S])
-                state_to_a(m, 1, [V, S])
-                quantise("v", m)
-            for b in range(4):
-                product(n, 1, b, V if b % 2 == 1 else S)
-                if n >= 6 and b == 1:
-                    store(n, 1, 0, 2)
-            store(n, 1, 2 if n >= 6 else 0, 4)
+                next_groups((1, 1, 0)[n])
+            state_to_b(m)
+            if n > 0:
+                turn("v", m, 0, S)
+                turn("v", m, 1, S)
+            if not early:
+                product(n, 0, 3, S)
+                store(n, 0, 0, 4)
+            product(n, 1, 0, V)
+            product(n, 1, 1, S)
+            if halves_1:
+                store(n, 1, 0, 2)
             if n < 3:
-                next_groups((1, 0, 0)[n], S)
+                next_groups((1, 0, 0)[n])
+            quantise("b", m)
+            quantise("v", m)
+            state_to_a(m, 0, [S])
+            state_to_a(m, 1, [S])
+            product(n, 1, 2, S)
+            product(n, 1, 3, V)
+            store(n, 1, 2 if halves_1 else 0, 4)
             if late_loads:
                 load_tokens(late_loads.pop(0), 5, 3)
+
+        n = PAIRS - 1
+        quantise("a", n)
+        for half in range(2):
+            turn("k", n, half, S)
+            if half == 1:
+                quantise("k", n, 0, 256)
+            product(n, 0, 2 * half, V)
+            product(n, 0, 2 * half + 1, S)
+            store(n, 0, 2 * half, 2 * half + 2)
+        quantise("k", n, 256, 512)
+        for half in range(2):
+            product(n, 1, 2 * half, S)
+            product(n, 1, 2 * half + 1, V)
+            store(n, 1, 2 * half, 2 * half + 2)

@@ -18,6 +18,7 @@ PAIRS = H * N
 FLOPS = 2 * 2 * PAIRS * W * D * D
 BANKS = 8
 HELD = 3
+QUADS = 52
 GROUPS = 16
 RAW_WINDOWS = 3
 RESULT_BUFS = 3
@@ -49,6 +50,7 @@ def tile_mhla_pa_v_kernel(tc, k_feat, v, w_piece, grad_out, out_0, out_1):
 
         tokens = {}
         g_groups = {}
+        g_rows = {}
 
         def load_tokens(which, n, windows, tile=None, place=0):
             if tile is None:
@@ -60,10 +62,20 @@ def tile_mhla_pa_v_kernel(tc, k_feat, v, w_piece, grad_out, out_0, out_1):
             nc.sync.dma_start(out=dst, in_=src[:, n : n + windows, :])
             return tile
 
-        def load_group(x):
-            tile = keep.tile([P, 512], BF16, name="g_one%d" % x, align_bytes=256)
-            g_groups[0, x] = tile[:, :]
-            nc.sync.dma_start(out=tile[:], in_=grad_out[0, 0, :, 32 * x : 32 * x + 32, :].rearrange("i r d -> r i d"))
+        def load_rows(i0, windows):
+            tile = keep.tile([P, 1024 * windows], BF16, name="g_rows%d" % i0, align_bytes=256)
+            for w in range(windows):
+                g_rows[i0 + w] = tile[:, 1024 * w : 1024 * (w + 1)]
+            src = grad_out[0, 0, i0 : i0 + windows, 256:512, :].rearrange("i (r e) d -> r i (e d)", e=2)
+            nc.sync.dma_start(out=tile[:].rearrange("p (w c) -> p w c", w=windows), in_=src)
+
+        def load_groups(x0, x1):
+            tile = keep.tile([P, x1 - x0, 512], BF16, name="g_mix%d" % x0, align_bytes=256)
+            for x in range(x0, x1):
+                g_groups[0, x] = tile[:, x - x0, :]
+            for i in range(N):
+                src = grad_out[0, 0, i].rearrange("(x r) d -> r x d", r=32)
+                nc.sync.dma_start(out=tile[i:P:4, :, :], in_=src[:, x0:x1, :])
 
         def load_every(h, x0, step):
             tile = keep.tile([P, GROUPS // step, 512], BF16, name="g_every%d_%d" % (h, x0), align_bytes=256)
@@ -86,9 +98,10 @@ def tile_mhla_pa_v_kernel(tc, k_feat, v, w_piece, grad_out, out_0, out_1):
             nc.gpsimd.memset(w_rows[64:P, :], 0.0)
             make_identity(nc, ident[:])
             nc.vector.tensor_copy(
-                out=sorter[:].rearrange("p (i u q e) -> p i u q e", i=N, u=2, e=2),
-                in_=ident[:].rearrange("p (q u e i) -> p i u q e", u=2, e=2, i=N),
+                out=sorter[:, 0 : 2 * QUADS].rearrange("p (u q) -> p u q", u=2),
+                in_=ident[:, P - 2 * QUADS : P].rearrange("p (q u) -> p u q", u=2),
             )
+            nc.vector.tensor_copy(out=sorter[:, 2 * QUADS : P], in_=ident[:, 0 : P - 2 * QUADS])
             nc.scalar.copy(out=spread[:], in_=ident[:, 0:32].unsqueeze(1).to_broadcast([P, N, 32]))
             nc.vector.tensor_reduce(
                 out=eye[:].rearrange("p (u q e) -> p q u e", u=2, e=2),
@@ -127,39 +140,50 @@ def tile_mhla_pa_v_kernel(tc, k_feat, v, w_piece, grad_out, out_0, out_1):
         codes = {}
         results = {}
 
-        def turn_groups(x0, count):
+        def turn_rows(i, w0, w1):
             bank = next_bank(F32, BANKS - HELD + len(raw) % HELD)
-            view = bank[:, 0 : 256 * count].rearrange("p (i w u g y) -> p i w u g y", i=N, w=2, u=2, g=count)
-            for g in range(count):
-                words = g_groups[0, x0 + g].bitcast(F32)
-                for w in range(2):
-                    nc.tensor.transpose(view[:, :, w, :, g, :], words[:, w:256:2], sorter[:])
-            halves = bank[:, 0 : 256 * count].bitcast(BF16).rearrange("p (i c f) -> p i f c", i=N, f=2)
-            raw[x0] = (halves.rearrange("p i f (a y) -> p i f a y", a=4), 16 * count)
+            words = g_rows[i].bitcast(F32)
+            run = 2 * QUADS
+            for e in range(2):
+                for w in range(w0, w1):
+                    c0 = 256 * e + run * (w - w0)
+                    nc.tensor.transpose(bank[:, c0 : c0 + P], words[:, 256 * e + w : 256 * (e + 1) : 2], sorter[:])
+            view = bank[:].bitcast(BF16).rearrange("p (e c) -> p e c", e=2)[:, :, 0 : 2 * run * (w1 - w0)]
+            raw[i, w0] = (view.rearrange("p e (a q f) -> p f a q e", q=QUADS, f=2), w1)
 
-        def mix_term(x0, j, i, engine=V):
-            terms, run = raw[x0]
+        def mix_term(j, i, w0=0, engine=V):
+            term, w1 = raw[i, w0]
             w_ij = w_all[:, N * j + i : N * j + i + 1]
-            if i == 0:
-                sums[x0, j] = work.tile([P, 256], F32, name="acc", bufs=2 * N)
-            acc = sums[x0, j][:, 0 : 8 * run].rearrange("p (f a y) -> p f a y", f=2, a=4)
-            if i == 0 and engine is V:
-                nc.vector.tensor_scalar(out=acc, in0=terms[:, i], scalar1=w_ij, scalar2=None, op0=MULT)
-            elif i == 0:
-                nc.scalar.activation(out=acc, in_=terms[:, i], func=mybir.ActivationFunctionType.Copy, scale=w_ij)
-            else:
-                window = state[0][:, 2048 * j : 2048 * (j + 1)].rearrange("p (f a c) -> p f a c", f=2, a=4)
-                dst = acc if i < N - 1 else window[:, :, :, 16 * x0 : 16 * x0 + run]
-                nc.vector.scalar_tensor_tensor(out=dst, in0=terms[:, i], scalar=w_ij, in1=acc, op0=MULT, op1=ADD)
+            if j not in sums:
+                sums[j] = work.tile([P, 16 * QUADS], F32, name="acc", bufs=N)
+            acc = sums[j][:].rearrange("p (f a q e) -> p f a q e", f=2, a=4, e=2)[:, :, 2 * w0 : 2 * w1]
+            if engine is S:
+                nc.scalar.activation(out=acc, in_=term, func=mybir.ActivationFunctionType.Copy, scale=w_ij)
+                return
+            window = state[0][:, 2048 * j : 2048 * (j + 1)].rearrange("p (f a q e) -> p f a q e", f=2, a=4, e=2)
+            dst = acc if i < N - 1 else window[:, :, :, P - QUADS : P, :]
+            for f in range(2):
+                if i == 0:
+                    nc.vector.tensor_scalar(out=acc[:, f], in0=term[:, f], scalar1=w_ij, scalar2=None, op0=MULT)
+                else:
+                    nc.vector.scalar_tensor_tensor(
+                        out=dst[:, f], in0=term[:, f], scalar=w_ij, in1=acc[:, f], op0=MULT, op1=ADD
+                    )
 
-        def first_terms(x0, engine):
-            for j in range(N):
-                mix_term(x0, j, 0, engine)
-
-        def later_terms(x0):
-            for i in range(1, N):
-                for j in range(N):
-                    mix_term(x0, j, i)
+        def mix_group_and_half(x):
+            bank = next_bank(BF16)
+            whole = bank[:, 0:512].rearrange("p (j t c) -> p j t c", j=N, t=4)
+            half = bank[:, 512:768].rearrange("p (j t u c) -> p j t u c", j=N, t=4, u=2)
+            lower = mixer[:].rearrange("p (j u c) -> p j u c", j=N, u=2)[:, :, :, 0:8]
+            for t in range(4):
+                out = whole[:, :, 2 * (t % 2) + t // 2, :]
+                nc.tensor.matmul(out, lhsT=g_groups[0, x][:, t:512:4], rhs=mixer[:], start=True, stop=True)
+            for t in range(4):
+                out = half[:, :, 2 * (t % 2) + t // 2, :, :]
+                nc.tensor.matmul(out, lhsT=g_groups[0, x + 1][:, t:512:4], rhs=lower, start=True, stop=True)
+            dst = state[0][:].bitcast(F32).rearrange("p (a q) -> p a q", q=128)
+            copy(S, dst[:, :, 8 * x : 8 * x + 8], bank[:, 0:512].bitcast(F32).rearrange("p (a y) -> p a y", y=8))
+            copy(S, dst[:, :, 8 * x + 8 : 8 * x + 12], bank[:, 512:768].bitcast(F32).rearrange("p (a y) -> p a y", y=4))
 
         def mix_groups(h, x0, count, engine=S, step=1):
             bank = next_bank(BF16)
@@ -271,18 +295,13 @@ def tile_mhla_pa_v_kernel(tc, k_feat, v, w_piece, grad_out, out_0, out_1):
             nc.sync.dma_start(out=view[:, b0:b1, :], in_=results[which][:, b0:b1, :])
 
         patterns()
-        load_group(0)
-        load_group(4)
-        load_group(5)
+        load_rows(0, 1)
+        load_rows(1, 1)
         first_v = load_tokens("v", 0, 1)
-        load_every(0, 2, 4)
-        load_group(8)
-        load_group(9)
+        load_groups(0, 4)
+        load_rows(2, 2)
         first_k = load_tokens("k", 0, 1)
-        load_every(0, 3, 4)
-        load_group(12)
-        load_group(13)
-        load_group(1)
+        load_groups(4, 10)
         load_tokens("v", 1, 1, first_v, 1)
         load_tokens("k", 1, 1, first_k, 1)
         load_every(1, 0, 2)
@@ -298,42 +317,49 @@ def tile_mhla_pa_v_kernel(tc, k_feat, v, w_piece, grad_out, out_0, out_1):
                 mix_groups(1, banks_left.pop(0), 2, engine, 2)
 
         weights()
-        turn_groups(0, 1)
-        first_terms(0, V)
-        turn_groups(4, 2)
-        first_terms(4, S)
-        later_terms(0)
+        turn_rows(0, 0, 1)
+        turn_rows(0, 1, 2)
+        turn_rows(1, 0, 2)
+        for j in range(2):
+            mix_term(j, 0, 0, V)
+        for j in range(N):
+            mix_term(j, 0, 1, S)
+        for j in range(2, N):
+            mix_term(j, 0, 0, S)
         turn("v", 0, 0, S)
         turn("v", 0, 1, S)
-        mix_groups(0, 2, 2, S, 4)
-        turn_groups(8, 2)
-        first_terms(8, S)
-        mix_groups(0, 10, 2, S, 4)
-        later_terms(4)
+        mix_groups(0, 0, 2)
+        turn_rows(2, 0, 2)
+        turn_rows(3, 0, 2)
+        mix_groups(0, 2, 2)
+        for j in range(N):
+            mix_term(j, 1)
         turn("k", 0, 0, S)
         turn("k", 0, 1, S)
-        mix_groups(0, 3, 2, S, 4)
-        mix_groups(0, 11, 2, S, 4)
-        turn_groups(12, 2)
-        first_terms(12, S)
-        later_terms(8)
-        mix_groups(0, 1, 1)
-        later_terms(12)
+        mix_groups(0, 4, 2)
+        mix_groups(0, 6, 2)
+        mix_group_and_half(8)
+        for j in range(N):
+            mix_term(j, 2)
         turn("v", 1, 0, S)
         turn("v", 1, 1, S)
         load_tokens("v", 5, 3)
-        ring.extend([6, 7])
+        ring.extend([5, 7])
         turn("k", 1, 0, S)
         turn("k", 1, 1, S)
-        next_groups(2)
-        ring.append(5)
-        state_to_b(0)
+        next_groups(0)
+        mix_term(0, 3)
+        mix_term(1, 3)
         state_to_a(0, 0, [S])
         state_to_a(0, 1, [S])
-        next_groups(3)
+        state_to_b(0)
         quantise("v", 0)
         quantise("b", 0)
+        next_groups(4)
+        mix_term(2, 3)
         quantise("k", 0)
+        mix_term(3, 3)
+        ring.append(6)
 
         for n in range(PAIRS - 1):
             m = n + 1
@@ -355,7 +381,7 @@ def tile_mhla_pa_v_kernel(tc, k_feat, v, w_piece, grad_out, out_0, out_1):
                 product(n, 0, 3, S)
                 store(n, 0, 2 if halves else 0, 4)
             if n < 3:
-                next_groups((1, 1, 0)[n])
+                next_groups((2, 1, 0)[n])
             state_to_b(m)
             if n > 0:
                 turn("v", m, 0, S)

@@ -20,8 +20,7 @@ BANKS = 8
 HELD = 3
 QUADS = 52
 GROUPS = 16
-RAW_WINDOWS = 3
-RESULT_BUFS = 3
+STORED_IN_TWOS = 2
 
 
 def tile_mhla_pa_v_kernel(tc, k_feat, v, w_piece, grad_out, out_0, out_1):
@@ -52,15 +51,14 @@ def tile_mhla_pa_v_kernel(tc, k_feat, v, w_piece, grad_out, out_0, out_1):
         g_groups = {}
         g_rows = {}
 
-        def load_tokens(which, n, windows, tile=None, place=0):
-            if tile is None:
-                tile = keep.tile([P, 2048 * RAW_WINDOWS], BF16, name="raw_" + which, bufs=2, align_bytes=256)
+        def room(name, windows):
+            return keep.tile([P, 2048 * windows], BF16, name=name, align_bytes=256)[:]
+
+        def load_tokens(which, n, windows, tile):
             for w in range(windows):
-                tokens[which, n + w] = tile[:, 2048 * (place + w) : 2048 * (place + w + 1)]
+                tokens[which, n + w] = tile[:, 2048 * w : 2048 * (w + 1)]
             src = (k_feat if which == "k" else v)[0].rearrange("h j (m b) d -> m (h j) (b d)", b=4)
-            dst = tile[:, 2048 * place : 2048 * (place + windows)].rearrange("p (w c) -> p w c", w=windows)
-            nc.sync.dma_start(out=dst, in_=src[:, n : n + windows, :])
-            return tile
+            nc.sync.dma_start(out=tile.rearrange("p (w c) -> p w c", w=windows), in_=src[:, n : n + windows, :])
 
         def load_rows(i0, windows):
             tile = keep.tile([P, 1024 * windows], BF16, name="g_rows%d" % i0, align_bytes=256)
@@ -133,7 +131,7 @@ def tile_mhla_pa_v_kernel(tc, k_feat, v, w_piece, grad_out, out_0, out_1):
 
         state = [keep.tile([P, N * 2048], BF16, name="mixed%d" % h, align_bytes=64) for h in range(H)]
         raw = {}
-        sums = {}
+        sums = work.tile([P, N * 16 * QUADS], F32, name="res1", align_bytes=256)
         b_in = {}
         a_in = {}
         turned = {}
@@ -154,9 +152,7 @@ def tile_mhla_pa_v_kernel(tc, k_feat, v, w_piece, grad_out, out_0, out_1):
         def mix_term(j, i, w0=0, engine=V):
             term, w1 = raw[i, w0]
             w_ij = w_all[:, N * j + i : N * j + i + 1]
-            if j not in sums:
-                sums[j] = work.tile([P, 16 * QUADS], F32, name="acc", bufs=N)
-            acc = sums[j][:].rearrange("p (f a q e) -> p f a q e", f=2, a=4, e=2)[:, :, 2 * w0 : 2 * w1]
+            acc = sums[:, 16 * QUADS * j : 16 * QUADS * (j + 1)].rearrange("p (f a q e) -> p f a q e", f=2, a=4, e=2)[:, :, 2 * w0 : 2 * w1]
             if engine is S:
                 nc.scalar.activation(out=acc, in_=term, func=mybir.ActivationFunctionType.Copy, scale=w_ij)
                 return
@@ -262,8 +258,8 @@ def tile_mhla_pa_v_kernel(tc, k_feat, v, w_piece, grad_out, out_0, out_1):
             left, right = ("v", "b") if which == 0 else ("k", "a")
             lc, ls = codes[left, n]
             rc, rs = codes[right, n]
-            if b == 0:
-                results[which] = work.tile([P, 4, 512], F32, name="res%d" % which, bufs=RESULT_BUFS, align_bytes=256)
+            if b == 0 and n % 2 == 0:
+                results[which] = work.tile([P, 4096], F32, name="res%d" % which, align_bytes=256)
             bank = next_bank(F32)
             cols = slice(128 * b, 128 * b + 128)
             nc.tensor.matmul_mx(
@@ -275,7 +271,7 @@ def tile_mhla_pa_v_kernel(tc, k_feat, v, w_piece, grad_out, out_0, out_1):
                 start=True,
                 stop=True,
             )
-            res = results[which][:, b, :]
+            res = results[which][:, 2048 * (n % 2) + 512 * b : 2048 * (n % 2) + 512 * (b + 1)]
             if which == 0:
                 copy(
                     engine,
@@ -291,24 +287,22 @@ def tile_mhla_pa_v_kernel(tc, k_feat, v, w_piece, grad_out, out_0, out_1):
 
         def store(n, which, b0, b1):
             h, j = divmod(n, N)
-            view = (out_0 if which == 0 else out_1)[0, h, j].rearrange("(m b) d -> m b d", b=4)
-            nc.sync.dma_start(out=view[:, b0:b1, :], in_=results[which][:, b0:b1, :])
+            out = (out_0 if which == 0 else out_1)[0, h].rearrange("j (m b) d -> m j (b d)", b=4)
+            held = results[which][:].rearrange("m (j c) -> m j c", j=2)
+            if n >= STORED_IN_TWOS:
+                nc.sync.dma_start(out=out[:, j, 512 * b0 : 512 * b1], in_=held[:, n % 2, 512 * b0 : 512 * b1])
+            elif n % 2 == 1:
+                nc.sync.dma_start(out=out[:, j - 1 : j + 1, :], in_=held)
 
         patterns()
         load_rows(0, 1)
         load_rows(1, 1)
-        first_v = load_tokens("v", 0, 1)
+        first = room("first", 3)
+        load_tokens("v", 0, 1, first[:, 0:2048])
         load_groups(0, 4)
         load_rows(2, 2)
-        first_k = load_tokens("k", 0, 1)
+        load_tokens("k", 0, 1, first[:, 2048:4096])
         load_groups(4, 10)
-        load_tokens("v", 1, 1, first_v, 1)
-        load_tokens("k", 1, 1, first_k, 1)
-        load_every(1, 0, 2)
-        load_every(1, 1, 2)
-        load_tokens("v", 2, 3)
-        load_tokens("k", 2, 3)
-        late_loads = ["k"]
 
         banks_left = [x + odd for odd in range(2) for x in range(0, GROUPS, 4)]
 
@@ -332,6 +326,12 @@ def tile_mhla_pa_v_kernel(tc, k_feat, v, w_piece, grad_out, out_0, out_1):
         turn_rows(2, 0, 2)
         turn_rows(3, 0, 2)
         mix_groups(0, 2, 2)
+        load_tokens("v", 1, 1, first[:, 4096:6144])
+        load_every(1, 0, 2)
+        load_tokens("k", 1, 1, room("g_mix0", 1))
+        load_every(1, 1, 2)
+        load_tokens("v", 2, 6, room("v_rest", 6))
+        load_tokens("k", 2, 3, room("k_middle", 3))
         for j in range(N):
             mix_term(j, 1)
         turn("k", 0, 0, S)
@@ -343,19 +343,19 @@ def tile_mhla_pa_v_kernel(tc, k_feat, v, w_piece, grad_out, out_0, out_1):
             mix_term(j, 2)
         turn("v", 1, 0, S)
         turn("v", 1, 1, S)
-        load_tokens("v", 5, 3)
+        load_tokens("k", 5, 3, room("first", 3))
         ring.extend([5, 7])
-        turn("k", 1, 0, S)
-        turn("k", 1, 1, S)
-        next_groups(0)
         mix_term(0, 3)
         mix_term(1, 3)
         state_to_a(0, 0, [S])
         state_to_a(0, 1, [S])
         state_to_b(0)
+        next_groups(2)
+        turn("k", 1, 0, S)
+        turn("k", 1, 1, S)
         quantise("v", 0)
         quantise("b", 0)
-        next_groups(4)
+        next_groups(2)
         mix_term(2, 3)
         quantise("k", 0)
         mix_term(3, 3)
@@ -364,7 +364,7 @@ def tile_mhla_pa_v_kernel(tc, k_feat, v, w_piece, grad_out, out_0, out_1):
         for n in range(PAIRS - 1):
             m = n + 1
             halves = n >= 6
-            halves_1 = n >= 5
+            halves_1 = n >= 6
             early = n >= 5
             quantise("a", n)
             if n > 1:
@@ -402,8 +402,6 @@ def tile_mhla_pa_v_kernel(tc, k_feat, v, w_piece, grad_out, out_0, out_1):
             product(n, 1, 2, S)
             product(n, 1, 3, V)
             store(n, 1, 2 if halves_1 else 0, 4)
-            if late_loads:
-                load_tokens(late_loads.pop(0), 5, 3)
 
         n = PAIRS - 1
         quantise("a", n)

@@ -17,8 +17,8 @@ P = 128
 PAIRS = H * N
 FLOPS = 2 * 2 * PAIRS * W * D * D
 BANKS = 8
-HELD = 3
-QUADS = 52
+HELD = 5
+QUADS = 48
 GROUPS = 16
 STORED_IN_TWOS = 2
 
@@ -131,15 +131,17 @@ def tile_mhla_pa_v_kernel(tc, k_feat, v, w_piece, grad_out, out_0, out_1):
 
         state = [keep.tile([P, N * 2048], BF16, name="mixed%d" % h, align_bytes=64) for h in range(H)]
         raw = {}
-        sums = work.tile([P, N * 16 * QUADS], F32, name="res1", align_bytes=256)
+        sums = work.tile([P, (N - 1) * 16 * QUADS], F32, name="res1", align_bytes=256)
+        terms = work.tile([P, N * 1024], F32, name="res0", align_bytes=256)
+        pool_rows = keep.tile([P, 1024], BF16, name="pool_rows", align_bytes=64)
         b_in = {}
         a_in = {}
         turned = {}
         codes = {}
         results = {}
 
-        def turn_rows(i, w0, w1):
-            bank = next_bank(F32, BANKS - HELD + len(raw) % HELD)
+        def turn_rows(i, w0, w1, slot):
+            bank = next_bank(F32, slot)
             words = g_rows[i].bitcast(F32)
             run = 2 * QUADS
             for e in range(2):
@@ -166,34 +168,46 @@ def tile_mhla_pa_v_kernel(tc, k_feat, v, w_piece, grad_out, out_0, out_1):
                         out=dst[:, f], in0=term[:, f], scalar=w_ij, in1=acc[:, f], op0=MULT, op1=ADD
                     )
 
-        def mix_group_and_half(x):
-            bank = next_bank(BF16)
-            whole = bank[:, 0:512].rearrange("p (j t c) -> p j t c", j=N, t=4)
-            half = bank[:, 512:768].rearrange("p (j t u c) -> p j t u c", j=N, t=4, u=2)
-            lower = mixer[:].rearrange("p (j u c) -> p j u c", j=N, u=2)[:, :, :, 0:8]
-            for t in range(4):
-                out = whole[:, :, 2 * (t % 2) + t // 2, :]
-                nc.tensor.matmul(out, lhsT=g_groups[0, x][:, t:512:4], rhs=mixer[:], start=True, stop=True)
-            for t in range(4):
-                out = half[:, :, 2 * (t % 2) + t // 2, :, :]
-                nc.tensor.matmul(out, lhsT=g_groups[0, x + 1][:, t:512:4], rhs=lower, start=True, stop=True)
-            dst = state[0][:].bitcast(F32).rearrange("p (a q) -> p a q", q=128)
-            copy(S, dst[:, :, 8 * x : 8 * x + 8], bank[:, 0:512].bitcast(F32).rearrange("p (a y) -> p a y", y=8))
-            copy(S, dst[:, :, 8 * x + 8 : 8 * x + 12], bank[:, 512:768].bitcast(F32).rearrange("p (a y) -> p a y", y=4))
+        def pool_product(i, engine=None):
+            w_ij = w_all[:, N * (N - 1) + i : N * (N - 1) + i + 1]
+            out = terms[:, 1024 * i : 1024 * (i + 1)]
+            if engine is S:
+                nc.scalar.activation(out=out, in_=g_rows[i], func=mybir.ActivationFunctionType.Copy, scale=w_ij)
+            else:
+                nc.vector.tensor_scalar(out=out, in0=g_rows[i], scalar1=w_ij, scalar2=None, op0=MULT)
 
-        def mix_groups(h, x0, count, engine=S, step=1):
+        def pool_add(a, b, last=False):
+            for c0 in range(0, 1024, 512):
+                acc = terms[:, 1024 * a + c0 : 1024 * a + c0 + 512]
+                out = pool_rows[:, c0 : c0 + 512] if last else acc
+                nc.gpsimd.tensor_tensor(out=out, in0=acc, in1=terms[:, 1024 * b + c0 : 1024 * b + c0 + 512], op=ADD)
+
+        def pool_rows_to_state(engines):
+            bank = next_bank(F32)
+            words = pool_rows[:].bitcast(F32)
+            for e in range(2):
+                for w in range(2):
+                    c0 = 256 * e + 128 * w
+                    nc.tensor.transpose(bank[:, c0 : c0 + P], words[:, 256 * e + w : 256 * (e + 1) : 2], ident[:])
+            src = bank[:].bitcast(BF16).rearrange("p (e w q u f) -> p w f u q e", e=2, w=2, u=2, f=2)
+            dst = state[0][:, 2048 * (N - 1) : 2048 * N].rearrange("p (f w u q e) -> p w f u q e", f=2, w=2, u=2, e=2)
+            for w in range(2):
+                copy(engines[w], dst[:, w, :, :, 64:P, :], src[:, w])
+
+        def mix_groups(h, x0, count, engine=S, step=1, windows=N):
             bank = next_bank(BF16)
-            view = bank[:, 0 : 512 * count].rearrange("p (g j f w c) -> p g j f w c", g=count, j=N, f=2, w=2)
+            used = bank[:, 0 : 128 * windows * count]
+            view = used.rearrange("p (g j f w c) -> p g j f w c", g=count, j=windows, f=2, w=2)
             for g in range(count):
                 for t in range(4):
                     rows = g_groups[h, x0 + step * g]
                     out = view[:, g, :, t % 2, t // 2, :]
-                    nc.tensor.matmul(out, lhsT=rows[:, t:512:4], rhs=mixer[:], start=True, stop=True)
+                    nc.tensor.matmul(out, lhsT=rows[:, t:512:4], rhs=mixer[:, 0 : 32 * windows], start=True, stop=True)
             dst = state[h][:].bitcast(F32).rearrange("p (a x y) -> p a x y", x=GROUPS, y=8)
             copy(
                 engine,
-                dst[:, :, x0 : x0 + step * (count - 1) + 1 : step, :],
-                bank[:, 0 : 512 * count].bitcast(F32).rearrange("p (g a y) -> p a g y", g=count, y=8),
+                dst[:, 0 : 8 * windows, x0 : x0 + step * (count - 1) + 1 : step, :],
+                used.bitcast(F32).rearrange("p (g a y) -> p a g y", g=count, y=8),
             )
 
         def state_to_b(n):
@@ -298,11 +312,13 @@ def tile_mhla_pa_v_kernel(tc, k_feat, v, w_piece, grad_out, out_0, out_1):
         load_rows(0, 1)
         load_rows(1, 1)
         first = room("first", 3)
-        load_tokens("v", 0, 1, first[:, 0:2048])
-        load_groups(0, 4)
         load_rows(2, 2)
-        load_tokens("k", 0, 1, first[:, 2048:4096])
+        load_groups(0, 4)
+        load_tokens("v", 0, 1, first[:, 0:2048])
         load_groups(4, 10)
+        load_tokens("k", 0, 1, first[:, 2048:4096])
+        load_every(1, 0, 2)
+        load_tokens("v", 1, 1, first[:, 4096:6144])
 
         banks_left = [x + odd for odd in range(2) for x in range(0, GROUPS, 4)]
 
@@ -311,55 +327,57 @@ def tile_mhla_pa_v_kernel(tc, k_feat, v, w_piece, grad_out, out_0, out_1):
                 mix_groups(1, banks_left.pop(0), 2, engine, 2)
 
         weights()
-        turn_rows(0, 0, 1)
-        turn_rows(0, 1, 2)
-        turn_rows(1, 0, 2)
-        for j in range(2):
+        turn_rows(0, 0, 1, 3)
+        turn_rows(0, 1, 2, 4)
+        turn_rows(1, 0, 2, 5)
+        turn_rows(2, 0, 2, 6)
+        turn_rows(3, 0, 2, 7)
+        pool_product(0)
+        pool_product(1, S)
+        for j in range(N - 1):
             mix_term(j, 0, 0, V)
-        for j in range(N):
+        for j in range(N - 1):
             mix_term(j, 0, 1, S)
-        for j in range(2, N):
-            mix_term(j, 0, 0, S)
-        turn("v", 0, 0, S)
-        turn("v", 0, 1, S)
+        ring.extend([3, 4])
+        pool_add(0, 1)
+        pool_product(2, S)
+        pool_product(3, S)
+        pool_add(0, 2)
+        pool_add(0, 3, True)
         mix_groups(0, 0, 2)
-        turn_rows(2, 0, 2)
-        turn_rows(3, 0, 2)
         mix_groups(0, 2, 2)
-        load_tokens("v", 1, 1, first[:, 4096:6144])
-        load_every(1, 0, 2)
         load_tokens("k", 1, 1, room("g_mix0", 1))
         load_every(1, 1, 2)
         load_tokens("v", 2, 6, room("v_rest", 6))
         load_tokens("k", 2, 3, room("k_middle", 3))
-        for j in range(N):
+        for j in range(N - 1):
             mix_term(j, 1)
-        turn("k", 0, 0, S)
-        turn("k", 0, 1, S)
+        ring.append(5)
+        turn("v", 0, 0, S)
+        turn("v", 0, 1, S)
         mix_groups(0, 4, 2)
         mix_groups(0, 6, 2)
-        mix_group_and_half(8)
-        for j in range(N):
+        mix_groups(0, 8, 2, S, 1, N - 1)
+        for j in range(N - 1):
             mix_term(j, 2)
-        turn("v", 1, 0, S)
-        turn("v", 1, 1, S)
-        load_tokens("k", 5, 3, room("first", 3))
-        ring.extend([5, 7])
-        mix_term(0, 3)
-        mix_term(1, 3)
+        for j in range(N - 1):
+            mix_term(j, 3)
+        turn("k", 0, 0, S)
+        turn("k", 0, 1, S)
         state_to_a(0, 0, [S])
         state_to_a(0, 1, [S])
         state_to_b(0)
         next_groups(2)
-        turn("k", 1, 0, S)
-        turn("k", 1, 1, S)
+        pool_rows_to_state([S, S])
         quantise("v", 0)
         quantise("b", 0)
-        next_groups(2)
-        mix_term(2, 3)
+        pass
+        ring.extend([6, 7])
+        next_groups(1, V)
+        turn("v", 1, 0, S)
+        turn("v", 1, 1, S)
+        load_tokens("k", 5, 3, room("first", 3))
         quantise("k", 0)
-        mix_term(3, 3)
-        ring.append(6)
 
         for n in range(PAIRS - 1):
             m = n + 1
@@ -367,7 +385,7 @@ def tile_mhla_pa_v_kernel(tc, k_feat, v, w_piece, grad_out, out_0, out_1):
             halves_1 = n >= 6
             early = n >= 5
             quantise("a", n)
-            if n > 1:
+            if n > 0:
                 turn("k", n, 0, S)
                 turn("k", n, 1, S if n in (4, 6) else V)
             product(n, 0, 0, V)
@@ -381,7 +399,9 @@ def tile_mhla_pa_v_kernel(tc, k_feat, v, w_piece, grad_out, out_0, out_1):
                 product(n, 0, 3, S)
                 store(n, 0, 2 if halves else 0, 4)
             if n < 3:
-                next_groups((2, 1, 0)[n])
+                next_groups((2, 1, 1)[n])
+            if n == 9:
+                pool_rows_to_state([S, S])
             state_to_b(m)
             if n > 0:
                 turn("v", m, 0, S)

@@ -18,7 +18,7 @@ PAIRS = H * N
 FLOPS = 2 * 2 * PAIRS * W * D * D
 BANKS = 8
 HELD = 5
-QUADS = 48
+QUADS = 56
 GROUPS = 16
 STORED_IN_TWOS = 2
 
@@ -140,6 +140,11 @@ def tile_mhla_pa_v_kernel(tc, k_feat, v, w_piece, grad_out, out_0, out_1):
         codes = {}
         results = {}
 
+        def warm_up(count):
+            bank = next_bank(F32)
+            for c in range(count):
+                nc.tensor.matmul(bank[:, P * c : P * (c + 1)], lhsT=ident[:], rhs=ident[:], start=True, stop=True)
+
         def turn_rows(i, w0, w1, slot):
             bank = next_bank(F32, slot)
             words = g_rows[i].bitcast(F32)
@@ -173,8 +178,15 @@ def tile_mhla_pa_v_kernel(tc, k_feat, v, w_piece, grad_out, out_0, out_1):
             out = terms[:, 1024 * i : 1024 * (i + 1)]
             if engine is S:
                 nc.scalar.activation(out=out, in_=g_rows[i], func=mybir.ActivationFunctionType.Copy, scale=w_ij)
-            else:
+            elif engine is V:
                 nc.vector.tensor_scalar(out=out, in0=g_rows[i], scalar1=w_ij, scalar2=None, op0=MULT)
+            else:
+                nc.gpsimd.tensor_scalar(out=out, in0=g_rows[i], scalar1=w_ij, scalar2=0.0, op0=MULT, op1=ADD)
+
+        def pool_second():
+            w_ij = w_all[:, N * (N - 1) + 1 : N * (N - 1) + 2]
+            acc = terms[:, 0:1024]
+            nc.vector.scalar_tensor_tensor(out=acc, in0=g_rows[1], scalar=w_ij, in1=acc, op0=MULT, op1=ADD)
 
         def pool_add(a, b, last=False):
             for c0 in range(0, 1024, 512):
@@ -308,36 +320,36 @@ def tile_mhla_pa_v_kernel(tc, k_feat, v, w_piece, grad_out, out_0, out_1):
             elif n % 2 == 1:
                 nc.sync.dma_start(out=out[:, j - 1 : j + 1, :], in_=held)
 
-        patterns()
-        load_rows(0, 1)
-        load_rows(1, 1)
-        first = room("first", 3)
-        load_rows(2, 2)
-        load_groups(0, 4)
-        load_tokens("v", 0, 1, first[:, 0:2048])
-        load_groups(4, 10)
-        load_tokens("k", 0, 1, first[:, 2048:4096])
-        load_every(1, 0, 2)
-        load_tokens("v", 1, 1, first[:, 4096:6144])
-
         banks_left = [x + odd for odd in range(2) for x in range(0, GROUPS, 4)]
 
         def next_groups(count, engine=S):
             for x in range(count):
                 mix_groups(1, banks_left.pop(0), 2, engine, 2)
 
+        patterns()
+        load_rows(0, 2)
+        first = room("first", 3)
+        load_rows(2, 2)
+        load_groups(0, 9)
+        load_tokens("v", 0, 1, first[:, 0:2048])
+        load_every(1, 0, 2)
+        load_tokens("k", 0, 1, first[:, 2048:4096])
+        load_tokens("v", 1, 1, first[:, 4096:6144])
         weights()
         turn_rows(0, 0, 1, 3)
         turn_rows(0, 1, 2, 4)
         turn_rows(1, 0, 2, 5)
         turn_rows(2, 0, 2, 6)
         turn_rows(3, 0, 2, 7)
-        pool_product(0)
+        warm_up(3)
+        pool_product(0, V)
         pool_product(1, S)
-        for j in range(N - 1):
+        for j in range(3):
             mix_term(j, 0, 0, V)
         for j in range(N - 1):
             mix_term(j, 0, 1, S)
+        for j in range(3, N - 1):
+            mix_term(j, 0, 0, S)
         ring.extend([3, 4])
         pool_add(0, 1)
         pool_product(2, S)
@@ -346,6 +358,9 @@ def tile_mhla_pa_v_kernel(tc, k_feat, v, w_piece, grad_out, out_0, out_1):
         pool_add(0, 3, True)
         mix_groups(0, 0, 2)
         mix_groups(0, 2, 2)
+        mix_groups(0, 4, 2)
+        mix_groups(0, 6, 2)
+        mix_groups(0, 8, 1, S, 1, N - 1)
         load_tokens("k", 1, 1, room("g_mix0", 1))
         load_every(1, 1, 2)
         load_tokens("v", 2, 6, room("v_rest", 6))
@@ -355,29 +370,28 @@ def tile_mhla_pa_v_kernel(tc, k_feat, v, w_piece, grad_out, out_0, out_1):
         ring.append(5)
         turn("v", 0, 0, S)
         turn("v", 0, 1, S)
-        mix_groups(0, 4, 2)
-        mix_groups(0, 6, 2)
-        mix_groups(0, 8, 2, S, 1, N - 1)
+        pass
         for j in range(N - 1):
             mix_term(j, 2)
-        for j in range(N - 1):
-            mix_term(j, 3)
+        ring.append(6)
+        mix_term(0, 3)
+        mix_term(1, 3)
+        next_groups(2)
         turn("k", 0, 0, S)
         turn("k", 0, 1, S)
         state_to_a(0, 0, [S])
         state_to_a(0, 1, [S])
         state_to_b(0)
         next_groups(2)
+        turn("v", 1, 0, S)
+        turn("v", 1, 1, S)
         pool_rows_to_state([S, S])
         quantise("v", 0)
         quantise("b", 0)
-        pass
-        ring.extend([6, 7])
-        next_groups(1, V)
-        turn("v", 1, 0, S)
-        turn("v", 1, 1, S)
+        mix_term(2, 3)
         load_tokens("k", 5, 3, room("first", 3))
         quantise("k", 0)
+        ring.append(7)
 
         for n in range(PAIRS - 1):
             m = n + 1
@@ -414,7 +428,7 @@ def tile_mhla_pa_v_kernel(tc, k_feat, v, w_piece, grad_out, out_0, out_1):
             if halves_1:
                 store(n, 1, 0, 2)
             if n < 3:
-                next_groups((1, 0, 0)[n])
+                next_groups((0, 0, 0)[n])
             quantise("b", m)
             quantise("v", m)
             state_to_a(m, 0, [S])

@@ -18,7 +18,7 @@ PAIRS = H * N
 FLOPS = 2 * 2 * PAIRS * W * D * D
 BANKS = 8
 HELD = 5
-QUADS = 56
+QUADS = 64
 GROUPS = 16
 STORED_IN_TWOS = 2
 
@@ -99,7 +99,6 @@ def tile_mhla_pa_v_kernel(tc, k_feat, v, w_piece, grad_out, out_0, out_1):
                 out=sorter[:, 0 : 2 * QUADS].rearrange("p (u q) -> p u q", u=2),
                 in_=ident[:, P - 2 * QUADS : P].rearrange("p (q u) -> p u q", u=2),
             )
-            nc.vector.tensor_copy(out=sorter[:, 2 * QUADS : P], in_=ident[:, 0 : P - 2 * QUADS])
             nc.scalar.copy(out=spread[:], in_=ident[:, 0:32].unsqueeze(1).to_broadcast([P, N, 32]))
             nc.vector.tensor_reduce(
                 out=eye[:].rearrange("p (u q e) -> p q u e", u=2, e=2),
@@ -327,10 +326,11 @@ def tile_mhla_pa_v_kernel(tc, k_feat, v, w_piece, grad_out, out_0, out_1):
                 mix_groups(1, banks_left.pop(0), 2, engine, 2)
 
         patterns()
-        load_rows(0, 2)
+        load_rows(0, 1)
+        load_rows(1, 1)
         first = room("first", 3)
         load_rows(2, 2)
-        load_groups(0, 9)
+        load_groups(0, 8)
         load_tokens("v", 0, 1, first[:, 0:2048])
         load_every(1, 0, 2)
         load_tokens("k", 0, 1, first[:, 2048:4096])
@@ -343,12 +343,12 @@ def tile_mhla_pa_v_kernel(tc, k_feat, v, w_piece, grad_out, out_0, out_1):
         turn_rows(3, 0, 2, 7)
         warm_up(3)
         pool_product(0, V)
-        pool_product(1, S)
-        for j in range(3):
+        pool_product(1, None)
+        for j in range(2):
             mix_term(j, 0, 0, V)
         for j in range(N - 1):
             mix_term(j, 0, 1, S)
-        for j in range(3, N - 1):
+        for j in range(2, N - 1):
             mix_term(j, 0, 0, S)
         ring.extend([3, 4])
         pool_add(0, 1)
@@ -360,7 +360,6 @@ def tile_mhla_pa_v_kernel(tc, k_feat, v, w_piece, grad_out, out_0, out_1):
         mix_groups(0, 2, 2)
         mix_groups(0, 4, 2)
         mix_groups(0, 6, 2)
-        mix_groups(0, 8, 1, S, 1, N - 1)
         load_tokens("k", 1, 1, room("g_mix0", 1))
         load_every(1, 1, 2)
         load_tokens("v", 2, 6, room("v_rest", 6))

@@ -139,11 +139,6 @@ def tile_mhla_pa_v_kernel(tc, k_feat, v, w_piece, grad_out, out_0, out_1):
         codes = {}
         results = {}
 
-        def warm_up(count):
-            bank = next_bank(F32)
-            for c in range(count):
-                nc.tensor.matmul(bank[:, P * c : P * (c + 1)], lhsT=ident[:], rhs=ident[:], start=True, stop=True)
-
         def turn_rows(i, w0, w1, slot):
             bank = next_bank(F32, slot)
             words = g_rows[i].bitcast(F32)
@@ -341,7 +336,6 @@ def tile_mhla_pa_v_kernel(tc, k_feat, v, w_piece, grad_out, out_0, out_1):
         turn_rows(1, 0, 2, 5)
         turn_rows(2, 0, 2, 6)
         turn_rows(3, 0, 2, 7)
-        warm_up(3)
         pool_product(0, V)
         pool_product(1, None)
         for j in range(2):

from contextlib import ExitStack

import concourse.mybir as mybir
from concourse.masks import make_identity

F32 = mybir.dt.float32
BF16 = mybir.dt.bfloat16
U32 = mybir.dt.uint32
U8 = mybir.dt.uint8
E4M3 = mybir.dt.float8_e4m3fn_x4
E5M2 = mybir.dt.float8_e5m2_x4
MULT = mybir.AluOpType.mult
ADD = mybir.AluOpType.add

H, N, W, D = 2, 4, 512, 512
P = 128
PAIRS = H * N
FLOPS = 2 * 2 * PAIRS * W * D * D
BANKS = 8
HELD = 5
QUADS = 64
GROUPS = 16
STORED_IN_TWOS = 2


def tile_mhla_pa_v_kernel(tc, k_feat, v, w_piece, grad_out, out_0, out_1):
    nc = tc.nc
    V, S = nc.vector, nc.scalar
    with ExitStack() as ctx:
        const = ctx.enter_context(tc.tile_pool(name="const", bufs=1))
        keep = ctx.enter_context(tc.tile_pool(name="keep", bufs=1))
        work = ctx.enter_context(tc.tile_pool(name="work", bufs=2))
        psum = ctx.enter_context(tc.psum_pool(name="psum", bufs=1))
        ctx.enter_context(tc.manual_schedule())

        ring = list(range(BANKS - HELD))

        def next_bank(dtype, slot=None):
            if slot is None:
                slot = ring.pop(0)
                ring.append(slot)
            return psum.tile([P, 512 if dtype == F32 else 1024], dtype, name="bank%d" % slot)

        def copy(engine, dst, src):
            if engine is V:
                nc.vector.tensor_copy(out=dst, in_=src)
            else:
                nc.scalar.copy(out=dst, in_=src)

        tokens = {}
        g_groups = {}
        g_rows = {}

        def room(name, windows):
            return keep.tile([P, 2048 * windows], BF16, name=name, align_bytes=256)[:]

        def load_tokens(which, n, windows, tile):
            for w in range(windows):
                tokens[which, n + w] = tile[:, 2048 * w : 2048 * (w + 1)]
            src = (k_feat if which == "k" else v)[0].rearrange("h j (m b) d -> m (h j) (b d)", b=4)
            nc.sync.dma_start(out=tile.rearrange("p (w c) -> p w c", w=windows), in_=src[:, n : n + windows, :])

        def load_rows(i0, windows):
            tile = keep.tile([P, 1024 * windows], BF16, name="g_rows%d" % i0, align_bytes=256)
            for w in range(windows):
                g_rows[i0 + w] = tile[:, 1024 * w : 1024 * (w + 1)]
            src = grad_out[0, 0, i0 : i0 + windows, 256:512, :].rearrange("i (r e) d -> r i (e d)", e=2)
            nc.sync.dma_start(out=tile[:].rearrange("p (w c) -> p w c", w=windows), in_=src)

        def load_groups(x0, x1):
            tile = keep.tile([P, x1 - x0, 512], BF16, name="g_mix%d" % x0, align_bytes=256)
            for x in range(x0, x1):
                g_groups[0, x] = tile[:, x - x0, :]
            for i in range(N):
                src = grad_out[0, 0, i].rearrange("(x r) d -> r x d", r=32)
                nc.sync.dma_start(out=tile[i:P:4, :, :], in_=src[:, x0:x1, :])

        def load_every(h, x0, step):
            tile = keep.tile([P, GROUPS // step, 512], BF16, name="g_every%d_%d" % (h, x0), align_bytes=256)
            for x in range(x0, GROUPS, step):
                g_groups[h, x] = tile[:, x // step, :]
            src = grad_out[0, h].rearrange("i (x r) d -> r (i x) d", r=32)
            nc.sync.dma_start(out=tile[:], in_=src[:, x0 : N * GROUPS : step, :])

        w_rows = const.tile([P, N], BF16, name="w_rows")
        ident = const.tile([P, P], F32, name="ident")
        eye = const.tile([P, 32], F32, name="eye")
        spread = const.tile([P, N, 32], BF16, name="spread", align_bytes=64)
        w_all = const.tile([P, N * N], F32, name="w_all")
        mixer = const.tile([P, P], BF16, name="mixer", align_bytes=64)
        sorter = const.tile([P, P], F32, name="sorter")

        def patterns():
            nc.sync.dma_start(out=w_rows[0:32, :], in_=w_piece.partition_broadcast(8))
            nc.gpsimd.memset(w_rows[32:64, :], 0.0)
            nc.gpsimd.memset(w_rows[64:P, :], 0.0)
            make_identity(nc, ident[:])
            nc.vector.tensor_copy(
                out=sorter[:, 0 : 2 * QUADS].rearrange("p (u q) -> p u q", u=2),
                in_=ident[:, P - 2 * QUADS : P].rearrange("p (q u) -> p u q", u=2),
            )
            nc.scalar.copy(out=spread[:], in_=ident[:, 0:32].unsqueeze(1).to_broadcast([P, N, 32]))
            nc.vector.tensor_reduce(
                out=eye[:].rearrange("p (u q e) -> p q u e", u=2, e=2),
                in_=ident[:].rearrange("p (q u e i) -> p q u e i", u=2, e=2, i=4),
                axis=mybir.AxisListType.X,
                op=ADD,
            )

        def weights():
            bank = next_bank(F32)
            for j in range(N):
                nc.tensor.matmul(
                    bank[:, N * j : N * j + N],
                    lhsT=w_rows[:, j : j + 1].to_broadcast([P, P]),
                    rhs=spread[:, 0, 0:N],
                    start=True,
                    stop=True,
                )
            nc.tensor.matmul(
                bank[:, 16:20], lhsT=spread[:].rearrange("p r i -> p (r i)"), rhs=w_rows[:], start=True, stop=True
            )
            nc.vector.tensor_copy(out=w_all[:], in_=bank[:, 0:16])
            nc.vector.tensor_tensor(
                out=mixer[:].rearrange("p (j r) -> p j r", j=N),
                in0=eye[:].unsqueeze(1).to_broadcast([P, N, 32]),
                in1=bank[:, 16:20].unsqueeze(2).to_broadcast([P, N, 32]),
                op=MULT,
            )

        state = [keep.tile([P, N * 2048], BF16, name="mixed%d" % h, align_bytes=64) for h in range(H)]
        raw = {}
        sums = work.tile([P, (N - 1) * 16 * QUADS], F32, name="res1", align_bytes=256)
        terms = work.tile([P, N * 1024], F32, name="res0", align_bytes=256)
        pool_rows = keep.tile([P, 1024], BF16, name="pool_rows", align_bytes=64)
        b_in = {}
        a_in = {}
        turned = {}
        codes = {}
        results = {}

        def turn_rows(i, w0, w1, slot):
            bank = next_bank(F32, slot)
            words = g_rows[i].bitcast(F32)
            run = 2 * QUADS
            for e in range(2):
                for w in range(w0, w1):
                    c0 = 256 * e + run * (w - w0)
                    nc.tensor.transpose(bank[:, c0 : c0 + P], words[:, 256 * e + w : 256 * (e + 1) : 2], sorter[:])
            view = bank[:].bitcast(BF16).rearrange("p (e c) -> p e c", e=2)[:, :, 0 : 2 * run * (w1 - w0)]
            raw[i, w0] = (view.rearrange("p e (a q f) -> p f a q e", q=QUADS, f=2), w1)

        def mix_term(j, i, w0=0, engine=V):
            term, w1 = raw[i, w0]
            w_ij = w_all[:, N * j + i : N * j + i + 1]
            acc = sums[:, 16 * QUADS * j : 16 * QUADS * (j + 1)].rearrange("p (f a q e) -> p f a q e", f=2, a=4, e=2)[:, :, 2 * w0 : 2 * w1]
            if engine is S:
                nc.scalar.activation(out=acc, in_=term, func=mybir.ActivationFunctionType.Copy, scale=w_ij)
                return
            window = state[0][:, 2048 * j : 2048 * (j + 1)].rearrange("p (f a q e) -> p f a q e", f=2, a=4, e=2)
            dst = acc if i < N - 1 else window[:, :, :, P - QUADS : P, :]
            for f in range(2):
                if i == 0:
                    nc.vector.tensor_scalar(out=acc[:, f], in0=term[:, f], scalar1=w_ij, scalar2=None, op0=MULT)
                else:
                    nc.vector.scalar_tensor_tensor(
                        out=dst[:, f], in0=term[:, f], scalar=w_ij, in1=acc[:, f], op0=MULT, op1=ADD
                    )

        def pool_product(i, engine=None):
            w_ij = w_all[:, N * (N - 1) + i : N * (N - 1) + i + 1]
            out = terms[:, 1024 * i : 1024 * (i + 1)]
            if engine is S:
                nc.scalar.activation(out=out, in_=g_rows[i], func=mybir.ActivationFunctionType.Copy, scale=w_ij)
            elif engine is V:
                nc.vector.tensor_scalar(out=out, in0=g_rows[i], scalar1=w_ij, scalar2=None, op0=MULT)
            else:
                nc.gpsimd.tensor_scalar(out=out, in0=g_rows[i], scalar1=w_ij, scalar2=0.0, op0=MULT, op1=ADD)

        def pool_second():
            w_ij = w_all[:, N * (N - 1) + 1 : N * (N - 1) + 2]
            acc = terms[:, 0:1024]
            nc.vector.scalar_tensor_tensor(out=acc, in0=g_rows[1], scalar=w_ij, in1=acc, op0=MULT, op1=ADD)

        def pool_add(a, b, last=False):
            for c0 in range(0, 1024, 512):
                acc = terms[:, 1024 * a + c0 : 1024 * a + c0 + 512]
                out = pool_rows[:, c0 : c0 + 512] if last else acc
                nc.gpsimd.tensor_tensor(out=out, in0=acc, in1=terms[:, 1024 * b + c0 : 1024 * b + c0 + 512], op=ADD)

        def pool_rows_to_state(engines):
            bank = next_bank(F32)
            words = pool_rows[:].bitcast(F32)
            for e in range(2):
                for w in range(2):
                    c0 = 256 * e + 128 * w
                    nc.tensor.transpose(bank[:, c0 : c0 + P], words[:, 256 * e + w : 256 * (e + 1) : 2], ident[:])
            src = bank[:].bitcast(BF16).rearrange("p (e w q u f) -> p w f u q e", e=2, w=2, u=2, f=2)
            dst = state[0][:, 2048 * (N - 1) : 2048 * N].rearrange("p (f w u q e) -> p w f u q e", f=2, w=2, u=2, e=2)
            for w in range(2):
                copy(engines[w], dst[:, w, :, :, 64:P, :], src[:, w])

        def mix_groups(h, x0, count, engine=S, step=1, windows=N):
            bank = next_bank(BF16)
            used = bank[:, 0 : 128 * windows * count]
            view = used.rearrange("p (g j f w c) -> p g j f w c", g=count, j=windows, f=2, w=2)
            for g in range(count):
                for t in range(4):
                    rows = g_groups[h, x0 + step * g]
                    out = view[:, g, :, t % 2, t // 2, :]
                    nc.tensor.matmul(out, lhsT=rows[:, t:512:4], rhs=mixer[:, 0 : 32 * windows], start=True, stop=True)
            dst = state[h][:].bitcast(F32).rearrange("p (a x y) -> p a x y", x=GROUPS, y=8)
            copy(
                engine,
                dst[:, 0 : 8 * windows, x0 : x0 + step * (count - 1) + 1 : step, :],
                used.bitcast(F32).rearrange("p (g a y) -> p a g y", g=count, y=8),
            )

        def state_to_b(n):
            h, j = divmod(n, N)
            b_in[n] = work.tile([P, 2048], BF16, name="b_in", align_bytes=64)
            dst = b_in[n][:].rearrange("p (c i w f) -> p c w f i", i=4, w=2, f=2)
            src = state[h][:, 2048 * j : 2048 * (j + 1)].rearrange("p (f w c i) -> p c w f i", f=2, w=2, i=4)
            nc.vector.tensor_copy(out=dst, in_=src)

        def state_to_a(n, half, engines):
            h, j = divmod(n, N)
            if half == 0:
                a_in[n] = work.tile([P, 2048], BF16, name="a_in", align_bytes=64)
            words = state[h][:].bitcast(F32)
            bank = next_bank(F32)
            for t in range(2):
                for u in range(2):
                    c0 = 256 * t + 128 * u
                    w0 = 1024 * j + 512 * half + c0
                    nc.tensor.transpose(bank[:, c0 : c0 + 128], words[:, w0 : w0 + 128], ident[:])
            dst = a_in[n][:].bitcast(F32)[:, 512 * half : 512 * half + 512]
            dst = dst.rearrange("q (t p u) -> q t p u", t=2, u=2)
            src = bank[:].rearrange("q (t u p) -> q t p u", t=2, u=2)
            if len(engines) == 1:
                copy(engines[0], dst, src)
            else:
                for t in range(2):
                    copy(engines[t], dst[:, t, :, :], src[:, t, :, :])

        def turn(which, n, half, engine):
            if half == 0:
                turned[which, n] = work.tile([P, 2048], BF16, name="grouped_" + which, align_bytes=64)
            words = tokens[which, n][:].bitcast(F32)
            bank = next_bank(F32)
            for b in range(2):
                for u in range(2):
                    w0 = 256 * (2 * half + b)
                    c0 = 256 * b + 128 * u
                    nc.tensor.transpose(bank[:, c0 : c0 + 128], words[:, w0 + u : w0 + 256 : 2], ident[:])
            dst = turned[which, n][:].bitcast(F32)[:, 512 * half : 512 * half + 512]
            copy(
                engine,
                dst.rearrange("p (b m u) -> p b m u", b=2, u=2),
                bank[:].rearrange("p (b u m) -> p b m u", b=2, u=2),
            )

        def quantise(which, n, c0=0, c1=512):
            if which == "b":
                src, fmt = b_in[n], E5M2
            elif which == "a":
                src, fmt = a_in[n], E5M2
            else:
                src, fmt = turned[which, n], E4M3
            if c0 == 0:
                c = work.tile([P, 512], U32, name="codes_" + which, align_bytes=64)
                sc = work.tile([P, 512], U8, name="scales_" + which, align_bytes=64)
                codes[which, n] = (c, sc)
            c, sc = codes[which, n]
            nc.vector.quantize_mx(out=c[:, c0:c1].bitcast(fmt), scales=sc[:, c0:c1], in_=src[:, 4 * c0 : 4 * c1])

        def product(n, which, b, engine):
            left, right = ("v", "b") if which == 0 else ("k", "a")
            lc, ls = codes[left, n]
            rc, rs = codes[right, n]
            if b == 0 and n % 2 == 0:
                results[which] = work.tile([P, 4096], F32, name="res%d" % which, align_bytes=256)
            bank = next_bank(F32)
            cols = slice(128 * b, 128 * b + 128)
            nc.tensor.matmul_mx(
                out=bank[:],
                lhsT=lc[:, cols].bitcast(E4M3),
                lhsT_scale=ls[:, cols],
                rhs=rc[:].bitcast(E5M2),
                rhs_scale=rs[:],
                start=True,
                stop=True,
            )
            res = results[which][:, 2048 * (n % 2) + 512 * b : 2048 * (n % 2) + 512 * (b + 1)]
            if which == 0:
                copy(
                    engine,
                    res.rearrange("m (q u e) -> m q u e", u=2, e=2),
                    bank[:].rearrange("m (u q e) -> m q u e", u=2, e=2),
                )
            else:
                copy(
                    engine,
                    res.rearrange("m (p w f) -> m p w f", w=2, f=2),
                    bank[:].rearrange("m (f w p) -> m p w f", f=2, w=2),
                )

        def store(n, which, b0, b1):
            h, j = divmod(n, N)
            out = (out_0 if which == 0 else out_1)[0, h].rearrange("j (m b) d -> m j (b d)", b=4)
            held = results[which][:].rearrange("m (j c) -> m j c", j=2)
            if n >= STORED_IN_TWOS:
                nc.sync.dma_start(out=out[:, j, 512 * b0 : 512 * b1], in_=held[:, n % 2, 512 * b0 : 512 * b1])
            elif n % 2 == 1:
                nc.sync.dma_start(out=out[:, j - 1 : j + 1, :], in_=held)

        banks_left = [x + odd for odd in range(2) for x in range(0, GROUPS, 4)]

        def next_groups(count, engine=S):
            for x in range(count):
                mix_groups(1, banks_left.pop(0), 2, engine, 2)

        patterns()
        load_rows(0, 1)
        load_rows(1, 1)
        first = room("first", 3)
        load_rows(2, 2)
        load_groups(0, 8)
        load_tokens("v", 0, 1, first[:, 0:2048])
        load_every(1, 0, 2)
        load_tokens("k", 0, 1, first[:, 2048:4096])
        load_tokens("v", 1, 1, first[:, 4096:6144])
        weights()
        turn_rows(0, 0, 1, 3)
        turn_rows(0, 1, 2, 4)
        turn_rows(1, 0, 2, 5)
        turn_rows(2, 0, 2, 6)
        turn_rows(3, 0, 2, 7)
        pool_product(0, V)
        pool_product(1, None)
        for j in range(2):
            mix_term(j, 0, 0, V)
        for j in range(N - 1):
            mix_term(j, 0, 1, S)
        for j in range(2, N - 1):
            mix_term(j, 0, 0, S)
        ring.extend([3, 4])
        pool_add(0, 1)
        pool_product(2, S)
        pool_product(3, S)
        pool_add(0, 2)
        pool_add(0, 3, True)
        mix_groups(0, 0, 2)
        mix_groups(0, 2, 2)
        mix_groups(0, 4, 2)
        mix_groups(0, 6, 2)
        load_tokens("k", 1, 1, room("g_mix0", 1))
        load_every(1, 1, 2)
        load_tokens("v", 2, 6, room("v_rest", 6))
        load_tokens("k", 2, 3, room("k_middle", 3))
        for j in range(N - 1):
            mix_term(j, 1)
        ring.append(5)
        turn("v", 0, 0, S)
        turn("v", 0, 1, S)
        pass
        for j in range(N - 1):
            mix_term(j, 2)
        ring.append(6)
        mix_term(0, 3)
        mix_term(1, 3)
        next_groups(2)
        turn("k", 0, 0, S)
        turn("k", 0, 1, S)
        state_to_a(0, 0, [S])
        state_to_a(0, 1, [S])
        state_to_b(0)
        next_groups(2)
        turn("v", 1, 0, S)
        turn("v", 1, 1, S)
        pool_rows_to_state([S, S])
        quantise("v", 0)
        quantise("b", 0)
        mix_term(2, 3)
        load_tokens("k", 5, 3, room("first", 3))
        quantise("k", 0)
        ring.append(7)

        for n in range(PAIRS - 1):
            m = n + 1
            halves = n >= 6
            halves_1 = n >= 6
            early = n >= 5
            quantise("a", n)
            if n > 0:
                turn("k", n, 0, S)
                turn("k", n, 1, S if n in (4, 6) else V)
            product(n, 0, 0, V)
            product(n, 0, 1, S)
            if halves:
                store(n, 0, 0, 2)
            if n > 0:
                quantise("k", n)
            product(n, 0, 2, S)
            if early:
                product(n, 0, 3, S)
                store(n, 0, 2 if halves else 0, 4)
            if n < 3:
                next_groups((2, 1, 1)[n])
            if n == 9:
                pool_rows_to_state([S, S])
            state_to_b(m)
            if n > 0:
                turn("v", m, 0, S)
                turn("v", m, 1, S)
            if not early:
                product(n, 0, 3, S)
                store(n, 0, 0, 4)
            product(n, 1, 0, V)
            product(n, 1, 1, S)
            if halves_1:
                store(n, 1, 0, 2)
            if n < 3:
                next_groups((0, 0, 0)[n])
            quantise("b", m)
            quantise("v", m)
            state_to_a(m, 0, [S])
            state_to_a(m, 1, [S])
            product(n, 1, 2, S)
            product(n, 1, 3, V)
            store(n, 1, 2 if halves_1 else 0, 4)

        n = PAIRS - 1
        quantise("a", n)
        for half in range(2):
            turn("k", n, half, S)
            if half == 1:
                quantise("k", n, 0, 256)
            product(n, 0, 2 * half, V)
            product(n, 0, 2 * half + 1, S)
            store(n, 0, 2 * half, 2 * half + 2)
        quantise("k", n, 256, 512)
        for half in range(2):
            product(n, 1, 2 * half, S)
            product(n, 1, 2 * half + 1, V)
            store(n, 1, 2 * half, 2 * half + 2)
